import numpy as np
import ml_dtypes


def mxq(x, axis, fmt="e4m3"):
    dtype, down = {"e4m3": (ml_dtypes.float8_e4m3fn, 7), "e5m2": (ml_dtypes.float8_e5m2, 14)}[fmt]
    v = np.moveaxis(np.asarray(x, np.float32).astype(ml_dtypes.bfloat16).astype(np.float64), axis, -1)
    blocks = v.reshape(v.shape[:-1] + (-1, 32))
    amax = np.abs(blocks).max(-1, keepdims=True)
    byte = np.maximum(np.where(amax > 0, np.frexp(amax)[1] - 1 + 127, 0) - down, 1)
    scale = np.exp2(byte - 127.0)
    codes = (blocks / scale).astype(np.float32).astype(dtype).astype(np.float64)
    return np.moveaxis((codes * scale).reshape(v.shape), -1, axis)


WIDE = False


def mx_kscale(k):
    if not WIDE:
        return np.ones(k)
    levels = np.array([10, -10, 5, -5, 0])
    a = np.random.permutation(np.resize(levels, k // 512 * 4)).reshape(k // 512, 4)
    idx = np.arange(k)
    return np.exp2(a[idx // 512, idx % 128 // 32])


BF16 = ml_dtypes.bfloat16


def bf(x):
    return np.asarray(x, np.float32).astype(BF16)


def f64(x):
    return np.asarray(x).astype(np.float64)


C, H, W, CO, G = 256, 128, 256, 512, 128
K = 4 * C
P = (H // 2) * (W // 2)
EPS = 1e-5


def haar_bands(x):
    xr = x.reshape(C, H // 2, 2, W // 2, 2)
    x00 = xr[:, :, 0, :, 0]
    x01 = xr[:, :, 0, :, 1]
    x10 = xr[:, :, 1, :, 0]
    x11 = xr[:, :, 1, :, 1]
    half = 0.5
    LL = (x00 + x01 + x10 + x11) * half
    HL = (-x00 - x01 + x10 + x11) * half
    LH = (-x00 + x01 - x10 + x11) * half
    HH = (x00 - x01 - x10 + x11) * half
    return LL, HL, LH, HH


def group_norm(y, scale, bias, groups):
    c, h, w = y.shape
    yg = y.reshape(groups, c // groups, h, w)
    mean = np.mean(yg, axis=(1, 2, 3), keepdims=True)
    var = np.mean(np.square(yg - mean), axis=(1, 2, 3), keepdims=True)
    yn = ((yg - mean) / np.sqrt(var + EPS)).reshape(c, h, w)
    return yn * scale[:, None, None] + bias[:, None, None]


def setup_inputs():
    s = mx_kscale(K)
    return {"x": bf(np.random.standard_normal((C, H, W))),
            "gn_scale": bf((1.0 + 0.1 * np.random.standard_normal(K)) * s),
            "gn_bias": bf(0.1 * np.random.standard_normal(K) * s),
            "w_proj": bf(np.random.standard_normal((CO, K)) / np.sqrt(K) / s[None, :])}


def reference(x, gn_scale, gn_bias, w_proj):
    LL, HL, LH, HH = haar_bands(f64(x))
    y = np.concatenate([LL, HL, LH, HH], axis=0)
    y = group_norm(y, f64(gn_scale), f64(gn_bias), G)
    z = mxq(f64(w_proj), 1, "e4m3") @ mxq(y.reshape(K, P), 0, "e4m3")
    return np.maximum(z, 0.0).reshape(CO, H // 2, W // 2)

@@ -1,0 +1,292 @@
+from contextlib import ExitStack
+
+import concourse.mybir as mybir
+from concourse.masks import make_identity
+
+F32 = mybir.dt.float32
+BF16 = mybir.dt.bfloat16
+U32 = mybir.dt.uint32
+U8 = mybir.dt.uint8
+FP8X4 = mybir.dt.float8_e4m3fn_x4
+ALU = mybir.AluOpType
+ACTF = mybir.ActivationFunctionType
+AX = mybir.AxisListType
+
+P = 128
+CO = 512
+K = 1024
+NPIX = 8192
+NCH = 16
+COLS = 512
+NB = 17
+EPS = 1e-5
+FLOPS = 2 * CO * K * NPIX
+
+
+def tile_hwdconv_t_kernel(tc, x, gn_scale, gn_bias, w_proj, out):
+    nc = tc.nc
+    xv = x.rearrange("(p e) h w -> p e (h w)", e=2)
+    ov = out.rearrange("(a p) h w -> p a (h w)", p=P)
+    wv = w_proj.rearrange("(a p) k -> p a k", p=P)
+
+    with ExitStack() as ctx:
+        keep = ctx.enter_context(tc.tile_pool(name="keep", bufs=1))
+        bands = ctx.enter_context(tc.tile_pool(name="bands", bufs=NB))
+        work = ctx.enter_context(tc.tile_pool(name="work", bufs=2))
+        psum = ctx.enter_context(tc.psum_pool(name="psum", bufs=8))
+
+        one = keep.tile([P, 1], F32, name="one")
+        nc.vector.memset(one[:], 1.0)
+        wsq = keep.tile([P, 1], F32, name="wsq")
+        nc.scalar.activation(out=wsq[:], in_=one[:], func=ACTF.Sqrt)
+
+        ident = keep.tile([P, P], F32, name="ident")
+        make_identity(nc, ident[:])
+        rsum = keep.tile([P, 32], F32, name="rsum")
+        nc.vector.tensor_reduce(
+            out=rsum[:], in_=ident[:].rearrange("p (q j) -> p q j", j=4), axis=AX.X, op=ALU.add
+        )
+        gmat = keep.tile([P, 32, 4], F32, name="gmat")
+        nc.vector.tensor_copy(out=gmat[:], in_=rsum[:].unsqueeze(2).to_broadcast([P, 32, 4]))
+        gsum = gmat[:].rearrange("p q j -> p (q j)")
+
+        gsb = keep.tile([P, 4, 2], BF16, name="gsb")
+        gbb = keep.tile([P, 4, 2], BF16, name="gbb")
+        with nc.allow_non_contiguous_dma(reason="two small vectors, four bytes a piece"):
+            nc.scalar.dma_start(out=gsb[:], in_=gn_scale.rearrange("(b p e) -> p b e", b=4, e=2))
+            nc.scalar.dma_start(out=gbb[:], in_=gn_bias.rearrange("(b p e) -> p b e", b=4, e=2))
+        gsf = keep.tile([P, 4, 2], F32, name="gsf")
+        gbf = keep.tile([P, 4, 2], F32, name="gbf")
+        nc.vector.tensor_copy(out=gsf[:], in_=gsb[:])
+        nc.vector.tensor_copy(out=gbf[:], in_=gbb[:])
+
+        wc = keep.tile([P, 2, CO], U32, name="wc", align_bytes=64)
+        ws = keep.tile([P, 2, CO], U8, name="ws", align_bytes=64)
+        codes0 = keep.tile([P, NPIX], U32, name="codes0", align_bytes=64)
+        scales0 = keep.tile([P, NPIX], U8, name="scales0", align_bytes=64)
+
+        sums = [keep.tile([P, 2, NCH], F32, name="sums%d" % g) for g in range(2)]
+        sqs = [keep.tile([P, 2, NCH], F32, name="sqs%d" % g) for g in range(2)]
+        negc = [keep.tile([P, 2], F32, name="negc%d" % g) for g in range(2)]
+        gain = [keep.tile([P, 2, 2], F32, name="gain%d" % g) for g in range(2)]
+        shift = [keep.tile([P, 2, 2], F32, name="shift%d" % g) for g in range(2)]
+
+        def load_w():
+            raws = []
+            for h in range(2):
+                wraw = work.tile([P, 2048], BF16, name="wraw", tag="yp")
+                nc.scalar.dma_start(
+                    out=wraw[:].rearrange("p (a k) -> p a k", a=2), in_=wv[:, 2 * h : 2 * h + 2, :]
+                )
+                raws.append(wraw)
+            return raws
+
+        def prep_w(raws):
+            for g in range(2):
+                wgr = work.tile([P, 2048], BF16, name="wgr", tag="gr", align_bytes=64)
+                wgv = wgr[:].bitcast(F32).rearrange("p (o u) -> p o u", u=2)
+                for h in range(2):
+                    pt = psum.tile([P, 2, 2, P], F32, name="pt", tag="acc")
+                    src = raws[h][:].bitcast(F32)
+                    for a in range(2):
+                        for u in range(2):
+                            lo = 512 * a + 256 * g + 128 * u
+                            nc.tensor.transpose(pt[:, a, u, :], src[:, lo : lo + P], ident[:])
+                    nc.scalar.copy(
+                        out=wgv[:, 256 * h : 256 * h + 256, :].rearrange("p (a o) u -> p a o u", a=2),
+                        in_=pt[:].rearrange("p a u o -> p a o u"),
+                    )
+                nc.vector.quantize_mx(out=wc[:, g, :].bitcast(FP8X4), scales=ws[:, g, :], in_=wgr[:])
+
+        def load_x(c):
+            xt = work.tile([P, 2, 2048], BF16, name="xt", tag="xa")
+            nc.sync.dma_start(out=xt[:], in_=xv[:, :, 2048 * c : 2048 * (c + 1)])
+            return xt
+
+        def haar_h(g, xt):
+            st = work.tile([P, 2048], F32, name="st", tag="sa", bufs=1)
+            pair = xt[:].rearrange("p e (n two) -> p (e n) two", two=2)
+            if g == 0:
+                nc.vector.tensor_tensor(out=st[:], in0=pair[:, :, 0], in1=pair[:, :, 1], op=ALU.add)
+            else:
+                nc.vector.tensor_tensor(out=st[:], in0=pair[:, :, 1], in1=pair[:, :, 0], op=ALU.subtract)
+            return st
+
+        def haar_v(g, c, st):
+            bd = bands.tile([P, 2, 1024], F32, name="bd", tag="bd")
+            rows = st[:].rearrange("p (a r j) -> p a r j", r=2, j=P)
+            for u in range(2):
+                nc.vector.scalar_tensor_tensor(
+                    out=bd[:, u, :].rearrange("p (a j) -> p a j", j=P),
+                    in0=rows[:, :, 0, :],
+                    scalar=(1.0 if u == 0 else -1.0),
+                    in1=rows[:, :, 1, :],
+                    op0=ALU.mult,
+                    op1=ALU.add,
+                    accum_out=sums[g][:, u, c : c + 1],
+                )
+            return bd
+
+        def first_guess(g):
+            pz = psum.tile([P, 2], F32, name="pz", tag="acc")
+            nc.tensor.matmul(out=pz[:], lhsT=gsum, rhs=sums[g][:, :, 0], start=True, stop=True)
+            nc.vector.tensor_scalar_mul(out=negc[g][:], in0=pz[:], scalar1=-1.0 / (8 * COLS))
+
+        def squares(g, c, bd):
+            for u in range(2):
+                junk = work.tile([P, 1024], BF16, name="junk", tag="junk", bufs=1)
+                nc.scalar.activation(
+                    out=junk[:],
+                    in_=bd[:, u, :],
+                    func=ACTF.Square,
+                    bias=negc[g][:, u : u + 1],
+                    scale=1.0,
+                    accum_out=sqs[g][:, u, c : c + 1],
+                )
+
+        def finalise(g):
+            tot = keep.tile([P, 4], F32, name="tot%d" % g)
+            nc.vector.tensor_reduce(out=tot[:, 0:2], in_=sums[g][:], axis=AX.X, op=ALU.add)
+            nc.vector.tensor_reduce(out=tot[:, 2:4], in_=sqs[g][:], axis=AX.X, op=ALU.add)
+            pg = psum.tile([P, 4], F32, name="pg", tag="acc")
+            nc.tensor.matmul(out=pg[:], lhsT=gsum, rhs=tot[:], start=True, stop=True)
+            mv = keep.tile([P, 4], F32, name="mv%d" % g)
+            nc.vector.tensor_scalar_mul(out=mv[:], in0=pg[:], scalar1=1.0 / (8 * NPIX))
+            dl = keep.tile([P, 2], F32, name="dl%d" % g)
+            nc.vector.tensor_tensor(out=dl[:], in0=mv[:, 0:2], in1=negc[g][:], op=ALU.add)
+            d2 = keep.tile([P, 2], F32, name="d2%d" % g)
+            nc.vector.tensor_tensor(out=d2[:], in0=dl[:], in1=dl[:], op=ALU.mult)
+            var = keep.tile([P, 2], F32, name="var%d" % g)
+            nc.vector.tensor_tensor(out=var[:], in0=mv[:, 2:4], in1=d2[:], op=ALU.subtract)
+            ve = keep.tile([P, 2], F32, name="ve%d" % g)
+            nc.vector.tensor_scalar(
+                out=ve[:], in0=var[:], scalar1=0.0, scalar2=4.0 * EPS, op0=ALU.max, op1=ALU.add
+            )
+            sd = keep.tile([P, 2], F32, name="sd%d" % g)
+            nc.scalar.activation(out=sd[:], in_=ve[:], func=ACTF.Sqrt)
+            rs = keep.tile([P, 2], F32, name="rs%d" % g)
+            nc.vector.reciprocal(out=rs[:], in_=sd[:])
+            nc.vector.tensor_tensor(
+                out=gain[g][:],
+                in0=gsf[:, 2 * g : 2 * g + 2, :],
+                in1=rs[:].unsqueeze(2).to_broadcast([P, 2, 2]),
+                op=ALU.mult,
+            )
+            mg = keep.tile([P, 2, 2], F32, name="mg%d" % g)
+            nc.vector.tensor_tensor(
+                out=mg[:],
+                in0=gain[g][:],
+                in1=mv[:, 0:2].unsqueeze(2).to_broadcast([P, 2, 2]),
+                op=ALU.mult,
+            )
+            nc.vector.tensor_tensor(
+                out=shift[g][:], in0=gbf[:, 2 * g : 2 * g + 2, :], in1=mg[:], op=ALU.subtract
+            )
+
+        def affine(g, bd, on_scalar):
+            yp = work.tile([P, 4, COLS], BF16, name="yp", tag="yp")
+            for u in range(2):
+                for e in range(2):
+                    src = bd[:, u, COLS * e : COLS * (e + 1)]
+                    if on_scalar:
+                        nc.scalar.activation(
+                            out=yp[:, 2 * u + e, :],
+                            in_=src,
+                            func=ACTF.Identity,
+                            bias=shift[g][:, u, e : e + 1],
+                            scale=gain[g][:, u, e : e + 1],
+                        )
+                    else:
+                        nc.vector.tensor_scalar(
+                            out=yp[:, 2 * u + e, :],
+                            in0=src,
+                            scalar1=gain[g][:, u, e : e + 1],
+                            scalar2=shift[g][:, u, e : e + 1],
+                            op0=ALU.mult,
+                            op1=ALU.add,
+                        )
+            return yp
+
+        def regroup(yp):
+            gr = work.tile([P, COLS, 4], BF16, name="gr", tag="gr", align_bytes=64)
+            nc.vector.tensor_copy(
+                out=gr[:].rearrange("p (c i) t -> p c t i", i=4),
+                in_=yp[:].rearrange("p t (c i) -> p c t i", i=4),
+            )
+            return gr
+
+        def quantise(gr, codes, scales):
+            nc.vector.quantize_mx(
+                out=codes.bitcast(FP8X4), scales=scales, in_=gr[:].rearrange("p c t -> p (c t)")
+            )
+
+        def project(c, c1, s1):
+            cols = slice(COLS * c, COLS * (c + 1))
+            ost = work.tile(
+                [P, 4, COLS], F32, name="ost", tag=("sa" if c % 3 == 2 else "xa"), bufs=(1 if c % 3 == 2 else 2)
+            )
+            for a in range(4):
+                acc = psum.tile([P, COLS], F32, name="acc", tag="acc")
+                m = slice(P * a, P * (a + 1))
+                nc.tensor.matmul_mx(
+                    out=acc[:],
+                    lhsT=wc[:, 0, m].bitcast(FP8X4),
+                    lhsT_scale=ws[:, 0, m],
+                    rhs=codes0[:, cols].bitcast(FP8X4),
+                    rhs_scale=scales0[:, cols],
+                    start=True,
+                    stop=False,
+                )
+                nc.tensor.matmul_mx(
+                    out=acc[:],
+                    lhsT=wc[:, 1, m].bitcast(FP8X4),
+                    lhsT_scale=ws[:, 1, m],
+                    rhs=c1[:].bitcast(FP8X4),
+                    rhs_scale=s1[:],
+                    start=False,
+                    stop=True,
+                )
+                nc.scalar.activation(out=ost[:, a, :], in_=acc[:], func=ACTF.Relu)
+            nc.sync.dma_start(out=ov[:, :, cols], in_=ost[:])
+
+        raws = load_w()
+        bd0 = []
+        for c in range(NCH):
+            xt = load_x(c)
+            st = haar_h(0, xt)
+            bd0.append(haar_v(0, c, st))
+            if c == 0:
+                first_guess(0)
+            if c == 2:
+                prep_w(raws)
+            squares(0, c, bd0[c])
+
+        bd1 = []
+        xt = load_x(0)
+        st = haar_h(1, xt)
+        bd1.append(haar_v(1, 0, st))
+        first_guess(1)
+        finalise(0)
+        yps = [affine(0, bd0[0], True)]
+        for c in range(NCH):
+            if c + 1 < NCH:
+                yps.append(affine(0, bd0[c + 1], True))
+                xt = load_x(c + 1)
+                st = haar_h(1, xt)
+            gr = regroup(yps[c])
+            if c + 1 < NCH:
+                bd1.append(haar_v(1, c + 1, st))
+            cols = slice(COLS * c, COLS * (c + 1))
+            quantise(gr, codes0[:, cols], scales0[:, cols])
+            squares(1, c, bd1[c])
+
+        finalise(1)
+        yps = [affine(1, bd1[0], False)]
+        for c in range(NCH):
+            gr = regroup(yps[c])
+            if c + 1 < NCH:
+                yps.append(affine(1, bd1[c + 1], False))
+            c1 = work.tile([P, COLS], U32, name="c1", tag="c1", align_bytes=64)
+            s1 = work.tile([P, COLS], U8, name="s1", tag="s1", align_bytes=64)
+            quantise(gr, c1[:], s1[:])
+            project(c, c1, s1)

@@ -19,6 +19,8 @@ NPIX = 8192
 NCH = 16
 COLS = 512
 NB = 17
+PE_CHUNKS = tuple(range(1, 13))
+ACT_REGROUP = (1, 4, 7, 10, 13)
 EPS = 1e-5
 FLOPS = 2 * CO * K * NPIX
 
@@ -49,6 +51,10 @@ def tile_hwdconv_t_kernel(tc, x, gn_scale, gn_bias, w_proj, out):
         gmat = keep.tile([P, 32, 4], F32, name="gmat")
         nc.vector.tensor_copy(out=gmat[:], in_=rsum[:].unsqueeze(2).to_broadcast([P, 32, 4]))
         gsum = gmat[:].rearrange("p q j -> p (q j)")
+        identb = keep.tile([P, P], BF16, name="identb")
+        nc.vector.tensor_copy(out=identb[:], in_=ident[:])
+        nidentb = keep.tile([P, P], BF16, name="nidentb")
+        nc.vector.tensor_scalar_mul(out=nidentb[:], in0=ident[:], scalar1=-1.0)
 
         gsb = keep.tile([P, 4, 2], BF16, name="gsb")
         gbb = keep.tile([P, 4, 2], BF16, name="gbb")
@@ -65,7 +71,9 @@ def tile_hwdconv_t_kernel(tc, x, gn_scale, gn_bias, w_proj, out):
         codes0 = keep.tile([P, NPIX], U32, name="codes0", align_bytes=64)
         scales0 = keep.tile([P, NPIX], U8, name="scales0", align_bytes=64)
 
-        sums = [keep.tile([P, 2, NCH], F32, name="sums%d" % g) for g in range(2)]
+        sums = [keep.tile([P, 2, 2 * NCH], F32, name="sums%d" % g) for g in range(2)]
+        for g in range(2):
+            nc.vector.memset(sums[g][:], 0.0)
         sqs = [keep.tile([P, 2, NCH], F32, name="sqs%d" % g) for g in range(2)]
         negc = [keep.tile([P, 2], F32, name="negc%d" % g) for g in range(2)]
         gain = [keep.tile([P, 2, 2], F32, name="gain%d" % g) for g in range(2)]
@@ -123,8 +131,50 @@ def tile_hwdconv_t_kernel(tc, x, gn_scale, gn_bias, w_proj, out):
                     in1=rows[:, :, 1, :],
                     op0=ALU.mult,
                     op1=ALU.add,
-                    accum_out=sums[g][:, u, c : c + 1],
+                    accum_out=sums[g][:, u, 2 * c : 2 * c + 1],
                 )
+            return bd
+
+        def haar_pe(g, c, xt):
+            evens = []
+            for e in range(2):
+                ps = psum.tile([P, COLS], F32, name="ps", tag="acc")
+                v = xt[:, e, :].rearrange("p (i r j two) -> p i r j two", i=4, r=2, two=2)
+                nc.tensor.matmul(
+                    out=ps[:].rearrange("p (i j) -> p i j", i=4),
+                    lhsT=(identb[:] if g == 0 else nidentb[:]),
+                    rhs=v[:, :, 0, :, 0],
+                    start=True,
+                    stop=False,
+                )
+                nc.tensor.matmul(
+                    out=ps[:].rearrange("p (i j) -> p i j", i=4),
+                    lhsT=identb[:],
+                    rhs=v[:, :, 0, :, 1],
+                    start=False,
+                    stop=True,
+                )
+                evens.append(ps)
+            st = work.tile([P, 1024], F32, name="st", tag="sa", bufs=1)
+            w = xt[:].rearrange("p e (i r j two) -> p (e i) r j two", i=4, r=2, two=2)
+            nc.vector.tensor_tensor(
+                out=st[:].rearrange("p (a j) -> p a j", j=P),
+                in0=w[:, :, 1, :, 1],
+                in1=w[:, :, 1, :, 0],
+                op=(ALU.add if g == 0 else ALU.subtract),
+            )
+            bd = bands.tile([P, 2, 1024], F32, name="bd", tag="bd")
+            for e in range(2):
+                for u in range(2):
+                    nc.vector.scalar_tensor_tensor(
+                        out=bd[:, u, COLS * e : COLS * (e + 1)],
+                        in0=evens[e][:],
+                        scalar=(1.0 if u == 0 else -1.0),
+                        in1=st[:, COLS * e : COLS * (e + 1)],
+                        op0=ALU.mult,
+                        op1=ALU.add,
+                        accum_out=sums[g][:, u, 2 * c + e : 2 * c + e + 1],
+                    )
             return bd
 
         def first_guess(g):
@@ -207,12 +257,14 @@ def tile_hwdconv_t_kernel(tc, x, gn_scale, gn_bias, w_proj, out):
                         )
             return yp
 
-        def regroup(yp):
+        def regroup(yp, on_scalar):
             gr = work.tile([P, COLS, 4], BF16, name="gr", tag="gr", align_bytes=64)
-            nc.vector.tensor_copy(
-                out=gr[:].rearrange("p (c i) t -> p c t i", i=4),
-                in_=yp[:].rearrange("p t (c i) -> p c t i", i=4),
-            )
+            dst = gr[:].rearrange("p (c i) t -> p c t i", i=4)
+            src = yp[:].rearrange("p t (c i) -> p c t i", i=4)
+            if on_scalar:
+                nc.scalar.copy(out=dst, in_=src)
+            else:
+                nc.vector.tensor_copy(out=dst, in_=src)
             return gr
 
         def quantise(gr, codes, scales):
@@ -253,8 +305,11 @@ def tile_hwdconv_t_kernel(tc, x, gn_scale, gn_bias, w_proj, out):
         bd0 = []
         for c in range(NCH):
             xt = load_x(c)
-            st = haar_h(0, xt)
-            bd0.append(haar_v(0, c, st))
+            if c in PE_CHUNKS:
+                bd0.append(haar_pe(0, c, xt))
+            else:
+                st = haar_h(0, xt)
+                bd0.append(haar_v(0, c, st))
             if c == 0:
                 first_guess(0)
             if c == 2:
@@ -273,7 +328,7 @@ def tile_hwdconv_t_kernel(tc, x, gn_scale, gn_bias, w_proj, out):
                 yps.append(affine(0, bd0[c + 1], True))
                 xt = load_x(c + 1)
                 st = haar_h(1, xt)
-            gr = regroup(yps[c])
+            gr = regroup(yps[c], c in ACT_REGROUP)
             if c + 1 < NCH:
                 bd1.append(haar_v(1, c + 1, st))
             cols = slice(COLS * c, COLS * (c + 1))
@@ -283,7 +338,7 @@ def tile_hwdconv_t_kernel(tc, x, gn_scale, gn_bias, w_proj, out):
         finalise(1)
         yps = [affine(1, bd1[0], False)]
         for c in range(NCH):
-            gr = regroup(yps[c])
+            gr = regroup(yps[c], False)
             if c + 1 < NCH:
                 yps.append(affine(1, bd1[c + 1], False))
             c1 = work.tile([P, COLS], U32, name="c1", tag="c1", align_bytes=64)

@@ -18,9 +18,10 @@ K = 1024
 NPIX = 8192
 NCH = 16
 COLS = 512
-NB = 17
+NB = 18
 PE_CHUNKS = tuple(range(1, 13))
-ACT_REGROUP = (1, 4, 7, 10, 13)
+CA2 = 192
+CA3 = 64
 EPS = 1e-5
 FLOPS = 2 * CO * K * NPIX
 
@@ -36,14 +37,26 @@ def tile_hwdconv_t_kernel(tc, x, gn_scale, gn_bias, w_proj, out):
         bands = ctx.enter_context(tc.tile_pool(name="bands", bufs=NB))
         work = ctx.enter_context(tc.tile_pool(name="work", bufs=2))
         psum = ctx.enter_context(tc.psum_pool(name="psum", bufs=8))
+        ctx.enter_context(tc.manual_schedule())
 
         one = keep.tile([P, 1], F32, name="one")
         nc.vector.memset(one[:], 1.0)
         wsq = keep.tile([P, 1], F32, name="wsq")
         nc.scalar.activation(out=wsq[:], in_=one[:], func=ACTF.Sqrt)
 
+        gsb = keep.tile([P, 4, 2], BF16, name="gsb")
+        gbb = keep.tile([P, 4, 2], BF16, name="gbb")
+        with nc.allow_non_contiguous_dma(reason="two small vectors, four bytes a piece"):
+            nc.scalar.dma_start(out=gsb[:], in_=gn_scale.rearrange("(b p e) -> p b e", b=4, e=2))
+            nc.scalar.dma_start(out=gbb[:], in_=gn_bias.rearrange("(b p e) -> p b e", b=4, e=2))
+        gsf = keep.tile([P, 4, 2], F32, name="gsf")
+        gbf = keep.tile([P, 4, 2], F32, name="gbf")
+
         ident = keep.tile([P, P], F32, name="ident")
         make_identity(nc, ident[:])
+        sums = [keep.tile([P, 2, 2 * NCH], F32, name="sums%d" % g) for g in range(2)]
+        for g in range(2):
+            nc.vector.memset(sums[g][:], 0.0)
         rsum = keep.tile([P, 32], F32, name="rsum")
         nc.vector.tensor_reduce(
             out=rsum[:], in_=ident[:].rearrange("p (q j) -> p q j", j=4), axis=AX.X, op=ALU.add
@@ -56,28 +69,22 @@ def tile_hwdconv_t_kernel(tc, x, gn_scale, gn_bias, w_proj, out):
         nidentb = keep.tile([P, P], BF16, name="nidentb")
         nc.vector.tensor_scalar_mul(out=nidentb[:], in0=ident[:], scalar1=-1.0)
 
-        gsb = keep.tile([P, 4, 2], BF16, name="gsb")
-        gbb = keep.tile([P, 4, 2], BF16, name="gbb")
-        with nc.allow_non_contiguous_dma(reason="two small vectors, four bytes a piece"):
-            nc.scalar.dma_start(out=gsb[:], in_=gn_scale.rearrange("(b p e) -> p b e", b=4, e=2))
-            nc.scalar.dma_start(out=gbb[:], in_=gn_bias.rearrange("(b p e) -> p b e", b=4, e=2))
-        gsf = keep.tile([P, 4, 2], F32, name="gsf")
-        gbf = keep.tile([P, 4, 2], F32, name="gbf")
-        nc.vector.tensor_copy(out=gsf[:], in_=gsb[:])
-        nc.vector.tensor_copy(out=gbf[:], in_=gbb[:])
-
         wc = keep.tile([P, 2, CO], U32, name="wc", align_bytes=64)
         ws = keep.tile([P, 2, CO], U8, name="ws", align_bytes=64)
         codes0 = keep.tile([P, NPIX], U32, name="codes0", align_bytes=64)
-        scales0 = keep.tile([P, NPIX], U8, name="scales0", align_bytes=64)
+        scales0 = keep.tile([P, 4 * COLS], U8, name="scales0", align_bytes=64)
 
-        sums = [keep.tile([P, 2, 2 * NCH], F32, name="sums%d" % g) for g in range(2)]
-        for g in range(2):
-            nc.vector.memset(sums[g][:], 0.0)
         sqs = [keep.tile([P, 2, NCH], F32, name="sqs%d" % g) for g in range(2)]
         negc = [keep.tile([P, 2], F32, name="negc%d" % g) for g in range(2)]
         gain = [keep.tile([P, 2, 2], F32, name="gain%d" % g) for g in range(2)]
         shift = [keep.tile([P, 2, 2], F32, name="shift%d" % g) for g in range(2)]
+        small = {}
+
+        def code0(c):
+            return codes0[:, COLS * c : COLS * (c + 1)]
+
+        def scale0(c):
+            return scales0[4 * (c // 4) : P, COLS * (c % 4) : COLS * (c % 4 + 1)]
 
         def load_w():
             raws = []
@@ -89,7 +96,8 @@ def tile_hwdconv_t_kernel(tc, x, gn_scale, gn_bias, w_proj, out):
                 raws.append(wraw)
             return raws
 
-        def prep_w(raws):
+        def transpose_w(raws):
+            grouped = []
             for g in range(2):
                 wgr = work.tile([P, 2048], BF16, name="wgr", tag="gr", align_bytes=64)
                 wgv = wgr[:].bitcast(F32).rearrange("p (o u) -> p o u", u=2)
@@ -104,7 +112,14 @@ def tile_hwdconv_t_kernel(tc, x, gn_scale, gn_bias, w_proj, out):
                         out=wgv[:, 256 * h : 256 * h + 256, :].rearrange("p (a o) u -> p a o u", a=2),
                         in_=pt[:].rearrange("p a u o -> p a o u"),
                     )
-                nc.vector.quantize_mx(out=wc[:, g, :].bitcast(FP8X4), scales=ws[:, g, :], in_=wgr[:])
+                grouped.append(wgr)
+            return grouped
+
+        def quantise_w(grouped):
+            for g in range(2):
+                nc.vector.quantize_mx(
+                    out=wc[:, g, :].bitcast(FP8X4), scales=ws[:, g, :], in_=grouped[g][:]
+                )
 
         def load_x(c):
             xt = work.tile([P, 2, 2048], BF16, name="xt", tag="xa")
@@ -114,10 +129,12 @@ def tile_hwdconv_t_kernel(tc, x, gn_scale, gn_bias, w_proj, out):
         def haar_h(g, xt):
             st = work.tile([P, 2048], F32, name="st", tag="sa", bufs=1)
             pair = xt[:].rearrange("p e (n two) -> p (e n) two", two=2)
-            if g == 0:
-                nc.vector.tensor_tensor(out=st[:], in0=pair[:, :, 0], in1=pair[:, :, 1], op=ALU.add)
-            else:
-                nc.vector.tensor_tensor(out=st[:], in0=pair[:, :, 1], in1=pair[:, :, 0], op=ALU.subtract)
+            nc.vector.tensor_tensor(
+                out=st[:],
+                in0=pair[:, :, 1],
+                in1=pair[:, :, 0],
+                op=(ALU.add if g == 0 else ALU.subtract),
+            )
             return st
 
         def haar_v(g, c, st):
@@ -135,7 +152,7 @@ def tile_hwdconv_t_kernel(tc, x, gn_scale, gn_bias, w_proj, out):
                 )
             return bd
 
-        def haar_pe(g, c, xt):
+        def even_rows_pe(g, xt):
             evens = []
             for e in range(2):
                 ps = psum.tile([P, COLS], F32, name="ps", tag="acc")
@@ -155,6 +172,9 @@ def tile_hwdconv_t_kernel(tc, x, gn_scale, gn_bias, w_proj, out):
                     stop=True,
                 )
                 evens.append(ps)
+            return evens
+
+        def odd_rows(g, xt):
             st = work.tile([P, 1024], F32, name="st", tag="sa", bufs=1)
             w = xt[:].rearrange("p e (i r j two) -> p (e i) r j two", i=4, r=2, two=2)
             nc.vector.tensor_tensor(
@@ -163,6 +183,9 @@ def tile_hwdconv_t_kernel(tc, x, gn_scale, gn_bias, w_proj, out):
                 in1=w[:, :, 1, :, 0],
                 op=(ALU.add if g == 0 else ALU.subtract),
             )
+            return st
+
+        def haar_v_pe(g, c, evens, st):
             bd = bands.tile([P, 2, 1024], F32, name="bd", tag="bd")
             for e in range(2):
                 for u in range(2):
@@ -177,9 +200,12 @@ def tile_hwdconv_t_kernel(tc, x, gn_scale, gn_bias, w_proj, out):
                     )
             return bd
 
-        def first_guess(g):
+        def guess_mm(g):
             pz = psum.tile([P, 2], F32, name="pz", tag="acc")
             nc.tensor.matmul(out=pz[:], lhsT=gsum, rhs=sums[g][:, :, 0], start=True, stop=True)
+            return pz
+
+        def guess_out(g, pz):
             nc.vector.tensor_scalar_mul(out=negc[g][:], in0=pz[:], scalar1=-1.0 / (8 * COLS))
 
         def squares(g, c, bd):
@@ -194,39 +220,49 @@ def tile_hwdconv_t_kernel(tc, x, gn_scale, gn_bias, w_proj, out):
                     accum_out=sqs[g][:, u, c : c + 1],
                 )
 
-        def finalise(g):
-            tot = keep.tile([P, 4], F32, name="tot%d" % g)
+        def sm(name, g, shape):
+            t = keep.tile(shape, F32, name="%s%d" % (name, g))
+            small[(name, g)] = t
+            return t
+
+        def fin_a(g):
+            tot = sm("tot", g, [P, 4])
             nc.vector.tensor_reduce(out=tot[:, 0:2], in_=sums[g][:], axis=AX.X, op=ALU.add)
             nc.vector.tensor_reduce(out=tot[:, 2:4], in_=sqs[g][:], axis=AX.X, op=ALU.add)
             pg = psum.tile([P, 4], F32, name="pg", tag="acc")
             nc.tensor.matmul(out=pg[:], lhsT=gsum, rhs=tot[:], start=True, stop=True)
-            mv = keep.tile([P, 4], F32, name="mv%d" % g)
+            return pg
+
+        def fin_b(g, pg):
+            mv = sm("mv", g, [P, 4])
             nc.vector.tensor_scalar_mul(out=mv[:], in0=pg[:], scalar1=1.0 / (8 * NPIX))
-            dl = keep.tile([P, 2], F32, name="dl%d" % g)
+            dl = sm("dl", g, [P, 2])
             nc.vector.tensor_tensor(out=dl[:], in0=mv[:, 0:2], in1=negc[g][:], op=ALU.add)
-            d2 = keep.tile([P, 2], F32, name="d2%d" % g)
+            d2 = sm("d2", g, [P, 2])
             nc.vector.tensor_tensor(out=d2[:], in0=dl[:], in1=dl[:], op=ALU.mult)
-            var = keep.tile([P, 2], F32, name="var%d" % g)
+            var = sm("var", g, [P, 2])
             nc.vector.tensor_tensor(out=var[:], in0=mv[:, 2:4], in1=d2[:], op=ALU.subtract)
-            ve = keep.tile([P, 2], F32, name="ve%d" % g)
+            ve = sm("ve", g, [P, 2])
             nc.vector.tensor_scalar(
                 out=ve[:], in0=var[:], scalar1=0.0, scalar2=4.0 * EPS, op0=ALU.max, op1=ALU.add
             )
-            sd = keep.tile([P, 2], F32, name="sd%d" % g)
+            sd = sm("sd", g, [P, 2])
             nc.scalar.activation(out=sd[:], in_=ve[:], func=ACTF.Sqrt)
-            rs = keep.tile([P, 2], F32, name="rs%d" % g)
-            nc.vector.reciprocal(out=rs[:], in_=sd[:])
+
+        def fin_c(g):
+            rs = sm("rs", g, [P, 2])
+            nc.vector.reciprocal(out=rs[:], in_=small[("sd", g)][:])
             nc.vector.tensor_tensor(
                 out=gain[g][:],
                 in0=gsf[:, 2 * g : 2 * g + 2, :],
                 in1=rs[:].unsqueeze(2).to_broadcast([P, 2, 2]),
                 op=ALU.mult,
             )
-            mg = keep.tile([P, 2, 2], F32, name="mg%d" % g)
+            mg = sm("mg", g, [P, 2, 2])
             nc.vector.tensor_tensor(
                 out=mg[:],
                 in0=gain[g][:],
-                in1=mv[:, 0:2].unsqueeze(2).to_broadcast([P, 2, 2]),
+                in1=small[("mv", g)][:, 0:2].unsqueeze(2).to_broadcast([P, 2, 2]),
                 op=ALU.mult,
             )
             nc.vector.tensor_tensor(
@@ -257,14 +293,17 @@ def tile_hwdconv_t_kernel(tc, x, gn_scale, gn_bias, w_proj, out):
                         )
             return yp
 
-        def regroup(yp, on_scalar):
+        def regroup(yp, ca):
             gr = work.tile([P, COLS, 4], BF16, name="gr", tag="gr", align_bytes=64)
-            dst = gr[:].rearrange("p (c i) t -> p c t i", i=4)
-            src = yp[:].rearrange("p t (c i) -> p c t i", i=4)
-            if on_scalar:
-                nc.scalar.copy(out=dst, in_=src)
-            else:
-                nc.vector.tensor_copy(out=dst, in_=src)
+            if ca > 0:
+                nc.scalar.copy(
+                    out=gr[:, 0:ca, :].rearrange("p (c i) t -> p c t i", i=4),
+                    in_=yp[:, :, 0:ca].rearrange("p t (c i) -> p c t i", i=4),
+                )
+            nc.vector.tensor_copy(
+                out=gr[:, ca:COLS, :].rearrange("p (c i) t -> p c t i", i=4),
+                in_=yp[:, :, ca:COLS].rearrange("p t (c i) -> p c t i", i=4),
+            )
             return gr
 
         def quantise(gr, codes, scales):
@@ -272,11 +311,8 @@ def tile_hwdconv_t_kernel(tc, x, gn_scale, gn_bias, w_proj, out):
                 out=codes.bitcast(FP8X4), scales=scales, in_=gr[:].rearrange("p c t -> p (c t)")
             )
 
-        def project(c, c1, s1):
-            cols = slice(COLS * c, COLS * (c + 1))
-            ost = work.tile(
-                [P, 4, COLS], F32, name="ost", tag=("sa" if c % 3 == 2 else "xa"), bufs=(1 if c % 3 == 2 else 2)
-            )
+        def multiply(c, c1, s1):
+            accs = []
             for a in range(4):
                 acc = psum.tile([P, COLS], F32, name="acc", tag="acc")
                 m = slice(P * a, P * (a + 1))
@@ -284,8 +320,8 @@ def tile_hwdconv_t_kernel(tc, x, gn_scale, gn_bias, w_proj, out):
                     out=acc[:],
                     lhsT=wc[:, 0, m].bitcast(FP8X4),
                     lhsT_scale=ws[:, 0, m],
-                    rhs=codes0[:, cols].bitcast(FP8X4),
-                    rhs_scale=scales0[:, cols],
+                    rhs=code0(c).bitcast(FP8X4),
+                    rhs_scale=scale0(c),
                     start=True,
                     stop=False,
                 )
@@ -298,50 +334,98 @@ def tile_hwdconv_t_kernel(tc, x, gn_scale, gn_bias, w_proj, out):
                     start=False,
                     stop=True,
                 )
-                nc.scalar.activation(out=ost[:, a, :], in_=acc[:], func=ACTF.Relu)
-            nc.sync.dma_start(out=ov[:, :, cols], in_=ost[:])
+                accs.append(acc)
+            return accs
+
+        def relu_store(c, accs, last):
+            cols = slice(COLS * c, COLS * (c + 1))
+            ost = work.tile(
+                [P, 4, COLS], F32, name="ost", tag=("sa" if c % 3 == 2 else "xa"), bufs=(1 if c % 3 == 2 else 2)
+            )
+            for a in range(4):
+                if last and a % 2 == 1:
+                    nc.vector.tensor_scalar_max(out=ost[:, a, :], in0=accs[a][:], scalar1=0.0)
+                else:
+                    nc.scalar.activation(out=ost[:, a, :], in_=accs[a][:], func=ACTF.Relu)
+                if last:
+                    nc.sync.dma_start(out=ov[:, a, cols], in_=ost[:, a, :])
+            if not last:
+                nc.sync.dma_start(out=ov[:, :, cols], in_=ost[:])
 
         raws = load_w()
         bd0 = []
+        pz = None
+        grouped = None
         for c in range(NCH):
             xt = load_x(c)
             if c in PE_CHUNKS:
-                bd0.append(haar_pe(0, c, xt))
+                evens = even_rows_pe(0, xt)
+                st = odd_rows(0, xt)
             else:
                 st = haar_h(0, xt)
+            if c == 1:
+                guess_out(0, pz)
+            if c == 5:
+                quantise_w(grouped)
+                nc.vector.tensor_copy(out=gsf[:], in_=gsb[:])
+                nc.vector.tensor_copy(out=gbf[:], in_=gbb[:])
+            if c in PE_CHUNKS:
+                bd0.append(haar_v_pe(0, c, evens, st))
+            else:
                 bd0.append(haar_v(0, c, st))
             if c == 0:
-                first_guess(0)
+                pz = guess_mm(0)
+            if c >= 1:
+                squares(0, c - 1, bd0[c - 1])
             if c == 2:
-                prep_w(raws)
-            squares(0, c, bd0[c])
+                grouped = transpose_w(raws)
+        squares(0, NCH - 1, bd0[NCH - 1])
 
         bd1 = []
         xt = load_x(0)
         st = haar_h(1, xt)
         bd1.append(haar_v(1, 0, st))
-        first_guess(1)
-        finalise(0)
+        pz = guess_mm(1)
+        pg = fin_a(0)
+        xt = load_x(1)
+        st = haar_h(1, xt)
+        guess_out(1, pz)
+        fin_b(0, pg)
+        bd1.append(haar_v(1, 1, st))
+        fin_c(0)
         yps = [affine(0, bd0[0], True)]
+        squares(1, 0, bd1[0])
         for c in range(NCH):
-            if c + 1 < NCH:
-                yps.append(affine(0, bd0[c + 1], True))
-                xt = load_x(c + 1)
+            if c + 2 < NCH:
+                xt = load_x(c + 2)
                 st = haar_h(1, xt)
-            gr = regroup(yps[c], c in ACT_REGROUP)
-            if c + 1 < NCH:
-                bd1.append(haar_v(1, c + 1, st))
-            cols = slice(COLS * c, COLS * (c + 1))
-            quantise(gr, codes0[:, cols], scales0[:, cols])
-            squares(1, c, bd1[c])
+            if c == NCH - 2:
+                squares(1, NCH - 1, bd1[NCH - 1])
+                yps.append(affine(0, bd0[NCH - 1], False))
+            gr = regroup(yps[c], CA2 if c < NCH - 2 else 0)
+            if c + 1 < NCH - 1:
+                yps.append(affine(0, bd0[c + 1], True))
+            if c + 2 < NCH:
+                bd1.append(haar_v(1, c + 2, st))
+            if c == NCH - 1:
+                fin_b(1, pg)
+            quantise(gr, code0(c), scale0(c))
+            if c + 1 < NCH - 1:
+                squares(1, c + 1, bd1[c + 1])
+            if c == NCH - 2:
+                pg = fin_a(1)
+        fin_c(1)
 
-        finalise(1)
         yps = [affine(1, bd1[0], False)]
+        accs = None
         for c in range(NCH):
-            gr = regroup(yps[c], False)
+            gr = regroup(yps[c], CA3)
+            if c >= 1:
+                relu_store(c - 1, accs, False)
             if c + 1 < NCH:
                 yps.append(affine(1, bd1[c + 1], False))
             c1 = work.tile([P, COLS], U32, name="c1", tag="c1", align_bytes=64)
             s1 = work.tile([P, COLS], U8, name="s1", tag="s1", align_bytes=64)
             quantise(gr, c1[:], s1[:])
-            project(c, c1, s1)
+            accs = multiply(c, c1, s1)
+        relu_store(NCH - 1, accs, True)

@@ -19,9 +19,10 @@ NPIX = 8192
 NCH = 16
 COLS = 512
 NB = 18
-PE_CHUNKS = tuple(range(1, 13))
-CA2 = 192
-CA3 = 64
+PE_CHUNKS = (13, 14, 15)
+NV = 13
+CA2 = 352
+CA3 = 128
 EPS = 1e-5
 FLOPS = 2 * CO * K * NPIX
 
@@ -46,9 +47,6 @@ def tile_hwdconv_t_kernel(tc, x, gn_scale, gn_bias, w_proj, out):
 
         gsb = keep.tile([P, 4, 2], BF16, name="gsb")
         gbb = keep.tile([P, 4, 2], BF16, name="gbb")
-        with nc.allow_non_contiguous_dma(reason="two small vectors, four bytes a piece"):
-            nc.scalar.dma_start(out=gsb[:], in_=gn_scale.rearrange("(b p e) -> p b e", b=4, e=2))
-            nc.scalar.dma_start(out=gbb[:], in_=gn_bias.rearrange("(b p e) -> p b e", b=4, e=2))
         gsf = keep.tile([P, 4, 2], F32, name="gsf")
         gbf = keep.tile([P, 4, 2], F32, name="gbf")
 
@@ -78,6 +76,7 @@ def tile_hwdconv_t_kernel(tc, x, gn_scale, gn_bias, w_proj, out):
         negc = [keep.tile([P, 2], F32, name="negc%d" % g) for g in range(2)]
         gain = [keep.tile([P, 2, 2], F32, name="gain%d" % g) for g in range(2)]
         shift = [keep.tile([P, 2, 2], F32, name="shift%d" % g) for g in range(2)]
+        sums_pe = keep.tile([P, 2, 2 * len(PE_CHUNKS)], F32, name="sums_pe")
         small = {}
 
         def code0(c):
@@ -89,12 +88,17 @@ def tile_hwdconv_t_kernel(tc, x, gn_scale, gn_bias, w_proj, out):
         def load_w():
             raws = []
             for h in range(2):
-                wraw = work.tile([P, 2048], BF16, name="wraw", tag="yp")
-                nc.scalar.dma_start(
+                wraw = work.tile([P, 2048], BF16, name="wraw", tag="yp", align_bytes=64)
+                nc.sync.dma_start(
                     out=wraw[:].rearrange("p (a k) -> p a k", a=2), in_=wv[:, 2 * h : 2 * h + 2, :]
                 )
                 raws.append(wraw)
             return raws
+
+        def load_gn():
+            with nc.allow_non_contiguous_dma(reason="two small vectors, four bytes a piece"):
+                nc.sync.dma_start(out=gsb[:], in_=gn_scale.rearrange("(b p e) -> p b e", b=4, e=2))
+                nc.sync.dma_start(out=gbb[:], in_=gn_bias.rearrange("(b p e) -> p b e", b=4, e=2))
 
         def transpose_w(raws):
             grouped = []
@@ -126,6 +130,18 @@ def tile_hwdconv_t_kernel(tc, x, gn_scale, gn_bias, w_proj, out):
             nc.sync.dma_start(out=xt[:], in_=xv[:, :, 2048 * c : 2048 * (c + 1)])
             return xt
 
+        def first_chunk():
+            xt = work.tile([P, 2, 2048], BF16, name="xt", tag="xa")
+            st = work.tile([P, 2048], F32, name="st", tag="sa", bufs=1)
+            for e in range(2):
+                nc.sync.dma_start(out=xt[:, e, :], in_=xv[:, e, 0:2048])
+            for e in range(2):
+                pair = xt[:, e, :].rearrange("p (n two) -> p n two", two=2)
+                nc.vector.tensor_tensor(
+                    out=st[:, 1024 * e : 1024 * (e + 1)], in0=pair[:, :, 1], in1=pair[:, :, 0], op=ALU.add
+                )
+            return st
+
         def haar_h(g, xt):
             st = work.tile([P, 2048], F32, name="st", tag="sa", bufs=1)
             pair = xt[:].rearrange("p e (n two) -> p (e n) two", two=2)
@@ -152,51 +168,37 @@ def tile_hwdconv_t_kernel(tc, x, gn_scale, gn_bias, w_proj, out):
                 )
             return bd
 
-        def even_rows_pe(g, xt):
-            evens = []
+        def bands_pe(c, tag):
+            banks = []
+            views = []
             for e in range(2):
-                ps = psum.tile([P, COLS], F32, name="ps", tag="acc")
-                v = xt[:, e, :].rearrange("p (i r j two) -> p i r j two", i=4, r=2, two=2)
-                nc.tensor.matmul(
-                    out=ps[:].rearrange("p (i j) -> p i j", i=4),
-                    lhsT=(identb[:] if g == 0 else nidentb[:]),
-                    rhs=v[:, :, 0, :, 0],
-                    start=True,
-                    stop=False,
-                )
-                nc.tensor.matmul(
-                    out=ps[:].rearrange("p (i j) -> p i j", i=4),
-                    lhsT=identb[:],
-                    rhs=v[:, :, 0, :, 1],
-                    start=False,
-                    stop=True,
-                )
-                evens.append(ps)
-            return evens
+                xe = work.tile([P, 2048], BF16, name="xe", tag=tag, align_bytes=64)
+                nc.gpsimd.dma_start(out=xe[:], in_=xv[:, e, 2048 * c : 2048 * (c + 1)])
+                views.append(xe[:].rearrange("p (i r j two) -> p i r j two", i=4, r=2, two=2))
+            for u in range(2):
+                for e in range(2):
+                    ps = psum.tile([P, COLS], F32, name="ps", tag="acc")
+                    for n in range(4):
+                        r = n // 2
+                        nc.tensor.matmul(
+                            out=ps[:].rearrange("p (i j) -> p i j", i=4),
+                            lhsT=(nidentb[:] if (u == 1 and r == 0) else identb[:]),
+                            rhs=views[e][:, :, r, :, n % 2],
+                            start=(n == 0),
+                            stop=(n == 3),
+                        )
+                    banks.append(ps)
+            return banks
 
-        def odd_rows(g, xt):
-            st = work.tile([P, 1024], F32, name="st", tag="sa", bufs=1)
-            w = xt[:].rearrange("p e (i r j two) -> p (e i) r j two", i=4, r=2, two=2)
-            nc.vector.tensor_tensor(
-                out=st[:].rearrange("p (a j) -> p a j", j=P),
-                in0=w[:, :, 1, :, 1],
-                in1=w[:, :, 1, :, 0],
-                op=(ALU.add if g == 0 else ALU.subtract),
-            )
-            return st
-
-        def haar_v_pe(g, c, evens, st):
+        def evacuate_pe(n, banks):
             bd = bands.tile([P, 2, 1024], F32, name="bd", tag="bd")
-            for e in range(2):
-                for u in range(2):
-                    nc.vector.scalar_tensor_tensor(
+            for u in range(2):
+                for e in range(2):
+                    nc.scalar.activation(
                         out=bd[:, u, COLS * e : COLS * (e + 1)],
-                        in0=evens[e][:],
-                        scalar=(1.0 if u == 0 else -1.0),
-                        in1=st[:, COLS * e : COLS * (e + 1)],
-                        op0=ALU.mult,
-                        op1=ALU.add,
-                        accum_out=sums[g][:, u, 2 * c + e : 2 * c + e + 1],
+                        in_=banks[2 * u + e][:],
+                        func=ACTF.Identity,
+                        accum_out=sums_pe[:, u, 2 * n + e : 2 * n + e + 1],
                     )
             return bd
 
@@ -229,6 +231,10 @@ def tile_hwdconv_t_kernel(tc, x, gn_scale, gn_bias, w_proj, out):
             tot = sm("tot", g, [P, 4])
             nc.vector.tensor_reduce(out=tot[:, 0:2], in_=sums[g][:], axis=AX.X, op=ALU.add)
             nc.vector.tensor_reduce(out=tot[:, 2:4], in_=sqs[g][:], axis=AX.X, op=ALU.add)
+            if g == 0:
+                tpe = sm("tpe", g, [P, 2])
+                nc.vector.tensor_reduce(out=tpe[:], in_=sums_pe[:], axis=AX.X, op=ALU.add)
+                nc.vector.tensor_tensor(out=tot[:, 0:2], in0=tot[:, 0:2], in1=tpe[:], op=ALU.add)
             pg = psum.tile([P, 4], F32, name="pg", tag="acc")
             nc.tensor.matmul(out=pg[:], lhsT=gsum, rhs=tot[:], start=True, stop=True)
             return pg
@@ -270,7 +276,7 @@ def tile_hwdconv_t_kernel(tc, x, gn_scale, gn_bias, w_proj, out):
             )
 
         def affine(g, bd, on_scalar):
-            yp = work.tile([P, 4, COLS], BF16, name="yp", tag="yp")
+            yp = work.tile([P, 4, COLS], BF16, name="yp", tag="yp", align_bytes=64)
             for u in range(2):
                 for e in range(2):
                     src = bd[:, u, COLS * e : COLS * (e + 1)]
@@ -352,34 +358,45 @@ def tile_hwdconv_t_kernel(tc, x, gn_scale, gn_bias, w_proj, out):
             if not last:
                 nc.sync.dma_start(out=ov[:, :, cols], in_=ost[:])
 
-        raws = load_w()
+        raws = None
         bd0 = []
+        ids0 = []
         pz = None
         grouped = None
-        for c in range(NCH):
-            xt = load_x(c)
-            if c in PE_CHUNKS:
-                evens = even_rows_pe(0, xt)
-                st = odd_rows(0, xt)
+        pending = []
+        prev = None
+        for c in range(NV):
+            if c == 0:
+                st = first_chunk()
             else:
+                xt = load_x(c)
                 st = haar_h(0, xt)
             if c == 1:
+                raws = load_w()
                 guess_out(0, pz)
+            if c == 2:
+                load_gn()
             if c == 5:
                 quantise_w(grouped)
                 nc.vector.tensor_copy(out=gsf[:], in_=gsb[:])
                 nc.vector.tensor_copy(out=gbf[:], in_=gbb[:])
-            if c in PE_CHUNKS:
-                bd0.append(haar_v_pe(0, c, evens, st))
-            else:
-                bd0.append(haar_v(0, c, st))
+            if c >= 1:
+                squares(0, c - 1, prev)
+            prev = haar_v(0, c, st)
+            bd0.append(prev)
+            ids0.append(c)
             if c == 0:
                 pz = guess_mm(0)
-            if c >= 1:
-                squares(0, c - 1, bd0[c - 1])
             if c == 2:
                 grouped = transpose_w(raws)
-        squares(0, NCH - 1, bd0[NCH - 1])
+            if c in (6, 8, 10):
+                n = (c - 6) // 2
+                bd0.append(evacuate_pe(n, pending[n]))
+                ids0.append(PE_CHUNKS[n])
+                squares(0, PE_CHUNKS[n], bd0[len(bd0) - 1])
+            if c in (3, 5, 7):
+                pending.append(bands_pe(PE_CHUNKS[(c - 3) // 2], "gr" if c == 5 else "yp"))
+        squares(0, NV - 1, prev)
 
         bd1 = []
         xt = load_x(0)
@@ -409,7 +426,7 @@ def tile_hwdconv_t_kernel(tc, x, gn_scale, gn_bias, w_proj, out):
                 bd1.append(haar_v(1, c + 2, st))
             if c == NCH - 1:
                 fin_b(1, pg)
-            quantise(gr, code0(c), scale0(c))
+            quantise(gr, code0(ids0[c]), scale0(ids0[c]))
             if c + 1 < NCH - 1:
                 squares(1, c + 1, bd1[c + 1])
             if c == NCH - 2:

@@ -21,8 +21,8 @@ COLS = 512
 NB = 18
 PE_CHUNKS = (13, 14, 15)
 NV = 13
-CA2 = 352
-CA3 = 128
+CA2 = 192
+CA3 = 64
 EPS = 1e-5
 FLOPS = 2 * CO * K * NPIX
 

@@ -18,9 +18,11 @@ K = 1024
 NPIX = 8192
 NCH = 16
 COLS = 512
-NB = 18
+SLOTS = 18
+SLOT = 4 * COLS
+UNITS = ((0,), (1, 2), (3, 4), (5, 6), (7, 8), (9, 10), (11, 12))
 PE_CHUNKS = (13, 14, 15)
-NV = 13
+PAIRS = NCH // 2
 CA2 = 192
 CA3 = 64
 EPS = 1e-5
@@ -35,8 +37,7 @@ def tile_hwdconv_t_kernel(tc, x, gn_scale, gn_bias, w_proj, out):
 
     with ExitStack() as ctx:
         keep = ctx.enter_context(tc.tile_pool(name="keep", bufs=1))
-        bands = ctx.enter_context(tc.tile_pool(name="bands", bufs=NB))
-        work = ctx.enter_context(tc.tile_pool(name="work", bufs=2))
+        work = ctx.enter_context(tc.tile_pool(name="work", bufs=3))
         psum = ctx.enter_context(tc.psum_pool(name="psum", bufs=8))
         ctx.enter_context(tc.manual_schedule())
 
@@ -52,9 +53,9 @@ def tile_hwdconv_t_kernel(tc, x, gn_scale, gn_bias, w_proj, out):
 
         ident = keep.tile([P, P], F32, name="ident")
         make_identity(nc, ident[:])
-        sums = [keep.tile([P, 2, 2 * NCH], F32, name="sums%d" % g) for g in range(2)]
-        for g in range(2):
-            nc.vector.memset(sums[g][:], 0.0)
+        nsum = (len(UNITS), PAIRS)
+        nsq = (len(UNITS) + len(PE_CHUNKS), PAIRS)
+        sums = [keep.tile([P, 2, nsum[g]], F32, name="sums%d" % g) for g in range(2)]
         rsum = keep.tile([P, 32], F32, name="rsum")
         nc.vector.tensor_reduce(
             out=rsum[:], in_=ident[:].rearrange("p (q j) -> p q j", j=4), axis=AX.X, op=ALU.add
@@ -72,7 +73,12 @@ def tile_hwdconv_t_kernel(tc, x, gn_scale, gn_bias, w_proj, out):
         codes0 = keep.tile([P, NPIX], U32, name="codes0", align_bytes=64)
         scales0 = keep.tile([P, 4 * COLS], U8, name="scales0", align_bytes=64)
 
-        sqs = [keep.tile([P, 2, NCH], F32, name="sqs%d" % g) for g in range(2)]
+        bands = keep.tile([P, SLOTS * SLOT], F32, name="bands", align_bytes=64)
+        yp = keep.tile([P, 2, 4, COLS], BF16, name="yp", align_bytes=64)
+        gr = keep.tile([P, 2, COLS, 4], BF16, name="gr", align_bytes=64)
+        junk = keep.tile([P, 2048], BF16, name="junk")
+
+        sqs = [keep.tile([P, 2, nsq[g]], F32, name="sqs%d" % g) for g in range(2)]
         negc = [keep.tile([P, 2], F32, name="negc%d" % g) for g in range(2)]
         gain = [keep.tile([P, 2, 2], F32, name="gain%d" % g) for g in range(2)]
         shift = [keep.tile([P, 2, 2], F32, name="shift%d" % g) for g in range(2)]
@@ -85,29 +91,27 @@ def tile_hwdconv_t_kernel(tc, x, gn_scale, gn_bias, w_proj, out):
         def scale0(c):
             return scales0[4 * (c // 4) : P, COLS * (c % 4) : COLS * (c % 4 + 1)]
 
+        def band(slot, n, u):
+            return bands[:, SLOT * slot : SLOT * (slot + n)].rearrange("p (n u x) -> p n u x", n=n, u=2)[:, :, u, :]
+
         def load_w():
-            raws = []
             for h in range(2):
-                wraw = work.tile([P, 2048], BF16, name="wraw", tag="yp", align_bytes=64)
                 nc.sync.dma_start(
-                    out=wraw[:].rearrange("p (a k) -> p a k", a=2), in_=wv[:, 2 * h : 2 * h + 2, :]
+                    out=yp[:, h, :, :].rearrange("p t x -> p (t x)").rearrange("p (a k) -> p a k", a=2),
+                    in_=wv[:, 2 * h : 2 * h + 2, :],
                 )
-                raws.append(wraw)
-            return raws
 
         def load_gn():
             with nc.allow_non_contiguous_dma(reason="two small vectors, four bytes a piece"):
                 nc.sync.dma_start(out=gsb[:], in_=gn_scale.rearrange("(b p e) -> p b e", b=4, e=2))
                 nc.sync.dma_start(out=gbb[:], in_=gn_bias.rearrange("(b p e) -> p b e", b=4, e=2))
 
-        def transpose_w(raws):
-            grouped = []
+        def transpose_w():
             for g in range(2):
-                wgr = work.tile([P, 2048], BF16, name="wgr", tag="gr", align_bytes=64)
-                wgv = wgr[:].bitcast(F32).rearrange("p (o u) -> p o u", u=2)
+                wgv = gr[:, g, :, :].rearrange("p c t -> p (c t)").bitcast(F32).rearrange("p (o u) -> p o u", u=2)
                 for h in range(2):
                     pt = psum.tile([P, 2, 2, P], F32, name="pt", tag="acc")
-                    src = raws[h][:].bitcast(F32)
+                    src = yp[:, h, :, :].rearrange("p t x -> p (t x)").bitcast(F32)
                     for a in range(2):
                         for u in range(2):
                             lo = 512 * a + 256 * g + 128 * u
@@ -116,65 +120,54 @@ def tile_hwdconv_t_kernel(tc, x, gn_scale, gn_bias, w_proj, out):
                         out=wgv[:, 256 * h : 256 * h + 256, :].rearrange("p (a o) u -> p a o u", a=2),
                         in_=pt[:].rearrange("p a u o -> p a o u"),
                     )
-                grouped.append(wgr)
-            return grouped
 
-        def quantise_w(grouped):
+        def quantise_w():
             for g in range(2):
                 nc.vector.quantize_mx(
-                    out=wc[:, g, :].bitcast(FP8X4), scales=ws[:, g, :], in_=grouped[g][:]
+                    out=wc[:, g, :].bitcast(FP8X4),
+                    scales=ws[:, g, :],
+                    in_=gr[:, g, :, :].rearrange("p c t -> p (c t)"),
                 )
 
-        def load_x(c):
-            xt = work.tile([P, 2, 2048], BF16, name="xt", tag="xa")
-            nc.sync.dma_start(out=xt[:], in_=xv[:, :, 2048 * c : 2048 * (c + 1)])
+        def load_x(c, halves=False):
+            xt = work.tile([P, 2, 2048], BF16, name="xt", tag="xa", align_bytes=64)
+            if halves:
+                for e in range(2):
+                    nc.sync.dma_start(out=xt[:, e, :], in_=xv[:, e, 2048 * c : 2048 * (c + 1)])
+            else:
+                nc.sync.dma_start(out=xt[:], in_=xv[:, :, 2048 * c : 2048 * (c + 1)])
             return xt
 
-        def first_chunk():
-            xt = work.tile([P, 2, 2048], BF16, name="xt", tag="xa")
-            st = work.tile([P, 2048], F32, name="st", tag="sa", bufs=1)
-            for e in range(2):
-                nc.sync.dma_start(out=xt[:, e, :], in_=xv[:, e, 0:2048])
-            for e in range(2):
-                pair = xt[:, e, :].rearrange("p (n two) -> p n two", two=2)
+        def haar_h(g, xt, slot, halves=False):
+            src = xt[:].rearrange("p e (i r j two) -> p (e i) r j two", r=2, j=P, two=2)
+            dst = bands[:, SLOT * slot : SLOT * (slot + 1)].rearrange("p (r ei j) -> p ei r j", r=2, j=P)
+            parts = (slice(0, 4), slice(4, 8)) if halves else (slice(0, 8),)
+            for part in parts:
                 nc.vector.tensor_tensor(
-                    out=st[:, 1024 * e : 1024 * (e + 1)], in0=pair[:, :, 1], in1=pair[:, :, 0], op=ALU.add
+                    out=dst[:, part, :, :],
+                    in0=src[:, part, :, :, 1],
+                    in1=src[:, part, :, :, 0],
+                    op=(ALU.add if g == 0 else ALU.subtract),
                 )
-            return st
 
-        def haar_h(g, xt):
-            st = work.tile([P, 2048], F32, name="st", tag="sa", bufs=1)
-            pair = xt[:].rearrange("p e (n two) -> p (e n) two", two=2)
-            nc.vector.tensor_tensor(
-                out=st[:],
-                in0=pair[:, :, 1],
-                in1=pair[:, :, 0],
-                op=(ALU.add if g == 0 else ALU.subtract),
+        def haar_v(g, slot, n, col, u):
+            nc.vector.scalar_tensor_tensor(
+                out=band(slot, n, u),
+                in0=band(slot, n, 0),
+                scalar=(-1.0 if u == 1 else 2.0),
+                in1=band(slot, n, 1),
+                op0=ALU.mult,
+                op1=ALU.add,
+                accum_out=sums[g][:, u, col : col + 1],
             )
-            return st
 
-        def haar_v(g, c, st):
-            bd = bands.tile([P, 2, 1024], F32, name="bd", tag="bd")
-            rows = st[:].rearrange("p (a r j) -> p a r j", r=2, j=P)
-            for u in range(2):
-                nc.vector.scalar_tensor_tensor(
-                    out=bd[:, u, :].rearrange("p (a j) -> p a j", j=P),
-                    in0=rows[:, :, 0, :],
-                    scalar=(1.0 if u == 0 else -1.0),
-                    in1=rows[:, :, 1, :],
-                    op0=ALU.mult,
-                    op1=ALU.add,
-                    accum_out=sums[g][:, u, 2 * c : 2 * c + 1],
-                )
-            return bd
-
-        def bands_pe(c, tag):
+        def bands_pe(c, store):
             banks = []
             views = []
             for e in range(2):
-                xe = work.tile([P, 2048], BF16, name="xe", tag=tag, align_bytes=64)
-                nc.gpsimd.dma_start(out=xe[:], in_=xv[:, e, 2048 * c : 2048 * (c + 1)])
-                views.append(xe[:].rearrange("p (i r j two) -> p i r j two", i=4, r=2, two=2))
+                xe = store[:, 2048 * e : 2048 * (e + 1)]
+                nc.gpsimd.dma_start(out=xe, in_=xv[:, e, 2048 * c : 2048 * (c + 1)])
+                views.append(xe.rearrange("p (i r j two) -> p i r j two", i=4, r=2, two=2))
             for u in range(2):
                 for e in range(2):
                     ps = psum.tile([P, COLS], F32, name="ps", tag="acc")
@@ -191,36 +184,37 @@ def tile_hwdconv_t_kernel(tc, x, gn_scale, gn_bias, w_proj, out):
             return banks
 
         def evacuate_pe(n, banks):
-            bd = bands.tile([P, 2, 1024], F32, name="bd", tag="bd")
             for u in range(2):
                 for e in range(2):
+                    lo = SLOT * PE_CHUNKS[n] + 2 * COLS * u + COLS * e
                     nc.scalar.activation(
-                        out=bd[:, u, COLS * e : COLS * (e + 1)],
+                        out=bands[:, lo : lo + COLS],
                         in_=banks[2 * u + e][:],
                         func=ACTF.Identity,
                         accum_out=sums_pe[:, u, 2 * n + e : 2 * n + e + 1],
                     )
-            return bd
 
         def guess_mm(g):
             pz = psum.tile([P, 2], F32, name="pz", tag="acc")
             nc.tensor.matmul(out=pz[:], lhsT=gsum, rhs=sums[g][:, :, 0], start=True, stop=True)
             return pz
 
-        def guess_out(g, pz):
-            nc.vector.tensor_scalar_mul(out=negc[g][:], in0=pz[:], scalar1=-1.0 / (8 * COLS))
+        def guess_out(g, pz, n):
+            nc.vector.tensor_scalar_mul(out=negc[g][:], in0=pz[:], scalar1=-1.0 / (8 * COLS * n))
 
-        def squares(g, c, bd):
-            for u in range(2):
-                junk = work.tile([P, 1024], BF16, name="junk", tag="junk", bufs=1)
-                nc.scalar.activation(
-                    out=junk[:],
-                    in_=bd[:, u, :],
-                    func=ACTF.Square,
-                    bias=negc[g][:, u : u + 1],
-                    scale=1.0,
-                    accum_out=sqs[g][:, u, c : c + 1],
-                )
+        def square(g, slot, n, col, u):
+            nc.scalar.activation(
+                out=junk[:, 0 : 2 * COLS * n].rearrange("p (n x) -> p n x", n=n),
+                in_=band(slot, n, u),
+                func=ACTF.Square,
+                bias=negc[g][:, u : u + 1],
+                scale=1.0,
+                accum_out=sqs[g][:, u, col : col + 1],
+            )
+
+        def squares(g, slot, n, col):
+            for u in (1, 0):
+                square(g, slot, n, col, u)
 
         def sm(name, g, shape):
             t = keep.tile(shape, F32, name="%s%d" % (name, g))
@@ -275,46 +269,44 @@ def tile_hwdconv_t_kernel(tc, x, gn_scale, gn_bias, w_proj, out):
                 out=shift[g][:], in0=gbf[:, 2 * g : 2 * g + 2, :], in1=mg[:], op=ALU.subtract
             )
 
-        def affine(g, bd, on_scalar):
-            yp = work.tile([P, 4, COLS], BF16, name="yp", tag="yp", align_bytes=64)
+        def affine_scalar(g, slot, half):
             for u in range(2):
                 for e in range(2):
-                    src = bd[:, u, COLS * e : COLS * (e + 1)]
-                    if on_scalar:
-                        nc.scalar.activation(
-                            out=yp[:, 2 * u + e, :],
-                            in_=src,
-                            func=ACTF.Identity,
-                            bias=shift[g][:, u, e : e + 1],
-                            scale=gain[g][:, u, e : e + 1],
-                        )
-                    else:
-                        nc.vector.tensor_scalar(
-                            out=yp[:, 2 * u + e, :],
-                            in0=src,
-                            scalar1=gain[g][:, u, e : e + 1],
-                            scalar2=shift[g][:, u, e : e + 1],
-                            op0=ALU.mult,
-                            op1=ALU.add,
-                        )
-            return yp
+                    lo = SLOT * slot + 2 * COLS * u + COLS * e
+                    nc.scalar.activation(
+                        out=yp[:, half, 2 * u + e, :],
+                        in_=bands[:, lo : lo + COLS],
+                        func=ACTF.Identity,
+                        bias=shift[g][:, u, e : e + 1],
+                        scale=gain[g][:, u, e : e + 1],
+                    )
 
-        def regroup(yp, ca):
-            gr = work.tile([P, COLS, 4], BF16, name="gr", tag="gr", align_bytes=64)
+        def affine_vector(g, slot):
+            for u in range(2):
+                for e in range(2):
+                    nc.vector.tensor_scalar(
+                        out=yp[:, :, 2 * u + e, :],
+                        in0=band(slot, 2, u)[:, :, COLS * e : COLS * (e + 1)],
+                        scalar1=gain[g][:, u, e : e + 1],
+                        scalar2=shift[g][:, u, e : e + 1],
+                        op0=ALU.mult,
+                        op1=ALU.add,
+                    )
+
+        def regroup(half, ca):
             if ca > 0:
                 nc.scalar.copy(
-                    out=gr[:, 0:ca, :].rearrange("p (c i) t -> p c t i", i=4),
-                    in_=yp[:, :, 0:ca].rearrange("p t (c i) -> p c t i", i=4),
+                    out=gr[:, half, 0:ca, :].rearrange("p (c i) t -> p c t i", i=4),
+                    in_=yp[:, half, :, 0:ca].rearrange("p t (c i) -> p c t i", i=4),
                 )
             nc.vector.tensor_copy(
-                out=gr[:, ca:COLS, :].rearrange("p (c i) t -> p c t i", i=4),
-                in_=yp[:, :, ca:COLS].rearrange("p t (c i) -> p c t i", i=4),
+                out=gr[:, half, ca:COLS, :].rearrange("p (c i) t -> p c t i", i=4),
+                in_=yp[:, half, :, ca:COLS].rearrange("p t (c i) -> p c t i", i=4),
             )
-            return gr
 
-        def quantise(gr, codes, scales):
+        def quantise(half, codes, scales):
             nc.vector.quantize_mx(
-                out=codes.bitcast(FP8X4), scales=scales, in_=gr[:].rearrange("p c t -> p (c t)")
+                out=codes.bitcast(FP8X4), scales=scales, in_=gr[:, half, :, :].rearrange("p c t -> p (c t)")
             )
 
         def multiply(c, c1, s1):
@@ -345,9 +337,7 @@ def tile_hwdconv_t_kernel(tc, x, gn_scale, gn_bias, w_proj, out):
 
         def relu_store(c, accs, last):
             cols = slice(COLS * c, COLS * (c + 1))
-            ost = work.tile(
-                [P, 4, COLS], F32, name="ost", tag=("sa" if c % 3 == 2 else "xa"), bufs=(1 if c % 3 == 2 else 2)
-            )
+            ost = work.tile([P, 4, COLS], F32, name="ost", tag="xa", align_bytes=64)
             for a in range(4):
                 if last and a % 2 == 1:
                     nc.vector.tensor_scalar_max(out=ost[:, a, :], in0=accs[a][:], scalar1=0.0)
@@ -358,91 +348,96 @@ def tile_hwdconv_t_kernel(tc, x, gn_scale, gn_bias, w_proj, out):
             if not last:
                 nc.sync.dma_start(out=ov[:, :, cols], in_=ost[:])
 
-        raws = None
-        bd0 = []
-        ids0 = []
-        pz = None
-        grouped = None
+        yp_flat = yp[:].rearrange("p h t x -> p (h t x)")
+        gr_flat = gr[:].rearrange("p h c t -> p (h c t)")
         pending = []
-        prev = None
-        for c in range(NV):
-            if c == 0:
-                st = first_chunk()
-            else:
-                xt = load_x(c)
-                st = haar_h(0, xt)
-            if c == 1:
-                raws = load_w()
-                guess_out(0, pz)
-            if c == 2:
-                load_gn()
-            if c == 5:
-                quantise_w(grouped)
+        pz = None
+        for k, unit in enumerate(UNITS):
+            n = len(unit)
+            for c in unit:
+                xt = load_x(c, halves=(c == 0))
+                haar_h(0, xt, c, halves=(c == 0))
+                if c == 1:
+                    load_w()
+                    guess_out(0, pz, 1)
+                if c == 2:
+                    load_gn()
+            if k == 3:
+                quantise_w()
                 nc.vector.tensor_copy(out=gsf[:], in_=gsb[:])
                 nc.vector.tensor_copy(out=gbf[:], in_=gbb[:])
-            if c >= 1:
-                squares(0, c - 1, prev)
-            prev = haar_v(0, c, st)
-            bd0.append(prev)
-            ids0.append(c)
-            if c == 0:
+            if k >= 1:
+                squares(0, UNITS[k - 1][0], len(UNITS[k - 1]), k - 1)
+            haar_v(0, unit[0], n, k, 1)
+            haar_v(0, unit[0], n, k, 0)
+            if k == 0:
                 pz = guess_mm(0)
-            if c == 2:
-                grouped = transpose_w(raws)
-            if c in (6, 8, 10):
-                n = (c - 6) // 2
-                bd0.append(evacuate_pe(n, pending[n]))
-                ids0.append(PE_CHUNKS[n])
-                squares(0, PE_CHUNKS[n], bd0[len(bd0) - 1])
-            if c in (3, 5, 7):
-                pending.append(bands_pe(PE_CHUNKS[(c - 3) // 2], "gr" if c == 5 else "yp"))
-        squares(0, NV - 1, prev)
+            if k == 1:
+                transpose_w()
+            if k in (3, 4, 5):
+                evacuate_pe(k - 3, pending[k - 3])
+                squares(0, PE_CHUNKS[k - 3], 1, len(UNITS) + k - 3)
+            if k in (2, 3, 4):
+                pending.append(bands_pe(PE_CHUNKS[k - 2], gr_flat if k == 3 else yp_flat))
+        squares(0, UNITS[-1][0], len(UNITS[-1]), len(UNITS) - 1)
 
-        bd1 = []
-        xt = load_x(0)
-        st = haar_h(1, xt)
-        bd1.append(haar_v(1, 0, st))
-        pz = guess_mm(1)
-        pg = fin_a(0)
-        xt = load_x(1)
-        st = haar_h(1, xt)
-        guess_out(1, pz)
+        def slot2(c):
+            return (c - 2) % SLOTS
+
+        for c in range(2):
+            xt = load_x(c)
+            haar_h(1, xt, slot2(c))
+            if c == 0:
+                pg = fin_a(0)
         fin_b(0, pg)
-        bd1.append(haar_v(1, 1, st))
+        haar_v(1, slot2(0), 2, 0, 1)
         fin_c(0)
-        yps = [affine(0, bd0[0], True)]
-        squares(1, 0, bd1[0])
-        for c in range(NCH):
-            if c + 2 < NCH:
-                xt = load_x(c + 2)
-                st = haar_h(1, xt)
-            if c == NCH - 2:
-                squares(1, NCH - 1, bd1[NCH - 1])
-                yps.append(affine(0, bd0[NCH - 1], False))
-            gr = regroup(yps[c], CA2 if c < NCH - 2 else 0)
-            if c + 1 < NCH - 1:
-                yps.append(affine(0, bd0[c + 1], True))
-            if c + 2 < NCH:
-                bd1.append(haar_v(1, c + 2, st))
-            if c == NCH - 1:
-                fin_b(1, pg)
-            quantise(gr, code0(ids0[c]), scale0(ids0[c]))
-            if c + 1 < NCH - 1:
-                squares(1, c + 1, bd1[c + 1])
-            if c == NCH - 2:
+        affine_scalar(0, 0, 0)
+        haar_v(1, slot2(0), 2, 0, 0)
+        pz = guess_mm(1)
+        affine_scalar(0, 1, 1)
+        for k in range(PAIRS):
+            a, b = 2 * k, 2 * k + 1
+            more = k + 1 < PAIRS
+            ca = CA2 if more else 0
+            if more:
+                xt = load_x(a + 2)
+                haar_h(1, xt, slot2(a + 2))
+            if k == 0:
+                guess_out(1, pz, 2)
+            regroup(0, ca)
+            if more:
+                xt = load_x(b + 2)
+                haar_h(1, xt, slot2(b + 2))
+            regroup(1, ca)
+            square(1, slot2(a), 2, k, 1)
+            if more:
+                affine_scalar(0, a + 2, 0)
+                haar_v(1, slot2(a + 2), 2, k + 1, 1)
+            square(1, slot2(a), 2, k, 0)
+            quantise(0, code0(a), scale0(a))
+            if more:
+                affine_scalar(0, b + 2, 1)
+                haar_v(1, slot2(a + 2), 2, k + 1, 0)
+            else:
                 pg = fin_a(1)
+            quantise(1, code0(b), scale0(b))
+        fin_b(1, pg)
         fin_c(1)
 
-        yps = [affine(1, bd1[0], False)]
+        affine_vector(1, slot2(0))
         accs = None
-        for c in range(NCH):
-            gr = regroup(yps[c], CA3)
-            if c >= 1:
-                relu_store(c - 1, accs, False)
-            if c + 1 < NCH:
-                yps.append(affine(1, bd1[c + 1], False))
-            c1 = work.tile([P, COLS], U32, name="c1", tag="c1", align_bytes=64)
-            s1 = work.tile([P, COLS], U8, name="s1", tag="s1", align_bytes=64)
-            quantise(gr, c1[:], s1[:])
-            accs = multiply(c, c1, s1)
+        for k in range(PAIRS):
+            for half in range(2):
+                regroup(half, CA3)
+            for half in range(2):
+                c = 2 * k + half
+                if c >= 1:
+                    relu_store(c - 1, accs, False)
+                if half == 1 and k + 1 < PAIRS:
+                    affine_vector(1, slot2(c + 1))
+                c1 = work.tile([P, COLS], U32, name="c1", tag="c1", bufs=2, align_bytes=64)
+                s1 = work.tile([P, COLS], U8, name="s1", tag="s1", bufs=2, align_bytes=64)
+                quantise(half, c1[:], s1[:])
+                accs = multiply(c, c1, s1)
         relu_store(NCH - 1, accs, True)

@@ -20,11 +20,11 @@ NCH = 16
 COLS = 512
 SLOTS = 18
 SLOT = 4 * COLS
-UNITS = ((0,), (1, 2), (3, 4), (5, 6), (7, 8), (9, 10), (11, 12))
-PE_CHUNKS = (13, 14, 15)
+UNITS = ((0,), (1, 2), (3, 4), (5, 6), (7, 8), (9,))
+FIRST_PE = 10
+GROUPS = 3
 PAIRS = NCH // 2
-CA2 = 192
-CA3 = 64
+CA2 = 256
 EPS = 1e-5
 FLOPS = 2 * CO * K * NPIX
 
@@ -34,10 +34,12 @@ def tile_hwdconv_t_kernel(tc, x, gn_scale, gn_bias, w_proj, out):
     xv = x.rearrange("(p e) h w -> p e (h w)", e=2)
     ov = out.rearrange("(a p) h w -> p a (h w)", p=P)
     wv = w_proj.rearrange("(a p) k -> p a k", p=P)
+    xb = x.rearrange("(q t) (i r) w -> t r q i w", t=4, r=2)
 
     with ExitStack() as ctx:
         keep = ctx.enter_context(tc.tile_pool(name="keep", bufs=1))
         work = ctx.enter_context(tc.tile_pool(name="work", bufs=3))
+        turns = ctx.enter_context(tc.tile_pool(name="turns", bufs=1))
         psum = ctx.enter_context(tc.psum_pool(name="psum", bufs=8))
         ctx.enter_context(tc.manual_schedule())
 
@@ -50,43 +52,68 @@ def tile_hwdconv_t_kernel(tc, x, gn_scale, gn_bias, w_proj, out):
         gbb = keep.tile([P, 4, 2], BF16, name="gbb")
         gsf = keep.tile([P, 4, 2], F32, name="gsf")
         gbf = keep.tile([P, 4, 2], F32, name="gbf")
+        gsb4 = keep.tile([P, 4], BF16, name="gsb4")
+        gbb4 = keep.tile([P, 4], BF16, name="gbb4")
+        gsf4 = keep.tile([P, 4], F32, name="gsf4")
+        gbf4 = keep.tile([P, 4], F32, name="gbf4")
 
         ident = keep.tile([P, P], F32, name="ident")
         make_identity(nc, ident[:])
         nsum = (len(UNITS), PAIRS)
-        nsq = (len(UNITS) + len(PE_CHUNKS), PAIRS)
         sums = [keep.tile([P, 2, nsum[g]], F32, name="sums%d" % g) for g in range(2)]
         rsum = keep.tile([P, 32], F32, name="rsum")
         nc.vector.tensor_reduce(
             out=rsum[:], in_=ident[:].rearrange("p (q j) -> p q j", j=4), axis=AX.X, op=ALU.add
         )
-        gmat = keep.tile([P, 32, 4], F32, name="gmat")
-        nc.vector.tensor_copy(out=gmat[:], in_=rsum[:].unsqueeze(2).to_broadcast([P, 32, 4]))
-        gsum = gmat[:].rearrange("p q j -> p (q j)")
-        identb = keep.tile([P, P], BF16, name="identb")
-        nc.vector.tensor_copy(out=identb[:], in_=ident[:])
-        nidentb = keep.tile([P, P], BF16, name="nidentb")
-        nc.vector.tensor_scalar_mul(out=nidentb[:], in0=ident[:], scalar1=-1.0)
+        lo, hi = ident[:, 0:64], ident[:, 64:128]
+        haar = keep.tile([P, P], BF16, name="haar")
+        nc.vector.tensor_tensor(out=haar[:, 0:64], in0=hi, in1=lo, op=ALU.add)
+        nc.vector.tensor_tensor(out=haar[:, 64:128], in0=hi, in1=lo, op=ALU.subtract)
+        same = keep.tile([P, 64], F32, name="same")
+        nc.vector.tensor_tensor(out=same[:], in0=hi, in1=lo, op=ALU.add)
+        rsum4 = keep.tile([P, 32], F32, name="rsum4")
+        nc.vector.tensor_reduce(
+            out=rsum4[:], in_=same[:].rearrange("p (q j) -> p q j", j=2), axis=AX.X, op=ALU.add
+        )
+        own = keep.tile([P, 2], F32, name="own")
+        nc.vector.tensor_reduce(
+            out=own[:], in_=ident[:].rearrange("p (u q) -> p u q", u=2), axis=AX.X, op=ALU.add
+        )
+        gmats = {}
+        for name, src in (("2", rsum), ("4", rsum4)):
+            to2 = keep.tile([P, 32, 4], F32, name="g%sto2" % name)
+            nc.vector.tensor_copy(out=to2[:], in_=src[:].unsqueeze(2).to_broadcast([P, 32, 4]))
+            gmats[name + "2"] = to2[:].rearrange("p q j -> p (q j)")
+            to4 = keep.tile([P, 2, 32, 2], F32, name="g%sto4" % name)
+            for u in range(2):
+                nc.vector.tensor_copy(out=to4[:, u, :, :], in_=src[:].unsqueeze(2).to_broadcast([P, 32, 2]))
+            gmats[name + "4"] = to4[:].rearrange("p u q j -> p (u q j)")
 
-        wc = keep.tile([P, 2, CO], U32, name="wc", align_bytes=64)
-        ws = keep.tile([P, 2, CO], U8, name="ws", align_bytes=64)
-        codes0 = keep.tile([P, NPIX], U32, name="codes0", align_bytes=64)
+        wc = keep.tile([P, 3, CO], U32, name="wc", align_bytes=64)
+        ws = keep.tile([P, 3, CO], U8, name="ws", align_bytes=64)
+        early_x = turns.tile([P, 2, 8192], BF16, name="early_x", tag="codes0", align_bytes=64)
         scales0 = keep.tile([P, 4 * COLS], U8, name="scales0", align_bytes=64)
 
         bands = keep.tile([P, SLOTS * SLOT], F32, name="bands", align_bytes=64)
         yp = keep.tile([P, 2, 4, COLS], BF16, name="yp", align_bytes=64)
         gr = keep.tile([P, 2, COLS, 4], BF16, name="gr", align_bytes=64)
-        junk = keep.tile([P, 2048], BF16, name="junk")
+        junk = turns.tile([P, 2048], BF16, name="junk", tag="c1", align_bytes=64)
 
-        sqs = [keep.tile([P, 2, nsq[g]], F32, name="sqs%d" % g) for g in range(2)]
-        negc = [keep.tile([P, 2], F32, name="negc%d" % g) for g in range(2)]
+        sqs = [keep.tile([P, 2, nsum[g]], F32, name="sqs%d" % g) for g in range(2)]
+        layouts = (2, 1)
+        negc = [keep.tile([P, layouts[g], 2], F32, name="negc%d" % g) for g in range(2)]
+        negc4 = keep.tile([P, 1], F32, name="negc4")
+        gain4 = keep.tile([P, 4], F32, name="gain4")
+        shift4 = keep.tile([P, 4], F32, name="shift4")
+        stat4 = keep.tile([P, 2, 8 * GROUPS], F32, name="stat4")
+        nc.vector.memset(stat4[:], 0.0)
         gain = [keep.tile([P, 2, 2], F32, name="gain%d" % g) for g in range(2)]
         shift = [keep.tile([P, 2, 2], F32, name="shift%d" % g) for g in range(2)]
-        sums_pe = keep.tile([P, 2, 2 * len(PE_CHUNKS)], F32, name="sums_pe")
         small = {}
+        late = {}
 
         def code0(c):
-            return codes0[:, COLS * c : COLS * (c + 1)]
+            return late["codes0"][:, COLS * c : COLS * (c + 1)]
 
         def scale0(c):
             return scales0[4 * (c // 4) : P, COLS * (c % 4) : COLS * (c % 4 + 1)]
@@ -105,29 +132,38 @@ def tile_hwdconv_t_kernel(tc, x, gn_scale, gn_bias, w_proj, out):
             with nc.allow_non_contiguous_dma(reason="two small vectors, four bytes a piece"):
                 nc.sync.dma_start(out=gsb[:], in_=gn_scale.rearrange("(b p e) -> p b e", b=4, e=2))
                 nc.sync.dma_start(out=gbb[:], in_=gn_bias.rearrange("(b p e) -> p b e", b=4, e=2))
+                nc.sync.dma_start(out=gsb4[:], in_=gn_scale[0:512].rearrange("(p t) -> p t", t=4))
+                nc.sync.dma_start(out=gbb4[:], in_=gn_bias[0:512].rearrange("(p t) -> p t", t=4))
 
-        def transpose_w():
-            for g in range(2):
-                wgv = gr[:, g, :, :].rearrange("p c t -> p (c t)").bitcast(F32).rearrange("p (o u) -> p o u", u=2)
-                for h in range(2):
-                    pt = psum.tile([P, 2, 2, P], F32, name="pt", tag="acc")
-                    src = yp[:, h, :, :].rearrange("p t x -> p (t x)").bitcast(F32)
-                    for a in range(2):
-                        for u in range(2):
-                            lo = 512 * a + 256 * g + 128 * u
-                            nc.tensor.transpose(pt[:, a, u, :], src[:, lo : lo + P], ident[:])
-                    nc.scalar.copy(
-                        out=wgv[:, 256 * h : 256 * h + 256, :].rearrange("p (a o) u -> p a o u", a=2),
-                        in_=pt[:].rearrange("p a u o -> p a o u"),
-                    )
+        def grouped_w(plane):
+            if plane < 2:
+                return gr[:, plane, :, :].rearrange("p c t -> p (c t)")
+            return bands[:, SLOT * (NCH - 1) : SLOT * (NCH - 1) + SLOT // 2].bitcast(BF16)
 
-        def quantise_w():
-            for g in range(2):
-                nc.vector.quantize_mx(
-                    out=wc[:, g, :].bitcast(FP8X4),
-                    scales=ws[:, g, :],
-                    in_=gr[:, g, :, :].rearrange("p c t -> p (c t)"),
+        def transpose_w(plane):
+            wgv = grouped_w(plane).bitcast(F32).rearrange("p (o u) -> p o u", u=2)
+            for h in range(2):
+                pt = psum.tile([P, 2, 2, P], F32, name="pt", tag="acc")
+                src = yp[:, h, :, :].rearrange("p t x -> p (t x)").bitcast(F32)
+                for a in range(2):
+                    for u in range(2):
+                        if plane == 2:
+                            words = src[:, 512 * a + u : 512 * a + 256 : 2]
+                        else:
+                            at = 512 * a + 256 * plane + 128 * u
+                            words = src[:, at : at + P]
+                        nc.tensor.transpose(pt[:, a, u, :], words, ident[:])
+                nc.scalar.copy(
+                    out=wgv[:, 256 * h : 256 * h + 256, :].rearrange("p (a o) u -> p a o u", a=2),
+                    in_=pt[:].rearrange("p a u o -> p a o u"),
                 )
+
+        def quantise_w(plane):
+            nc.vector.quantize_mx(
+                out=wc[:, plane, :].bitcast(FP8X4),
+                scales=ws[:, plane, :],
+                in_=grouped_w(plane),
+            )
 
         def load_x(c, halves=False):
             xt = work.tile([P, 2, 2048], BF16, name="xt", tag="xa", align_bytes=64)
@@ -161,53 +197,88 @@ def tile_hwdconv_t_kernel(tc, x, gn_scale, gn_bias, w_proj, out):
                 accum_out=sums[g][:, u, col : col + 1],
             )
 
-        def bands_pe(c, store):
+        def group_x(n):
+            if n < 2:
+                raw = early_x[:, n, :]
+            else:
+                raw = bands[:, SLOT * NCH : SLOT * (NCH + 2)].bitcast(BF16)
+            return raw.rearrange("p (t i w) -> p t i w", t=4, i=8)
+
+        def load_group(n, t):
+            i0 = 4 * (FIRST_PE + 2 * n)
+            for r in range(2):
+                nc.sync.dma_start(out=group_x(n)[64 * r : 64 * r + 64, t, :, :], in_=xb[t, r, :, i0 : i0 + 8, :])
+
+        def bands_pe(n, t):
+            view = group_x(n).rearrange("p t i (j two) -> p t i j two", two=2)
             banks = []
-            views = []
-            for e in range(2):
-                xe = store[:, 2048 * e : 2048 * (e + 1)]
-                nc.gpsimd.dma_start(out=xe, in_=xv[:, e, 2048 * c : 2048 * (c + 1)])
-                views.append(xe.rearrange("p (i r j two) -> p i r j two", i=4, r=2, two=2))
-            for u in range(2):
-                for e in range(2):
-                    ps = psum.tile([P, COLS], F32, name="ps", tag="acc")
-                    for n in range(4):
-                        r = n // 2
-                        nc.tensor.matmul(
-                            out=ps[:].rearrange("p (i j) -> p i j", i=4),
-                            lhsT=(nidentb[:] if (u == 1 and r == 0) else identb[:]),
-                            rhs=views[e][:, :, r, :, n % 2],
-                            start=(n == 0),
-                            stop=(n == 3),
-                        )
-                    banks.append(ps)
+            for h in range(2):
+                ps = psum.tile([P, COLS], F32, name="ps", tag="acc")
+                for m in range(2):
+                    nc.tensor.matmul(
+                        out=ps[:].rearrange("p (i j) -> p i j", i=4),
+                        lhsT=haar[:],
+                        rhs=view[:, t, 4 * h : 4 * h + 4, :, m],
+                        start=(m == 0),
+                        stop=(m == 1),
+                    )
+                banks.append(ps)
             return banks
 
-        def evacuate_pe(n, banks):
-            for u in range(2):
-                for e in range(2):
-                    lo = SLOT * PE_CHUNKS[n] + 2 * COLS * u + COLS * e
+        def evacuate_pe(n, t, banks, on_scalar):
+            for h in range(2):
+                at = SLOT * (FIRST_PE + 2 * n + h) + COLS * t
+                col = 8 * n + 4 * h + t
+                acc = stat4[:, 0, col : col + 1]
+                if on_scalar:
                     nc.scalar.activation(
-                        out=bands[:, lo : lo + COLS],
-                        in_=banks[2 * u + e][:],
-                        func=ACTF.Identity,
-                        accum_out=sums_pe[:, u, 2 * n + e : 2 * n + e + 1],
+                        out=bands[:, at : at + COLS], in_=banks[h][:], func=ACTF.Identity, accum_out=acc
+                    )
+                else:
+                    nc.vector.tensor_scalar(
+                        out=bands[:, at : at + COLS],
+                        in0=banks[h][:],
+                        scalar1=1.0,
+                        scalar2=0.0,
+                        op0=ALU.mult,
+                        op1=ALU.add,
+                        accum_out=acc,
                     )
 
+        def squares_pe(n):
+            for h in range(2):
+                slot = FIRST_PE + 2 * n + h
+                col = 2 * n + h
+                nc.scalar.activation(
+                    out=junk[:],
+                    in_=bands[:, SLOT * slot : SLOT * (slot + 1)],
+                    func=ACTF.Square,
+                    bias=negc4[:],
+                    scale=1.0,
+                    accum_out=stat4[:, 1, col : col + 1],
+                )
+
         def guess_mm(g):
-            pz = psum.tile([P, 2], F32, name="pz", tag="acc")
-            nc.tensor.matmul(out=pz[:], lhsT=gsum, rhs=sums[g][:, :, 0], start=True, stop=True)
+            pz = psum.tile([P, layouts[g], 2], F32, name="pz", tag="acc")
+            for l in range(layouts[g]):
+                nc.tensor.matmul(
+                    out=pz[:, l, :], lhsT=gmats[("22", "24")[l]], rhs=sums[g][:, :, 0], start=True, stop=True
+                )
             return pz
 
         def guess_out(g, pz, n):
             nc.vector.tensor_scalar_mul(out=negc[g][:], in0=pz[:], scalar1=-1.0 / (8 * COLS * n))
+            if g == 0:
+                for u in range(2):
+                    q = slice(64 * u, 64 * u + 64)
+                    nc.vector.tensor_copy(out=negc4[q, :], in_=negc[0][q, 1, u : u + 1])
 
         def square(g, slot, n, col, u):
             nc.scalar.activation(
                 out=junk[:, 0 : 2 * COLS * n].rearrange("p (n x) -> p n x", n=n),
                 in_=band(slot, n, u),
                 func=ACTF.Square,
-                bias=negc[g][:, u : u + 1],
+                bias=negc[g][:, 0, u : u + 1],
                 scale=1.0,
                 accum_out=sqs[g][:, u, col : col + 1],
             )
@@ -222,76 +293,118 @@ def tile_hwdconv_t_kernel(tc, x, gn_scale, gn_bias, w_proj, out):
             return t
 
         def fin_a(g):
-            tot = sm("tot", g, [P, 4])
-            nc.vector.tensor_reduce(out=tot[:, 0:2], in_=sums[g][:], axis=AX.X, op=ALU.add)
-            nc.vector.tensor_reduce(out=tot[:, 2:4], in_=sqs[g][:], axis=AX.X, op=ALU.add)
+            tot = sm("tot", g, [P, 2, 2])
+            nc.vector.tensor_reduce(out=tot[:, 0, :], in_=sums[g][:], axis=AX.X, op=ALU.add)
+            nc.vector.tensor_reduce(out=tot[:, 1, :], in_=sqs[g][:], axis=AX.X, op=ALU.add)
+            flat = tot[:].rearrange("p s u -> p (s u)")
+            flat4 = None
             if g == 0:
-                tpe = sm("tpe", g, [P, 2])
-                nc.vector.tensor_reduce(out=tpe[:], in_=sums_pe[:], axis=AX.X, op=ALU.add)
-                nc.vector.tensor_tensor(out=tot[:, 0:2], in0=tot[:, 0:2], in1=tpe[:], op=ALU.add)
-            pg = psum.tile([P, 4], F32, name="pg", tag="acc")
-            nc.tensor.matmul(out=pg[:], lhsT=gsum, rhs=tot[:], start=True, stop=True)
+                tot4 = sm("tot4", g, [P, 2])
+                nc.vector.tensor_reduce(out=tot4[:], in_=stat4[:], axis=AX.X, op=ALU.add)
+                spread = sm("spread", g, [P, 2, 2])
+                nc.vector.tensor_tensor(
+                    out=spread[:],
+                    in0=tot4[:].unsqueeze(2).to_broadcast([P, 2, 2]),
+                    in1=own[:].unsqueeze(1).to_broadcast([P, 2, 2]),
+                    op=ALU.mult,
+                )
+                flat4 = spread[:].rearrange("p s u -> p (s u)")
+            pg = psum.tile([P, layouts[g], 4], F32, name="pg", tag="acc")
+            for l in range(layouts[g]):
+                nc.tensor.matmul(
+                    out=pg[:, l, :], lhsT=gmats[("22", "24")[l]], rhs=flat, start=True, stop=(g == 1)
+                )
+                if g == 0:
+                    nc.tensor.matmul(
+                        out=pg[:, l, :], lhsT=gmats[("42", "44")[l]], rhs=flat4, start=False, stop=True
+                    )
             return pg
 
         def fin_b(g, pg):
-            mv = sm("mv", g, [P, 4])
+            n = layouts[g]
+            mv = sm("mv", g, [P, n, 4])
             nc.vector.tensor_scalar_mul(out=mv[:], in0=pg[:], scalar1=1.0 / (8 * NPIX))
-            dl = sm("dl", g, [P, 2])
-            nc.vector.tensor_tensor(out=dl[:], in0=mv[:, 0:2], in1=negc[g][:], op=ALU.add)
-            d2 = sm("d2", g, [P, 2])
+            dl = sm("dl", g, [P, n, 2])
+            nc.vector.tensor_tensor(out=dl[:], in0=mv[:, :, 0:2], in1=negc[g][:], op=ALU.add)
+            d2 = sm("d2", g, [P, n, 2])
             nc.vector.tensor_tensor(out=d2[:], in0=dl[:], in1=dl[:], op=ALU.mult)
-            var = sm("var", g, [P, 2])
-            nc.vector.tensor_tensor(out=var[:], in0=mv[:, 2:4], in1=d2[:], op=ALU.subtract)
-            ve = sm("ve", g, [P, 2])
+            var = sm("var", g, [P, n, 2])
+            nc.vector.tensor_tensor(out=var[:], in0=mv[:, :, 2:4], in1=d2[:], op=ALU.subtract)
+            ve = sm("ve", g, [P, n, 2])
             nc.vector.tensor_scalar(
                 out=ve[:], in0=var[:], scalar1=0.0, scalar2=4.0 * EPS, op0=ALU.max, op1=ALU.add
             )
-            sd = sm("sd", g, [P, 2])
+            sd = sm("sd", g, [P, n, 2])
             nc.scalar.activation(out=sd[:], in_=ve[:], func=ACTF.Sqrt)
 
         def fin_c(g):
-            rs = sm("rs", g, [P, 2])
+            n = layouts[g]
+            rs = sm("rs", g, [P, n, 2])
             nc.vector.reciprocal(out=rs[:], in_=small[("sd", g)][:])
+            mv = small[("mv", g)]
             nc.vector.tensor_tensor(
                 out=gain[g][:],
                 in0=gsf[:, 2 * g : 2 * g + 2, :],
-                in1=rs[:].unsqueeze(2).to_broadcast([P, 2, 2]),
+                in1=rs[:, 0, :].unsqueeze(2).to_broadcast([P, 2, 2]),
                 op=ALU.mult,
             )
             mg = sm("mg", g, [P, 2, 2])
             nc.vector.tensor_tensor(
                 out=mg[:],
                 in0=gain[g][:],
-                in1=small[("mv", g)][:, 0:2].unsqueeze(2).to_broadcast([P, 2, 2]),
+                in1=mv[:, 0, 0:2].unsqueeze(2).to_broadcast([P, 2, 2]),
                 op=ALU.mult,
             )
             nc.vector.tensor_tensor(
                 out=shift[g][:], in0=gbf[:, 2 * g : 2 * g + 2, :], in1=mg[:], op=ALU.subtract
             )
 
+        def fin_c4():
+            rs, mv = small[("rs", 0)], small[("mv", 0)]
+            mg = sm("mg4", 0, [P, 4])
+            for u in range(2):
+                q = slice(64 * u, 64 * u + 64)
+                nc.vector.tensor_scalar_mul(out=gain4[q, :], in0=gsf4[q, :], scalar1=rs[q, 1, u : u + 1])
+                nc.vector.tensor_scalar_mul(out=mg[q, :], in0=gain4[q, :], scalar1=mv[q, 1, u : u + 1])
+            nc.vector.tensor_tensor(out=shift4[:], in0=gbf4[:], in1=mg[:], op=ALU.subtract)
+
         def affine_scalar(g, slot, half):
             for u in range(2):
                 for e in range(2):
                     lo = SLOT * slot + 2 * COLS * u + COLS * e
+                    t = 2 * u + e
+                    if g == 0 and slot >= FIRST_PE:
+                        bias, scale = shift4[:, t : t + 1], gain4[:, t : t + 1]
+                    else:
+                        bias, scale = shift[g][:, u, e : e + 1], gain[g][:, u, e : e + 1]
                     nc.scalar.activation(
-                        out=yp[:, half, 2 * u + e, :],
+                        out=yp[:, half, t, :],
                         in_=bands[:, lo : lo + COLS],
                         func=ACTF.Identity,
-                        bias=shift[g][:, u, e : e + 1],
-                        scale=gain[g][:, u, e : e + 1],
+                        bias=bias,
+                        scale=scale,
                     )
 
-        def affine_vector(g, slot):
-            for u in range(2):
-                for e in range(2):
-                    nc.vector.tensor_scalar(
-                        out=yp[:, :, 2 * u + e, :],
-                        in0=band(slot, 2, u)[:, :, COLS * e : COLS * (e + 1)],
-                        scalar1=gain[g][:, u, e : e + 1],
-                        scalar2=shift[g][:, u, e : e + 1],
-                        op0=ALU.mult,
-                        op1=ALU.add,
-                    )
+        def affine_vector(slot):
+            for t in range(3):
+                u, e = t // 2, t % 2
+                nc.vector.tensor_scalar(
+                    out=yp[:, :, t, :],
+                    in0=band(slot, 2, u)[:, :, COLS * e : COLS * (e + 1)],
+                    scalar1=gain[1][:, u, e : e + 1],
+                    scalar2=shift[1][:, u, e : e + 1],
+                    op0=ALU.mult,
+                    op1=ALU.add,
+                )
+
+        def affine_rest(slot):
+            nc.scalar.activation(
+                out=yp[:, :, 3, :],
+                in_=band(slot, 2, 1)[:, :, COLS : 2 * COLS],
+                func=ACTF.Identity,
+                bias=shift[1][:, 1, 1:2],
+                scale=gain[1][:, 1, 1:2],
+            )
 
         def regroup(half, ca):
             if ca > 0:
@@ -309,15 +422,16 @@ def tile_hwdconv_t_kernel(tc, x, gn_scale, gn_bias, w_proj, out):
                 out=codes.bitcast(FP8X4), scales=scales, in_=gr[:, half, :, :].rearrange("p c t -> p (c t)")
             )
 
-        def multiply(c, c1, s1):
+        def multiply(c, half, s1):
             accs = []
+            first = 0 if c < FIRST_PE else 2
             for a in range(4):
                 acc = psum.tile([P, COLS], F32, name="acc", tag="acc")
                 m = slice(P * a, P * (a + 1))
                 nc.tensor.matmul_mx(
                     out=acc[:],
-                    lhsT=wc[:, 0, m].bitcast(FP8X4),
-                    lhsT_scale=ws[:, 0, m],
+                    lhsT=wc[:, first, m].bitcast(FP8X4),
+                    lhsT_scale=ws[:, first, m],
                     rhs=code0(c).bitcast(FP8X4),
                     rhs_scale=scale0(c),
                     start=True,
@@ -327,7 +441,7 @@ def tile_hwdconv_t_kernel(tc, x, gn_scale, gn_bias, w_proj, out):
                     out=acc[:],
                     lhsT=wc[:, 1, m].bitcast(FP8X4),
                     lhsT_scale=ws[:, 1, m],
-                    rhs=c1[:].bitcast(FP8X4),
+                    rhs=late["c1"][:, half, :].bitcast(FP8X4),
                     rhs_scale=s1[:],
                     start=False,
                     stop=True,
@@ -348,37 +462,48 @@ def tile_hwdconv_t_kernel(tc, x, gn_scale, gn_bias, w_proj, out):
             if not last:
                 nc.sync.dma_start(out=ov[:, :, cols], in_=ost[:])
 
-        yp_flat = yp[:].rearrange("p h t x -> p (h t x)")
-        gr_flat = gr[:].rearrange("p h c t -> p (h c t)")
-        pending = []
+        loads = {0: ((0, 0),), 2: ((0, 1),), 3: ((0, 2), (0, 3)), 5: ((1, 0), (1, 1)), 6: ((1, 2), (1, 3)), 7: ((2, 0), (2, 1)), 8: ((2, 2), (2, 3))}
         pz = None
+        banks = {}
         for k, unit in enumerate(UNITS):
             n = len(unit)
             for c in unit:
                 xt = load_x(c, halves=(c == 0))
+                for group, t in loads.get(c, ()):
+                    load_group(group, t)
+                if c == 2:
+                    load_w()
+                    load_gn()
                 haar_h(0, xt, c, halves=(c == 0))
                 if c == 1:
-                    load_w()
                     guess_out(0, pz, 1)
-                if c == 2:
-                    load_gn()
-            if k == 3:
-                quantise_w()
-                nc.vector.tensor_copy(out=gsf[:], in_=gsb[:])
-                nc.vector.tensor_copy(out=gbf[:], in_=gbb[:])
+            if k == 1:
+                evacuate_pe(0, 0, banks[(0, 0)], True)
             if k >= 1:
                 squares(0, UNITS[k - 1][0], len(UNITS[k - 1]), k - 1)
             haar_v(0, unit[0], n, k, 1)
             haar_v(0, unit[0], n, k, 0)
             if k == 0:
                 pz = guess_mm(0)
+                banks[(0, 0)] = bands_pe(0, 0)
             if k == 1:
-                transpose_w()
-            if k in (3, 4, 5):
-                evacuate_pe(k - 3, pending[k - 3])
-                squares(0, PE_CHUNKS[k - 3], 1, len(UNITS) + k - 3)
+                for plane in range(3):
+                    transpose_w(plane)
+                banks[(0, 1)] = bands_pe(0, 1)
+                evacuate_pe(0, 1, banks[(0, 1)], True)
+            if k == 2:
+                for plane in range(3):
+                    quantise_w(plane)
+            if k == 3:
+                for wide, narrow in ((gsf, gsb), (gbf, gbb), (gsf4, gsb4), (gbf4, gbb4)):
+                    nc.vector.tensor_copy(out=wide[:], in_=narrow[:])
+            if k >= 3:
+                squares_pe(k - 3)
             if k in (2, 3, 4):
-                pending.append(bands_pe(PE_CHUNKS[k - 2], gr_flat if k == 3 else yp_flat))
+                group = k - 2
+                for t in range(4):
+                    if (group, t) not in banks:
+                        evacuate_pe(group, t, bands_pe(group, t), on_scalar=(t < (4, 2, 1)[group]))
         squares(0, UNITS[-1][0], len(UNITS[-1]), len(UNITS) - 1)
 
         def slot2(c):
@@ -396,6 +521,9 @@ def tile_hwdconv_t_kernel(tc, x, gn_scale, gn_bias, w_proj, out):
         haar_v(1, slot2(0), 2, 0, 0)
         pz = guess_mm(1)
         affine_scalar(0, 1, 1)
+        fin_c4()
+        late["codes0"] = turns.tile([P, NPIX], U32, name="codes0", tag="codes0", align_bytes=64)
+
         for k in range(PAIRS):
             a, b = 2 * k, 2 * k + 1
             more = k + 1 < PAIRS
@@ -425,19 +553,22 @@ def tile_hwdconv_t_kernel(tc, x, gn_scale, gn_bias, w_proj, out):
         fin_b(1, pg)
         fin_c(1)
 
-        affine_vector(1, slot2(0))
+        late["c1"] = turns.tile([P, 2, COLS], U32, name="c1", tag="c1", align_bytes=64)
+        affine_rest(slot2(0))
+        affine_vector(slot2(0))
         accs = None
         for k in range(PAIRS):
             for half in range(2):
-                regroup(half, CA3)
+                regroup(half, 0)
             for half in range(2):
                 c = 2 * k + half
                 if c >= 1:
                     relu_store(c - 1, accs, False)
                 if half == 1 and k + 1 < PAIRS:
-                    affine_vector(1, slot2(c + 1))
-                c1 = work.tile([P, COLS], U32, name="c1", tag="c1", bufs=2, align_bytes=64)
+                    affine_vector(slot2(c + 1))
+                if half == 0 and k + 1 < PAIRS:
+                    affine_rest(slot2(c + 2))
                 s1 = work.tile([P, COLS], U8, name="s1", tag="s1", bufs=2, align_bytes=64)
-                quantise(half, c1[:], s1[:])
-                accs = multiply(c, c1, s1)
+                quantise(half, late["c1"][:, half, :], s1[:])
+                accs = multiply(c, half, s1)
         relu_store(NCH - 1, accs, True)

@@ -24,7 +24,7 @@ UNITS = ((0,), (1, 2), (3, 4), (5, 6), (7, 8), (9,))
 FIRST_PE = 10
 GROUPS = 3
 PAIRS = NCH // 2
-CA2 = 256
+CA2 = 192
 EPS = 1e-5
 FLOPS = 2 * CO * K * NPIX
 
@@ -65,10 +65,12 @@ def tile_hwdconv_t_kernel(tc, x, gn_scale, gn_bias, w_proj, out):
         nc.vector.tensor_reduce(
             out=rsum[:], in_=ident[:].rearrange("p (q j) -> p q j", j=4), axis=AX.X, op=ALU.add
         )
+        parity = ident[:].rearrange("p (q r) -> p q r", r=2)
+        even, odd = parity[:, :, 0], parity[:, :, 1]
         lo, hi = ident[:, 0:64], ident[:, 64:128]
         haar = keep.tile([P, P], BF16, name="haar")
-        nc.vector.tensor_tensor(out=haar[:, 0:64], in0=hi, in1=lo, op=ALU.add)
-        nc.vector.tensor_tensor(out=haar[:, 64:128], in0=hi, in1=lo, op=ALU.subtract)
+        nc.vector.tensor_tensor(out=haar[:, 0:64], in0=odd, in1=even, op=ALU.add)
+        nc.vector.tensor_tensor(out=haar[:, 64:128], in0=odd, in1=even, op=ALU.subtract)
         same = keep.tile([P, 64], F32, name="same")
         nc.vector.tensor_tensor(out=same[:], in0=hi, in1=lo, op=ALU.add)
         rsum4 = keep.tile([P, 32], F32, name="rsum4")
@@ -207,7 +209,7 @@ def tile_hwdconv_t_kernel(tc, x, gn_scale, gn_bias, w_proj, out):
         def load_group(n, t):
             i0 = 4 * (FIRST_PE + 2 * n)
             for r in range(2):
-                nc.sync.dma_start(out=group_x(n)[64 * r : 64 * r + 64, t, :, :], in_=xb[t, r, :, i0 : i0 + 8, :])
+                nc.sync.dma_start(out=group_x(n)[r:P:2, t, :, :], in_=xb[t, r, :, i0 : i0 + 8, :])
 
         def bands_pe(n, t):
             view = group_x(n).rearrange("p t i (j two) -> p t i j two", two=2)
@@ -451,7 +453,8 @@ def tile_hwdconv_t_kernel(tc, x, gn_scale, gn_bias, w_proj, out):
 
         def relu_store(c, accs, last):
             cols = slice(COLS * c, COLS * (c + 1))
-            ost = work.tile([P, 4, COLS], F32, name="ost", tag="xa", align_bytes=64)
+            slot = NCH - 2 + c if c < 2 else (c - 4) % SLOTS
+            ost = bands[:, SLOT * slot : SLOT * (slot + 1)].rearrange("p (a x) -> p a x", a=4)
             for a in range(4):
                 if last and a % 2 == 1:
                     nc.vector.tensor_scalar_max(out=ost[:, a, :], in0=accs[a][:], scalar1=0.0)
@@ -460,7 +463,7 @@ def tile_hwdconv_t_kernel(tc, x, gn_scale, gn_bias, w_proj, out):
                 if last:
                     nc.sync.dma_start(out=ov[:, a, cols], in_=ost[:, a, :])
             if not last:
-                nc.sync.dma_start(out=ov[:, :, cols], in_=ost[:])
+                nc.sync.dma_start(out=ov[:, :, cols], in_=ost)
 
         loads = {0: ((0, 0),), 2: ((0, 1),), 3: ((0, 2), (0, 3)), 5: ((1, 0), (1, 1)), 6: ((1, 2), (1, 3)), 7: ((2, 0), (2, 1)), 8: ((2, 2), (2, 3))}
         pz = None

@@ -96,7 +96,8 @@ def tile_hwdconv_t_kernel(tc, x, gn_scale, gn_bias, w_proj, out):
         early_x = turns.tile([P, 2, 8192], BF16, name="early_x", tag="codes0", align_bytes=64)
         scales0 = keep.tile([P, 4 * COLS], U8, name="scales0", align_bytes=64)
 
-        bands = keep.tile([P, SLOTS * SLOT], F32, name="bands", align_bytes=64)
+        bands = keep.tile([P, NCH * SLOT], F32, name="bands", align_bytes=64)
+        late_x = turns.tile([P, 8192], BF16, name="late_x", tag="spare", align_bytes=64)
         yp = keep.tile([P, 2, 4, COLS], BF16, name="yp", align_bytes=64)
         gr = keep.tile([P, 2, COLS, 4], BF16, name="gr", align_bytes=64)
         junk = turns.tile([P, 2048], BF16, name="junk", tag="c1", align_bytes=64)
@@ -120,8 +121,13 @@ def tile_hwdconv_t_kernel(tc, x, gn_scale, gn_bias, w_proj, out):
         def scale0(c):
             return scales0[4 * (c // 4) : P, COLS * (c % 4) : COLS * (c % 4 + 1)]
 
+        def span(slot, n):
+            if slot >= NCH:
+                return late["spare"][:, SLOT * (slot - NCH) : SLOT * (slot - NCH + n)]
+            return bands[:, SLOT * slot : SLOT * (slot + n)]
+
         def band(slot, n, u):
-            return bands[:, SLOT * slot : SLOT * (slot + n)].rearrange("p (n u x) -> p n u x", n=n, u=2)[:, :, u, :]
+            return span(slot, n).rearrange("p (n u x) -> p n u x", n=n, u=2)[:, :, u, :]
 
         def load_w():
             for h in range(2):
@@ -140,7 +146,7 @@ def tile_hwdconv_t_kernel(tc, x, gn_scale, gn_bias, w_proj, out):
         def grouped_w(plane):
             if plane < 2:
                 return gr[:, plane, :, :].rearrange("p c t -> p (c t)")
-            return bands[:, SLOT * (NCH - 1) : SLOT * (NCH - 1) + SLOT // 2].bitcast(BF16)
+            return early_x[:, 0, 0:2048]
 
         def transpose_w(plane):
             wgv = grouped_w(plane).bitcast(F32).rearrange("p (o u) -> p o u", u=2)
@@ -178,7 +184,7 @@ def tile_hwdconv_t_kernel(tc, x, gn_scale, gn_bias, w_proj, out):
 
         def haar_h(g, xt, slot, halves=False):
             src = xt[:].rearrange("p e (i r j two) -> p (e i) r j two", r=2, j=P, two=2)
-            dst = bands[:, SLOT * slot : SLOT * (slot + 1)].rearrange("p (r ei j) -> p ei r j", r=2, j=P)
+            dst = span(slot, 1).rearrange("p (r ei j) -> p ei r j", r=2, j=P)
             parts = (slice(0, 4), slice(4, 8)) if halves else (slice(0, 8),)
             for part in parts:
                 nc.vector.tensor_tensor(
@@ -200,15 +206,12 @@ def tile_hwdconv_t_kernel(tc, x, gn_scale, gn_bias, w_proj, out):
             )
 
         def group_x(n):
-            if n < 2:
-                raw = early_x[:, n, :]
-            else:
-                raw = bands[:, SLOT * NCH : SLOT * (NCH + 2)].bitcast(BF16)
+            raw = early_x[:, n, :] if n < 2 else late_x[:]
             return raw.rearrange("p (t i w) -> p t i w", t=4, i=8)
 
-        def load_group(n, t):
+        def load_group(n, r):
             i0 = 4 * (FIRST_PE + 2 * n)
-            for r in range(2):
+            for t in range(4):
                 nc.sync.dma_start(out=group_x(n)[r:P:2, t, :, :], in_=xb[t, r, :, i0 : i0 + 8, :])
 
         def bands_pe(n, t):
@@ -454,7 +457,7 @@ def tile_hwdconv_t_kernel(tc, x, gn_scale, gn_bias, w_proj, out):
         def relu_store(c, accs, last):
             cols = slice(COLS * c, COLS * (c + 1))
             slot = NCH - 2 + c if c < 2 else (c - 4) % SLOTS
-            ost = bands[:, SLOT * slot : SLOT * (slot + 1)].rearrange("p (a x) -> p a x", a=4)
+            ost = span(slot, 1).rearrange("p (a x) -> p a x", a=4)
             for a in range(4):
                 if last and a % 2 == 1:
                     nc.vector.tensor_scalar_max(out=ost[:, a, :], in0=accs[a][:], scalar1=0.0)
@@ -465,53 +468,48 @@ def tile_hwdconv_t_kernel(tc, x, gn_scale, gn_bias, w_proj, out):
             if not last:
                 nc.sync.dma_start(out=ov[:, :, cols], in_=ost)
 
-        loads = {0: ((0, 0),), 2: ((0, 1),), 3: ((0, 2), (0, 3)), 5: ((1, 0), (1, 1)), 6: ((1, 2), (1, 3)), 7: ((2, 0), (2, 1)), 8: ((2, 2), (2, 3))}
+        loads = {1: (0, 0), 2: (0, 1), 4: (1, 0), 5: (1, 1), 7: (2, 0), 8: (2, 1)}
         pz = None
-        banks = {}
         for k, unit in enumerate(UNITS):
             n = len(unit)
             for c in unit:
                 xt = load_x(c, halves=(c == 0))
-                for group, t in loads.get(c, ()):
-                    load_group(group, t)
-                if c == 2:
+                if c in loads:
+                    load_group(*loads[c])
+                if c == 6:
                     load_w()
                     load_gn()
                 haar_h(0, xt, c, halves=(c == 0))
                 if c == 1:
                     guess_out(0, pz, 1)
-            if k == 1:
-                evacuate_pe(0, 0, banks[(0, 0)], True)
             if k >= 1:
                 squares(0, UNITS[k - 1][0], len(UNITS[k - 1]), k - 1)
+            if k in (4, 5):
+                squares_pe(k - 3)
+            if k == 4:
+                for plane in range(3):
+                    quantise_w(plane)
             haar_v(0, unit[0], n, k, 1)
             haar_v(0, unit[0], n, k, 0)
             if k == 0:
                 pz = guess_mm(0)
-                banks[(0, 0)] = bands_pe(0, 0)
+            if k in (1, 3, 4):
+                group = k - 2 if k > 1 else 0
+                for t in range(4):
+                    evacuate_pe(group, t, bands_pe(group, t), on_scalar=(t < (4, 2, 1)[group]))
             if k == 1:
+                squares_pe(0)
+            if k == 3:
                 for plane in range(3):
                     transpose_w(plane)
-                banks[(0, 1)] = bands_pe(0, 1)
-                evacuate_pe(0, 1, banks[(0, 1)], True)
-            if k == 2:
-                for plane in range(3):
-                    quantise_w(plane)
-            if k == 3:
                 for wide, narrow in ((gsf, gsb), (gbf, gbb), (gsf4, gsb4), (gbf4, gbb4)):
-                    nc.vector.tensor_copy(out=wide[:], in_=narrow[:])
-            if k >= 3:
-                squares_pe(k - 3)
-            if k in (2, 3, 4):
-                group = k - 2
-                for t in range(4):
-                    if (group, t) not in banks:
-                        evacuate_pe(group, t, bands_pe(group, t), on_scalar=(t < (4, 2, 1)[group]))
+                    nc.gpsimd.tensor_copy(out=wide[:], in_=narrow[:])
         squares(0, UNITS[-1][0], len(UNITS[-1]), len(UNITS) - 1)
 
         def slot2(c):
             return (c - 2) % SLOTS
 
+        late["spare"] = turns.tile([P, 2 * SLOT], F32, name="spare", tag="spare", align_bytes=64)
         for c in range(2):
             xt = load_x(c)
             haar_h(1, xt, slot2(c))

@@ -20,11 +20,12 @@ NCH = 16
 COLS = 512
 SLOTS = 18
 SLOT = 4 * COLS
-UNITS = ((0,), (1, 2), (3, 4), (5, 6), (7, 8), (9,))
-FIRST_PE = 10
-GROUPS = 3
+UNITS = ((0,), (1,), (2,), (3, 4), (5, 6), (7, 8), (9, 10))
+LONE = 11
+FIRST_PE = 12
+GROUPS = 2
 PAIRS = NCH // 2
-CA2 = 192
+LAST_BY_SCALAR = 12
 EPS = 1e-5
 FLOPS = 2 * CO * K * NPIX
 
@@ -59,7 +60,8 @@ def tile_hwdconv_t_kernel(tc, x, gn_scale, gn_bias, w_proj, out):
 
         ident = keep.tile([P, P], F32, name="ident")
         make_identity(nc, ident[:])
-        nsum = (len(UNITS), PAIRS)
+        nsum = (len(UNITS) + 2, PAIRS)
+        nsq = (len(UNITS) + 1, PAIRS)
         sums = [keep.tile([P, 2, nsum[g]], F32, name="sums%d" % g) for g in range(2)]
         rsum = keep.tile([P, 32], F32, name="rsum")
         nc.vector.tensor_reduce(
@@ -71,6 +73,12 @@ def tile_hwdconv_t_kernel(tc, x, gn_scale, gn_bias, w_proj, out):
         haar = keep.tile([P, P], BF16, name="haar")
         nc.vector.tensor_tensor(out=haar[:, 0:64], in0=odd, in1=even, op=ALU.add)
         nc.vector.tensor_tensor(out=haar[:, 64:128], in0=odd, in1=even, op=ALU.subtract)
+        identb = keep.tile([P, P], BF16, name="identb")
+        nc.vector.tensor_copy(out=identb[:], in_=ident[:])
+        nidentb = keep.tile([P, P], BF16, name="nidentb")
+        nc.vector.tensor_scalar_mul(out=nidentb[:], in0=ident[:], scalar1=-1.0)
+        eps = keep.tile([P, 1], F32, name="eps")
+        nc.vector.memset(eps[:], 4.0 * EPS)
         same = keep.tile([P, 64], F32, name="same")
         nc.vector.tensor_tensor(out=same[:], in0=hi, in1=lo, op=ALU.add)
         rsum4 = keep.tile([P, 32], F32, name="rsum4")
@@ -96,13 +104,11 @@ def tile_hwdconv_t_kernel(tc, x, gn_scale, gn_bias, w_proj, out):
         early_x = turns.tile([P, 2, 8192], BF16, name="early_x", tag="codes0", align_bytes=64)
         scales0 = keep.tile([P, 4 * COLS], U8, name="scales0", align_bytes=64)
 
-        bands = keep.tile([P, NCH * SLOT], F32, name="bands", align_bytes=64)
-        late_x = turns.tile([P, 8192], BF16, name="late_x", tag="spare", align_bytes=64)
-        yp = keep.tile([P, 2, 4, COLS], BF16, name="yp", align_bytes=64)
-        gr = keep.tile([P, 2, COLS, 4], BF16, name="gr", align_bytes=64)
+        bands = keep.tile([P, SLOTS * SLOT], F32, name="bands", align_bytes=64)
+        ring = keep.tile([P, 4, 4 * COLS], BF16, name="ring", align_bytes=64)
         junk = turns.tile([P, 2048], BF16, name="junk", tag="c1", align_bytes=64)
 
-        sqs = [keep.tile([P, 2, nsum[g]], F32, name="sqs%d" % g) for g in range(2)]
+        sqs = [keep.tile([P, 2, nsq[g]], F32, name="sqs%d" % g) for g in range(2)]
         layouts = (2, 1)
         negc = [keep.tile([P, layouts[g], 2], F32, name="negc%d" % g) for g in range(2)]
         negc4 = keep.tile([P, 1], F32, name="negc4")
@@ -122,8 +128,6 @@ def tile_hwdconv_t_kernel(tc, x, gn_scale, gn_bias, w_proj, out):
             return scales0[4 * (c // 4) : P, COLS * (c % 4) : COLS * (c % 4 + 1)]
 
         def span(slot, n):
-            if slot >= NCH:
-                return late["spare"][:, SLOT * (slot - NCH) : SLOT * (slot - NCH + n)]
             return bands[:, SLOT * slot : SLOT * (slot + n)]
 
         def band(slot, n, u):
@@ -132,7 +136,7 @@ def tile_hwdconv_t_kernel(tc, x, gn_scale, gn_bias, w_proj, out):
         def load_w():
             for h in range(2):
                 nc.sync.dma_start(
-                    out=yp[:, h, :, :].rearrange("p t x -> p (t x)").rearrange("p (a k) -> p a k", a=2),
+                    out=ring[:, h, :].rearrange("p (a k) -> p a k", a=2),
                     in_=wv[:, 2 * h : 2 * h + 2, :],
                 )
 
@@ -145,14 +149,14 @@ def tile_hwdconv_t_kernel(tc, x, gn_scale, gn_bias, w_proj, out):
 
         def grouped_w(plane):
             if plane < 2:
-                return gr[:, plane, :, :].rearrange("p c t -> p (c t)")
+                return ring[:, 2 + plane, :]
             return early_x[:, 0, 0:2048]
 
         def transpose_w(plane):
             wgv = grouped_w(plane).bitcast(F32).rearrange("p (o u) -> p o u", u=2)
             for h in range(2):
                 pt = psum.tile([P, 2, 2, P], F32, name="pt", tag="acc")
-                src = yp[:, h, :, :].rearrange("p t x -> p (t x)").bitcast(F32)
+                src = ring[:, h, :].bitcast(F32)
                 for a in range(2):
                     for u in range(2):
                         if plane == 2:
@@ -206,8 +210,7 @@ def tile_hwdconv_t_kernel(tc, x, gn_scale, gn_bias, w_proj, out):
             )
 
         def group_x(n):
-            raw = early_x[:, n, :] if n < 2 else late_x[:]
-            return raw.rearrange("p (t i w) -> p t i w", t=4, i=8)
+            return early_x[:, n, :].rearrange("p (t i w) -> p t i w", t=4, i=8)
 
         def load_group(n, r):
             i0 = 4 * (FIRST_PE + 2 * n)
@@ -229,6 +232,37 @@ def tile_hwdconv_t_kernel(tc, x, gn_scale, gn_bias, w_proj, out):
                     )
                 banks.append(ps)
             return banks
+
+        def load_lone(e):
+            nc.sync.dma_start(out=ring[:, e, :], in_=xv[:, e, 2048 * LONE : 2048 * (LONE + 1)])
+
+        def lone_pe(e):
+            view = ring[:, e, :].rearrange("p (i r j two) -> p i r j two", i=4, r=2, two=2)
+            banks = []
+            for u in range(2):
+                ps = psum.tile([P, COLS], F32, name="ps", tag="acc")
+                for n in range(4):
+                    r = n // 2
+                    nc.tensor.matmul(
+                        out=ps[:].rearrange("p (i j) -> p i j", i=4),
+                        lhsT=(nidentb[:] if (u == 1 and r == 0) else identb[:]),
+                        rhs=view[:, :, r, :, n % 2],
+                        start=(n == 0),
+                        stop=(n == 3),
+                    )
+                banks.append(ps)
+            return banks
+
+        def evacuate_lone(e, banks):
+            for u in range(2):
+                at = SLOT * LONE + 2 * COLS * u + COLS * e
+                col = len(UNITS) + e
+                nc.scalar.activation(
+                    out=bands[:, at : at + COLS],
+                    in_=banks[u][:],
+                    func=ACTF.Identity,
+                    accum_out=sums[0][:, u, col : col + 1],
+                )
 
         def evacuate_pe(n, t, banks, on_scalar):
             for h in range(2):
@@ -327,249 +361,272 @@ def tile_hwdconv_t_kernel(tc, x, gn_scale, gn_bias, w_proj, out):
 
         def fin_b(g, pg):
             n = layouts[g]
-            mv = sm("mv", g, [P, n, 4])
-            nc.vector.tensor_scalar_mul(out=mv[:], in0=pg[:], scalar1=1.0 / (8 * NPIX))
+            per = 1.0 / (8 * NPIX)
             dl = sm("dl", g, [P, n, 2])
-            nc.vector.tensor_tensor(out=dl[:], in0=mv[:, :, 0:2], in1=negc[g][:], op=ALU.add)
-            d2 = sm("d2", g, [P, n, 2])
-            nc.vector.tensor_tensor(out=d2[:], in0=dl[:], in1=dl[:], op=ALU.mult)
+            nc.vector.scalar_tensor_tensor(
+                out=dl[:], in0=pg[:, :, 0:2], scalar=per, in1=negc[g][:], op0=ALU.mult, op1=ALU.add
+            )
+            nd2 = sm("nd2", g, [P, n, 2])
+            nc.vector.scalar_tensor_tensor(
+                out=nd2[:], in0=dl[:], scalar=-1.0, in1=dl[:], op0=ALU.mult, op1=ALU.mult
+            )
             var = sm("var", g, [P, n, 2])
-            nc.vector.tensor_tensor(out=var[:], in0=mv[:, :, 2:4], in1=d2[:], op=ALU.subtract)
-            ve = sm("ve", g, [P, n, 2])
-            nc.vector.tensor_scalar(
-                out=ve[:], in0=var[:], scalar1=0.0, scalar2=4.0 * EPS, op0=ALU.max, op1=ALU.add
+            nc.vector.scalar_tensor_tensor(
+                out=var[:], in0=pg[:, :, 2:4], scalar=per, in1=nd2[:], op0=ALU.mult, op1=ALU.add
             )
             sd = sm("sd", g, [P, n, 2])
-            nc.scalar.activation(out=sd[:], in_=ve[:], func=ACTF.Sqrt)
+            nc.scalar.activation(out=sd[:], in_=var[:], func=ACTF.Sqrt, bias=eps[:])
+            mean = sm("mean", g, [P, n, 2])
+            nc.vector.tensor_tensor(out=mean[:], in0=dl[:], in1=negc[g][:], op=ALU.subtract)
+            gm = sm("gm", g, [P, 2, 2])
+            nc.vector.tensor_tensor(
+                out=gm[:],
+                in0=gsf[:, 2 * g : 2 * g + 2, :],
+                in1=mean[:, 0, :].unsqueeze(2).to_broadcast([P, 2, 2]),
+                op=ALU.mult,
+            )
 
         def fin_c(g):
             n = layouts[g]
             rs = sm("rs", g, [P, n, 2])
             nc.vector.reciprocal(out=rs[:], in_=small[("sd", g)][:])
-            mv = small[("mv", g)]
+            rs2 = rs[:, 0, :].unsqueeze(2).to_broadcast([P, 2, 2])
+            sh = sm("sh", g, [P, 2, 2])
+            nc.vector.tensor_tensor(out=sh[:], in0=small[("gm", g)][:], in1=rs2, op=ALU.mult)
+            nc.vector.tensor_tensor(out=gain[g][:], in0=gsf[:, 2 * g : 2 * g + 2, :], in1=rs2, op=ALU.mult)
             nc.vector.tensor_tensor(
-                out=gain[g][:],
-                in0=gsf[:, 2 * g : 2 * g + 2, :],
-                in1=rs[:, 0, :].unsqueeze(2).to_broadcast([P, 2, 2]),
-                op=ALU.mult,
-            )
-            mg = sm("mg", g, [P, 2, 2])
-            nc.vector.tensor_tensor(
-                out=mg[:],
-                in0=gain[g][:],
-                in1=mv[:, 0, 0:2].unsqueeze(2).to_broadcast([P, 2, 2]),
-                op=ALU.mult,
-            )
-            nc.vector.tensor_tensor(
-                out=shift[g][:], in0=gbf[:, 2 * g : 2 * g + 2, :], in1=mg[:], op=ALU.subtract
+                out=shift[g][:], in0=gbf[:, 2 * g : 2 * g + 2, :], in1=sh[:], op=ALU.subtract
             )
 
         def fin_c4():
-            rs, mv = small[("rs", 0)], small[("mv", 0)]
+            rs, mean = small[("rs", 0)], small[("mean", 0)]
             mg = sm("mg4", 0, [P, 4])
             for u in range(2):
                 q = slice(64 * u, 64 * u + 64)
                 nc.vector.tensor_scalar_mul(out=gain4[q, :], in0=gsf4[q, :], scalar1=rs[q, 1, u : u + 1])
-                nc.vector.tensor_scalar_mul(out=mg[q, :], in0=gain4[q, :], scalar1=mv[q, 1, u : u + 1])
+            for u in range(2):
+                q = slice(64 * u, 64 * u + 64)
+                nc.vector.tensor_scalar_mul(out=mg[q, :], in0=gain4[q, :], scalar1=mean[q, 1, u : u + 1])
             nc.vector.tensor_tensor(out=shift4[:], in0=gbf4[:], in1=mg[:], op=ALU.subtract)
 
-        def affine_scalar(g, slot, half):
-            for u in range(2):
-                for e in range(2):
-                    lo = SLOT * slot + 2 * COLS * u + COLS * e
-                    t = 2 * u + e
-                    if g == 0 and slot >= FIRST_PE:
-                        bias, scale = shift4[:, t : t + 1], gain4[:, t : t + 1]
-                    else:
-                        bias, scale = shift[g][:, u, e : e + 1], gain[g][:, u, e : e + 1]
-                    nc.scalar.activation(
-                        out=yp[:, half, t, :],
-                        in_=bands[:, lo : lo + COLS],
-                        func=ACTF.Identity,
-                        bias=bias,
-                        scale=scale,
-                    )
+        def normed(slot):
+            return span(slot, 1).bitcast(BF16).rearrange("p (t x) -> p t x", t=4)[:, :, 0:COLS]
 
-        def affine_vector(slot):
-            for t in range(3):
+        def affine_scalar(g, slot):
+            for t in range(4):
+                u, e = t // 2, t % 2
+                if g == 0 and slot >= FIRST_PE:
+                    bias, scale = shift4[:, t : t + 1], gain4[:, t : t + 1]
+                else:
+                    bias, scale = shift[g][:, u, e : e + 1], gain[g][:, u, e : e + 1]
+                nc.scalar.activation(
+                    out=normed(slot)[:, t, :],
+                    in_=span(slot, 1)[:, COLS * t : COLS * (t + 1)],
+                    func=ACTF.Identity,
+                    bias=bias,
+                    scale=scale,
+                )
+
+        def affine_vector(slot, n):
+            dst = ring[:, 0:n, :].rearrange("p n (t x) -> p n t x", t=4)
+            for t in range(4):
                 u, e = t // 2, t % 2
                 nc.vector.tensor_scalar(
-                    out=yp[:, :, t, :],
-                    in0=band(slot, 2, u)[:, :, COLS * e : COLS * (e + 1)],
+                    out=dst[:, :, t, :],
+                    in0=band(slot, n, u)[:, :, COLS * e : COLS * (e + 1)],
                     scalar1=gain[1][:, u, e : e + 1],
                     scalar2=shift[1][:, u, e : e + 1],
                     op0=ALU.mult,
                     op1=ALU.add,
                 )
 
-        def affine_rest(slot):
-            nc.scalar.activation(
-                out=yp[:, :, 3, :],
-                in_=band(slot, 2, 1)[:, :, COLS : 2 * COLS],
-                func=ACTF.Identity,
-                bias=shift[1][:, 1, 1:2],
-                scale=gain[1][:, 1, 1:2],
-            )
+        def regroup(src, buf, on_scalar=False):
+            out = ring[:, buf, :].rearrange("p (c i t) -> p c t i", i=4, t=4)
+            in_ = src.rearrange("p t (c i) -> p c t i", i=4)
+            if on_scalar:
+                nc.scalar.copy(out=out, in_=in_)
+            else:
+                nc.vector.tensor_copy(out=out, in_=in_)
 
-        def regroup(half, ca):
-            if ca > 0:
-                nc.scalar.copy(
-                    out=gr[:, half, 0:ca, :].rearrange("p (c i) t -> p c t i", i=4),
-                    in_=yp[:, half, :, 0:ca].rearrange("p t (c i) -> p c t i", i=4),
-                )
-            nc.vector.tensor_copy(
-                out=gr[:, half, ca:COLS, :].rearrange("p (c i) t -> p c t i", i=4),
-                in_=yp[:, half, :, ca:COLS].rearrange("p t (c i) -> p c t i", i=4),
-            )
-
-        def quantise(half, codes, scales):
+        def quantise(buf, codes, scales, lo=0, hi=COLS):
             nc.vector.quantize_mx(
-                out=codes.bitcast(FP8X4), scales=scales, in_=gr[:, half, :, :].rearrange("p c t -> p (c t)")
+                out=codes[:, lo:hi].bitcast(FP8X4), scales=scales[:, lo:hi], in_=ring[:, buf, 4 * lo : 4 * hi]
             )
 
-        def multiply(c, half, s1):
+        def multiply(c, half, s1, lo, hi):
             accs = []
             first = 0 if c < FIRST_PE else 2
             for a in range(4):
                 acc = psum.tile([P, COLS], F32, name="acc", tag="acc")
                 m = slice(P * a, P * (a + 1))
                 nc.tensor.matmul_mx(
-                    out=acc[:],
+                    out=acc[:, 0 : hi - lo],
                     lhsT=wc[:, first, m].bitcast(FP8X4),
                     lhsT_scale=ws[:, first, m],
-                    rhs=code0(c).bitcast(FP8X4),
-                    rhs_scale=scale0(c),
+                    rhs=code0(c)[:, lo:hi].bitcast(FP8X4),
+                    rhs_scale=scale0(c)[:, lo:hi],
                     start=True,
                     stop=False,
                 )
                 nc.tensor.matmul_mx(
-                    out=acc[:],
+                    out=acc[:, 0 : hi - lo],
                     lhsT=wc[:, 1, m].bitcast(FP8X4),
                     lhsT_scale=ws[:, 1, m],
-                    rhs=late["c1"][:, half, :].bitcast(FP8X4),
-                    rhs_scale=s1[:],
+                    rhs=late["c1"][:, half, lo:hi].bitcast(FP8X4),
+                    rhs_scale=s1[:, lo:hi],
                     start=False,
                     stop=True,
                 )
                 accs.append(acc)
             return accs
 
-        def relu_store(c, accs, last):
-            cols = slice(COLS * c, COLS * (c + 1))
+        def out_tile(c):
             slot = NCH - 2 + c if c < 2 else (c - 4) % SLOTS
-            ost = span(slot, 1).rearrange("p (a x) -> p a x", a=4)
-            for a in range(4):
-                if last and a % 2 == 1:
-                    nc.vector.tensor_scalar_max(out=ost[:, a, :], in0=accs[a][:], scalar1=0.0)
-                else:
-                    nc.scalar.activation(out=ost[:, a, :], in_=accs[a][:], func=ACTF.Relu)
-                if last:
-                    nc.sync.dma_start(out=ov[:, a, cols], in_=ost[:, a, :])
-            if not last:
-                nc.sync.dma_start(out=ov[:, :, cols], in_=ost)
+            return span(slot, 1).rearrange("p (a x) -> p a x", a=4)
 
-        loads = {1: (0, 0), 2: (0, 1), 4: (1, 0), 5: (1, 1), 7: (2, 0), 8: (2, 1)}
+        def relu_store(c, accs):
+            ost = out_tile(c)
+            for a in range(4):
+                nc.scalar.activation(out=ost[:, a, :], in_=accs[a][:], func=ACTF.Relu)
+            nc.sync.dma_start(out=ov[:, :, COLS * c : COLS * (c + 1)], in_=ost)
+
+        loads = {3: (0, 0), 4: (0, 1), 6: (1, 0), 8: (1, 1)}
         pz = None
         for k, unit in enumerate(UNITS):
             n = len(unit)
             for c in unit:
                 xt = load_x(c, halves=(c == 0))
+                if c < 2:
+                    load_lone(c)
                 if c in loads:
                     load_group(*loads[c])
-                if c == 6:
+                if c == 8:
                     load_w()
                     load_gn()
                 haar_h(0, xt, c, halves=(c == 0))
                 if c == 1:
                     guess_out(0, pz, 1)
-            if k >= 1:
-                squares(0, UNITS[k - 1][0], len(UNITS[k - 1]), k - 1)
-            if k in (4, 5):
-                squares_pe(k - 3)
-            if k == 4:
-                for plane in range(3):
-                    quantise_w(plane)
-            haar_v(0, unit[0], n, k, 1)
-            haar_v(0, unit[0], n, k, 0)
-            if k == 0:
-                pz = guess_mm(0)
-            if k in (1, 3, 4):
-                group = k - 2 if k > 1 else 0
-                for t in range(4):
-                    evacuate_pe(group, t, bands_pe(group, t), on_scalar=(t < (4, 2, 1)[group]))
             if k == 1:
-                squares_pe(0)
+                evacuate_lone(0, lone)
+                squares(0, UNITS[0][0], 1, 0)
+                evacuate_lone(1, lone_pe(1))
+                squares(0, LONE, 1, len(UNITS))
+            if k in (4, 6):
+                squares_pe(k // 2 - 2)
+            if k >= 2:
+                squares(0, UNITS[k - 1][0], len(UNITS[k - 1]), k - 1)
             if k == 3:
+                for t in range(4):
+                    evacuate_pe(0, t, bands_pe(0, t), True)
+            if k == 5:
+                evacuate_pe(1, 0, bands_pe(1, 0), True)
                 for plane in range(3):
                     transpose_w(plane)
+            if k == 6:
+                for plane in range(3):
+                    quantise_w(plane)
                 for wide, narrow in ((gsf, gsb), (gbf, gbb), (gsf4, gsb4), (gbf4, gbb4)):
                     nc.gpsimd.tensor_copy(out=wide[:], in_=narrow[:])
+            haar_v(0, unit[0], n, k, 1)
+            haar_v(0, unit[0], n, k, 0)
+            if k == 5:
+                for t in range(1, 4):
+                    evacuate_pe(1, t, bands_pe(1, t), False)
+            if k == 0:
+                lone = lone_pe(0)
+                pz = guess_mm(0)
         squares(0, UNITS[-1][0], len(UNITS[-1]), len(UNITS) - 1)
 
         def slot2(c):
             return (c - 2) % SLOTS
 
-        late["spare"] = turns.tile([P, 2 * SLOT], F32, name="spare", tag="spare", align_bytes=64)
-        for c in range(2):
-            xt = load_x(c)
-            haar_h(1, xt, slot2(c))
-            if c == 0:
-                pg = fin_a(0)
+        xt = load_x(0)
+        haar_h(1, xt, slot2(0))
+        pg = fin_a(0)
+        xt = load_x(1)
+        haar_h(1, xt, slot2(1))
         fin_b(0, pg)
         haar_v(1, slot2(0), 2, 0, 1)
         fin_c(0)
-        affine_scalar(0, 0, 0)
         haar_v(1, slot2(0), 2, 0, 0)
         pz = guess_mm(1)
-        affine_scalar(0, 1, 1)
         fin_c4()
+        for c in range(4):
+            affine_scalar(0, c)
+        guess_out(1, pz, 2)
         late["codes0"] = turns.tile([P, NPIX], U32, name="codes0", tag="codes0", align_bytes=64)
-
-        for k in range(PAIRS):
+        regroup(normed(0), 0)
+        regroup(normed(1), 1)
+        for k in range(PAIRS - 1):
             a, b = 2 * k, 2 * k + 1
-            more = k + 1 < PAIRS
-            ca = CA2 if more else 0
-            if more:
-                xt = load_x(a + 2)
-                haar_h(1, xt, slot2(a + 2))
-            if k == 0:
-                guess_out(1, pz, 2)
-            regroup(0, ca)
-            if more:
-                xt = load_x(b + 2)
-                haar_h(1, xt, slot2(b + 2))
-            regroup(1, ca)
+            xt = load_x(a + 2)
+            haar_h(1, xt, slot2(a + 2))
+            if b + 2 < LAST_BY_SCALAR:
+                regroup(normed(b + 2), (b + 2) % 4, on_scalar=True)
+            quantise(a % 4, code0(a), scale0(a))
+            xt = load_x(b + 2)
+            haar_h(1, xt, slot2(b + 2))
             square(1, slot2(a), 2, k, 1)
-            if more:
-                affine_scalar(0, a + 2, 0)
-                haar_v(1, slot2(a + 2), 2, k + 1, 1)
+            quantise(b % 4, code0(b), scale0(b))
             square(1, slot2(a), 2, k, 0)
-            quantise(0, code0(a), scale0(a))
-            if more:
-                affine_scalar(0, b + 2, 1)
-                haar_v(1, slot2(a + 2), 2, k + 1, 0)
-            else:
-                pg = fin_a(1)
-            quantise(1, code0(b), scale0(b))
+            haar_v(1, slot2(a + 2), 2, k + 1, 1)
+            for c in (a + 4, b + 4):
+                if c < NCH:
+                    affine_scalar(0, c)
+            regroup(normed(a + 2), (a + 2) % 4)
+            haar_v(1, slot2(a + 2), 2, k + 1, 0)
+            if b + 2 >= LAST_BY_SCALAR:
+                regroup(normed(b + 2), (b + 2) % 4)
+        for u in (1, 0):
+            square(1, slot2(NCH - 2), 2, PAIRS - 1, u)
+        quantise(2, code0(NCH - 2), scale0(NCH - 2))
+        pg = fin_a(1)
         fin_b(1, pg)
+        quantise(3, code0(NCH - 1), scale0(NCH - 1))
         fin_c(1)
 
+        def scalar_norms(c):
+            return c % 4 == 3
+
         late["c1"] = turns.tile([P, 2, COLS], U32, name="c1", tag="c1", align_bytes=64)
-        affine_rest(slot2(0))
-        affine_vector(slot2(0))
+        affine_vector(slot2(0), 2)
+        affine_scalar(1, slot2(3))
         accs = None
         for k in range(PAIRS):
-            for half in range(2):
-                regroup(half, 0)
-            for half in range(2):
-                c = 2 * k + half
-                if c >= 1:
-                    relu_store(c - 1, accs, False)
-                if half == 1 and k + 1 < PAIRS:
-                    affine_vector(slot2(c + 1))
-                if half == 0 and k + 1 < PAIRS:
-                    affine_rest(slot2(c + 2))
-                s1 = work.tile([P, COLS], U8, name="s1", tag="s1", bufs=2, align_bytes=64)
-                quantise(half, late["c1"][:, half, :], s1[:])
-                accs = multiply(c, half, s1)
-        relu_store(NCH - 1, accs, True)
+            a, b = 2 * k, 2 * k + 1
+            final = k + 1 == PAIRS
+            src_b = normed(slot2(b)) if scalar_norms(b) else ring[:, 1, :].rearrange("p (t x) -> p t x", t=4)
+            regroup(ring[:, 0, :].rearrange("p (t x) -> p t x", t=4), 2)
+            if not final:
+                regroup(src_b, 3)
+            if a >= 1:
+                relu_store(a - 1, accs)
+            s1 = work.tile([P, COLS], U8, name="s1", tag="s1", bufs=2, align_bytes=64)
+            quantise(2, late["c1"][:, 0, :], s1[:])
+            accs = multiply(a, 0, s1, 0, COLS)
+            if scalar_norms(b) and b + 4 < NCH:
+                affine_scalar(1, slot2(b + 4))
+            relu_store(a, accs)
+            s1 = work.tile([P, COLS], U8, name="s1", tag="s1", bufs=2, align_bytes=64)
+            if not final:
+                affine_vector(slot2(a + 2), 1 if scalar_norms(b + 2) else 2)
+                quantise(3, late["c1"][:, 1, :], s1[:])
+                accs = multiply(b, 1, s1, 0, COLS)
+        regroup(src_b, 3)
+        for lo in (0, COLS // 2):
+            quantise(3, late["c1"][:, 1, :], s1[:], lo, lo + COLS // 2)
+        parts = [multiply(NCH - 1, 1, s1, lo, lo + COLS // 2) for lo in (0, COLS // 2)]
+        ost = out_tile(NCH - 1)
+        for j in range(2):
+            px = slice(COLS // 2 * j, COLS // 2 * (j + 1))
+            for a in range(4):
+                src = parts[j][a][:, 0 : COLS // 2]
+                if a % 2 == 1:
+                    nc.vector.tensor_scalar_max(out=ost[:, a, px], in0=src, scalar1=0.0)
+                else:
+                    nc.scalar.activation(out=ost[:, a, px], in_=src, func=ACTF.Relu)
+                if a % 2 == 1:
+                    first = COLS * (NCH - 1) + COLS // 2 * j
+                    nc.sync.dma_start(
+                        out=ov[:, a - 1 : a + 1, first : first + COLS // 2], in_=ost[:, a - 1 : a + 1, px]
+                    )

@@ -25,7 +25,6 @@ LONE = 11
 FIRST_PE = 12
 GROUPS = 2
 PAIRS = NCH // 2
-LAST_BY_SCALAR = 12
 EPS = 1e-5
 FLOPS = 2 * CO * K * NPIX
 
@@ -448,32 +447,30 @@ def tile_hwdconv_t_kernel(tc, x, gn_scale, gn_bias, w_proj, out):
             else:
                 nc.vector.tensor_copy(out=out, in_=in_)
 
-        def quantise(buf, codes, scales, lo=0, hi=COLS):
-            nc.vector.quantize_mx(
-                out=codes[:, lo:hi].bitcast(FP8X4), scales=scales[:, lo:hi], in_=ring[:, buf, 4 * lo : 4 * hi]
-            )
+        def quantise(buf, codes, scales):
+            nc.vector.quantize_mx(out=codes.bitcast(FP8X4), scales=scales, in_=ring[:, buf, :])
 
-        def multiply(c, half, s1, lo, hi):
+        def multiply(c, half, s1):
             accs = []
             first = 0 if c < FIRST_PE else 2
             for a in range(4):
                 acc = psum.tile([P, COLS], F32, name="acc", tag="acc")
                 m = slice(P * a, P * (a + 1))
                 nc.tensor.matmul_mx(
-                    out=acc[:, 0 : hi - lo],
+                    out=acc[:],
                     lhsT=wc[:, first, m].bitcast(FP8X4),
                     lhsT_scale=ws[:, first, m],
-                    rhs=code0(c)[:, lo:hi].bitcast(FP8X4),
-                    rhs_scale=scale0(c)[:, lo:hi],
+                    rhs=code0(c).bitcast(FP8X4),
+                    rhs_scale=scale0(c),
                     start=True,
                     stop=False,
                 )
                 nc.tensor.matmul_mx(
-                    out=acc[:, 0 : hi - lo],
+                    out=acc[:],
                     lhsT=wc[:, 1, m].bitcast(FP8X4),
                     lhsT_scale=ws[:, 1, m],
-                    rhs=late["c1"][:, half, lo:hi].bitcast(FP8X4),
-                    rhs_scale=s1[:, lo:hi],
+                    rhs=late["c1"][:, half, :].bitcast(FP8X4),
+                    rhs_scale=s1[:, half, :],
                     start=False,
                     stop=True,
                 )
@@ -484,11 +481,17 @@ def tile_hwdconv_t_kernel(tc, x, gn_scale, gn_bias, w_proj, out):
             slot = NCH - 2 + c if c < 2 else (c - 4) % SLOTS
             return span(slot, 1).rearrange("p (a x) -> p a x", a=4)
 
-        def relu_store(c, accs):
+        def relu_store(c, accs, shared=False, pieces=1):
             ost = out_tile(c)
             for a in range(4):
-                nc.scalar.activation(out=ost[:, a, :], in_=accs[a][:], func=ACTF.Relu)
-            nc.sync.dma_start(out=ov[:, :, COLS * c : COLS * (c + 1)], in_=ost)
+                if shared and a % 2 == 1:
+                    nc.vector.tensor_scalar_max(out=ost[:, a, :], in0=accs[a][:], scalar1=0.0)
+                else:
+                    nc.scalar.activation(out=ost[:, a, :], in_=accs[a][:], func=ACTF.Relu)
+                step = 4 // pieces
+                if (a + 1) % step == 0:
+                    rows = slice(a + 1 - step, a + 1)
+                    nc.sync.dma_start(out=ov[:, rows, COLS * c : COLS * (c + 1)], in_=ost[:, rows, :])
 
         loads = {3: (0, 0), 4: (0, 1), 6: (1, 0), 8: (1, 1)}
         pz = None
@@ -500,7 +503,7 @@ def tile_hwdconv_t_kernel(tc, x, gn_scale, gn_bias, w_proj, out):
                     load_lone(c)
                 if c in loads:
                     load_group(*loads[c])
-                if c == 8:
+                if c == 10:
                     load_w()
                     load_gn()
                 haar_h(0, xt, c, halves=(c == 0))
@@ -511,27 +514,23 @@ def tile_hwdconv_t_kernel(tc, x, gn_scale, gn_bias, w_proj, out):
                 squares(0, UNITS[0][0], 1, 0)
                 evacuate_lone(1, lone_pe(1))
                 squares(0, LONE, 1, len(UNITS))
-            if k in (4, 6):
-                squares_pe(k // 2 - 2)
+            if k == 4:
+                squares_pe(0)
             if k >= 2:
                 squares(0, UNITS[k - 1][0], len(UNITS[k - 1]), k - 1)
+            if k == 6:
+                squares_pe(1)
             if k == 3:
                 for t in range(4):
                     evacuate_pe(0, t, bands_pe(0, t), True)
             if k == 5:
-                evacuate_pe(1, 0, bands_pe(1, 0), True)
-                for plane in range(3):
-                    transpose_w(plane)
-            if k == 6:
-                for plane in range(3):
-                    quantise_w(plane)
-                for wide, narrow in ((gsf, gsb), (gbf, gbb), (gsf4, gsb4), (gbf4, gbb4)):
-                    nc.gpsimd.tensor_copy(out=wide[:], in_=narrow[:])
+                for t in range(2):
+                    evacuate_pe(1, t, bands_pe(1, t), True)
             haar_v(0, unit[0], n, k, 1)
-            haar_v(0, unit[0], n, k, 0)
             if k == 5:
-                for t in range(1, 4):
+                for t in range(2, 4):
                     evacuate_pe(1, t, bands_pe(1, t), False)
+            haar_v(0, unit[0], n, k, 0)
             if k == 0:
                 lone = lone_pe(0)
                 pz = guess_mm(0)
@@ -540,6 +539,10 @@ def tile_hwdconv_t_kernel(tc, x, gn_scale, gn_bias, w_proj, out):
         def slot2(c):
             return (c - 2) % SLOTS
 
+        for wide, narrow in ((gsf, gsb), (gbf, gbb), (gsf4, gsb4), (gbf4, gbb4)):
+            nc.gpsimd.tensor_copy(out=wide[:], in_=narrow[:])
+        for plane in range(3):
+            transpose_w(plane)
         xt = load_x(0)
         haar_h(1, xt, slot2(0))
         pg = fin_a(0)
@@ -551,18 +554,20 @@ def tile_hwdconv_t_kernel(tc, x, gn_scale, gn_bias, w_proj, out):
         haar_v(1, slot2(0), 2, 0, 0)
         pz = guess_mm(1)
         fin_c4()
-        for c in range(4):
+        for c in range(6):
             affine_scalar(0, c)
+        for plane in range(3):
+            quantise_w(plane)
         guess_out(1, pz, 2)
         late["codes0"] = turns.tile([P, NPIX], U32, name="codes0", tag="codes0", align_bytes=64)
         regroup(normed(0), 0)
-        regroup(normed(1), 1)
         for k in range(PAIRS - 1):
             a, b = 2 * k, 2 * k + 1
             xt = load_x(a + 2)
             haar_h(1, xt, slot2(a + 2))
-            if b + 2 < LAST_BY_SCALAR:
-                regroup(normed(b + 2), (b + 2) % 4, on_scalar=True)
+            if k == 0:
+                regroup(normed(1), 1)
+            regroup(normed(b + 2), (b + 2) % 4, on_scalar=True)
             quantise(a % 4, code0(a), scale0(a))
             xt = load_x(b + 2)
             haar_h(1, xt, slot2(b + 2))
@@ -570,13 +575,11 @@ def tile_hwdconv_t_kernel(tc, x, gn_scale, gn_bias, w_proj, out):
             quantise(b % 4, code0(b), scale0(b))
             square(1, slot2(a), 2, k, 0)
             haar_v(1, slot2(a + 2), 2, k + 1, 1)
-            for c in (a + 4, b + 4):
+            for c in (a + 6, b + 6):
                 if c < NCH:
                     affine_scalar(0, c)
             regroup(normed(a + 2), (a + 2) % 4)
             haar_v(1, slot2(a + 2), 2, k + 1, 0)
-            if b + 2 >= LAST_BY_SCALAR:
-                regroup(normed(b + 2), (b + 2) % 4)
         for u in (1, 0):
             square(1, slot2(NCH - 2), 2, PAIRS - 1, u)
         quantise(2, code0(NCH - 2), scale0(NCH - 2))
@@ -586,47 +589,38 @@ def tile_hwdconv_t_kernel(tc, x, gn_scale, gn_bias, w_proj, out):
         fin_c(1)
 
         def scalar_norms(c):
-            return c % 4 == 3
+            return c == 1 or (c % 4 == 3 and c < NCH - 4)
+
+        def vector_norms(a):
+            affine_vector(slot2(a), 1 if scalar_norms(a + 1) else 2)
 
         late["c1"] = turns.tile([P, 2, COLS], U32, name="c1", tag="c1", align_bytes=64)
-        affine_vector(slot2(0), 2)
+        vector_norms(0)
+        affine_scalar(1, slot2(1))
         affine_scalar(1, slot2(3))
         accs = None
         for k in range(PAIRS):
             a, b = 2 * k, 2 * k + 1
             final = k + 1 == PAIRS
-            src_b = normed(slot2(b)) if scalar_norms(b) else ring[:, 1, :].rearrange("p (t x) -> p t x", t=4)
-            regroup(ring[:, 0, :].rearrange("p (t x) -> p t x", t=4), 2)
-            if not final:
-                regroup(src_b, 3)
+            planar = ring[:, 0:2, :].rearrange("p n (t x) -> p n t x", t=4)
+            src_b = normed(slot2(b)) if scalar_norms(b) else planar[:, 1, :, :]
+            s1 = work.tile([P, 2, COLS], U8, name="s1", tag="s1", bufs=2, align_bytes=64)
+            regroup(planar[:, 0, :, :], 2)
+            if final:
+                quantise(2, late["c1"][:, 0, :], s1[:, 0, :])
+            regroup(src_b, 3)
             if a >= 1:
-                relu_store(a - 1, accs)
-            s1 = work.tile([P, COLS], U8, name="s1", tag="s1", bufs=2, align_bytes=64)
-            quantise(2, late["c1"][:, 0, :], s1[:])
-            accs = multiply(a, 0, s1, 0, COLS)
-            if scalar_norms(b) and b + 4 < NCH:
-                affine_scalar(1, slot2(b + 4))
-            relu_store(a, accs)
-            s1 = work.tile([P, COLS], U8, name="s1", tag="s1", bufs=2, align_bytes=64)
+                relu_store(a - 1, accs, shared=final)
             if not final:
-                affine_vector(slot2(a + 2), 1 if scalar_norms(b + 2) else 2)
-                quantise(3, late["c1"][:, 1, :], s1[:])
-                accs = multiply(b, 1, s1, 0, COLS)
-        regroup(src_b, 3)
-        for lo in (0, COLS // 2):
-            quantise(3, late["c1"][:, 1, :], s1[:], lo, lo + COLS // 2)
-        parts = [multiply(NCH - 1, 1, s1, lo, lo + COLS // 2) for lo in (0, COLS // 2)]
-        ost = out_tile(NCH - 1)
-        for j in range(2):
-            px = slice(COLS // 2 * j, COLS // 2 * (j + 1))
-            for a in range(4):
-                src = parts[j][a][:, 0 : COLS // 2]
-                if a % 2 == 1:
-                    nc.vector.tensor_scalar_max(out=ost[:, a, px], in0=src, scalar1=0.0)
-                else:
-                    nc.scalar.activation(out=ost[:, a, px], in_=src, func=ACTF.Relu)
-                if a % 2 == 1:
-                    first = COLS * (NCH - 1) + COLS // 2 * j
-                    nc.sync.dma_start(
-                        out=ov[:, a - 1 : a + 1, first : first + COLS // 2], in_=ost[:, a - 1 : a + 1, px]
-                    )
+                quantise(2, late["c1"][:, 0, :], s1[:, 0, :])
+            accs = multiply(a, 0, s1)
+            if scalar_norms(b + 4):
+                affine_scalar(1, slot2(b + 4))
+            if final:
+                quantise(3, late["c1"][:, 1, :], s1[:, 1, :])
+            relu_store(a, accs, shared=final)
+            if not final:
+                vector_norms(a + 2)
+                quantise(3, late["c1"][:, 1, :], s1[:, 1, :])
+            accs = multiply(b, 1, s1)
+        relu_store(NCH - 1, accs, shared=True, pieces=4)

@@ -20,7 +20,7 @@ NCH = 16
 COLS = 512
 SLOTS = 18
 SLOT = 4 * COLS
-UNITS = ((0,), (1,), (2,), (3, 4), (5, 6), (7, 8), (9, 10))
+UNITS = ((0,), (1,), (2,), (3, 4), (5, 6), (7, 8), (9,), (10,))
 LONE = 11
 FIRST_PE = 12
 GROUPS = 2
@@ -59,8 +59,8 @@ def tile_hwdconv_t_kernel(tc, x, gn_scale, gn_bias, w_proj, out):
 
         ident = keep.tile([P, P], F32, name="ident")
         make_identity(nc, ident[:])
-        nsum = (len(UNITS) + 2, PAIRS)
-        nsq = (len(UNITS) + 1, PAIRS)
+        nsum = (len(UNITS) + 2, PAIRS + 1)
+        nsq = (len(UNITS) + 1, PAIRS + 1)
         sums = [keep.tile([P, 2, nsum[g]], F32, name="sums%d" % g) for g in range(2)]
         rsum = keep.tile([P, 32], F32, name="rsum")
         nc.vector.tensor_reduce(
@@ -91,11 +91,11 @@ def tile_hwdconv_t_kernel(tc, x, gn_scale, gn_bias, w_proj, out):
         gmats = {}
         for name, src in (("2", rsum), ("4", rsum4)):
             to2 = keep.tile([P, 32, 4], F32, name="g%sto2" % name)
-            nc.vector.tensor_copy(out=to2[:], in_=src[:].unsqueeze(2).to_broadcast([P, 32, 4]))
+            nc.gpsimd.tensor_copy(out=to2[:], in_=src[:].unsqueeze(2).to_broadcast([P, 32, 4]))
             gmats[name + "2"] = to2[:].rearrange("p q j -> p (q j)")
             to4 = keep.tile([P, 2, 32, 2], F32, name="g%sto4" % name)
             for u in range(2):
-                nc.vector.tensor_copy(out=to4[:, u, :, :], in_=src[:].unsqueeze(2).to_broadcast([P, 32, 2]))
+                nc.gpsimd.tensor_copy(out=to4[:, u, :, :], in_=src[:].unsqueeze(2).to_broadcast([P, 32, 2]))
             gmats[name + "4"] = to4[:].rearrange("p u q j -> p (u q j)")
 
         wc = keep.tile([P, 3, CO], U32, name="wc", align_bytes=64)
@@ -176,20 +176,22 @@ def tile_hwdconv_t_kernel(tc, x, gn_scale, gn_bias, w_proj, out):
                 in_=grouped_w(plane),
             )
 
-        def load_x(c, halves=False):
+        def load_x(c, quarters=False):
             xt = work.tile([P, 2, 2048], BF16, name="xt", tag="xa", align_bytes=64)
-            if halves:
+            if quarters:
                 for e in range(2):
-                    nc.sync.dma_start(out=xt[:, e, :], in_=xv[:, e, 2048 * c : 2048 * (c + 1)])
+                    for lo in (0, 1024):
+                        at = 2048 * c + lo
+                        nc.sync.dma_start(out=xt[:, e, lo : lo + 1024], in_=xv[:, e, at : at + 1024])
             else:
                 nc.sync.dma_start(out=xt[:], in_=xv[:, :, 2048 * c : 2048 * (c + 1)])
             return xt
 
-        def haar_h(g, xt, slot, halves=False):
+        def haar_h(g, xt, slot, quarters=False):
             src = xt[:].rearrange("p e (i r j two) -> p (e i) r j two", r=2, j=P, two=2)
             dst = span(slot, 1).rearrange("p (r ei j) -> p ei r j", r=2, j=P)
-            parts = (slice(0, 4), slice(4, 8)) if halves else (slice(0, 8),)
-            for part in parts:
+            step = 2 if quarters else 8
+            for part in (slice(lo, lo + step) for lo in range(0, 8, step)):
                 nc.vector.tensor_tensor(
                     out=dst[:, part, :, :],
                     in0=src[:, part, :, :, 1],
@@ -309,7 +311,7 @@ def tile_hwdconv_t_kernel(tc, x, gn_scale, gn_bias, w_proj, out):
             if g == 0:
                 for u in range(2):
                     q = slice(64 * u, 64 * u + 64)
-                    nc.vector.tensor_copy(out=negc4[q, :], in_=negc[0][q, 1, u : u + 1])
+                    nc.gpsimd.tensor_copy(out=negc4[q, :], in_=negc[0][q, 1, u : u + 1])
 
         def square(g, slot, n, col, u):
             nc.scalar.activation(
@@ -402,11 +404,9 @@ def tile_hwdconv_t_kernel(tc, x, gn_scale, gn_bias, w_proj, out):
             mg = sm("mg4", 0, [P, 4])
             for u in range(2):
                 q = slice(64 * u, 64 * u + 64)
-                nc.vector.tensor_scalar_mul(out=gain4[q, :], in0=gsf4[q, :], scalar1=rs[q, 1, u : u + 1])
-            for u in range(2):
-                q = slice(64 * u, 64 * u + 64)
-                nc.vector.tensor_scalar_mul(out=mg[q, :], in0=gain4[q, :], scalar1=mean[q, 1, u : u + 1])
-            nc.vector.tensor_tensor(out=shift4[:], in0=gbf4[:], in1=mg[:], op=ALU.subtract)
+                nc.gpsimd.tensor_scalar_mul(out=gain4[q, :], in0=gsf4[q, :], scalar1=rs[q, 1, u : u + 1])
+                nc.gpsimd.tensor_scalar_mul(out=mg[q, :], in0=gain4[q, :], scalar1=mean[q, 1, u : u + 1])
+            nc.gpsimd.tensor_tensor(out=shift4[:], in0=gbf4[:], in1=mg[:], op=ALU.subtract)
 
         def normed(slot):
             return span(slot, 1).bitcast(BF16).rearrange("p (t x) -> p t x", t=4)[:, :, 0:COLS]
@@ -451,30 +451,20 @@ def tile_hwdconv_t_kernel(tc, x, gn_scale, gn_bias, w_proj, out):
             nc.vector.quantize_mx(out=codes.bitcast(FP8X4), scales=scales, in_=ring[:, buf, :])
 
         def multiply(c, half, s1):
-            accs = []
             first = 0 if c < FIRST_PE else 2
-            for a in range(4):
-                acc = psum.tile([P, COLS], F32, name="acc", tag="acc")
-                m = slice(P * a, P * (a + 1))
-                nc.tensor.matmul_mx(
-                    out=acc[:],
-                    lhsT=wc[:, first, m].bitcast(FP8X4),
-                    lhsT_scale=ws[:, first, m],
-                    rhs=code0(c).bitcast(FP8X4),
-                    rhs_scale=scale0(c),
-                    start=True,
-                    stop=False,
-                )
-                nc.tensor.matmul_mx(
-                    out=acc[:],
-                    lhsT=wc[:, 1, m].bitcast(FP8X4),
-                    lhsT_scale=ws[:, 1, m],
-                    rhs=late["c1"][:, half, :].bitcast(FP8X4),
-                    rhs_scale=s1[:, half, :],
-                    start=False,
-                    stop=True,
-                )
-                accs.append(acc)
+            accs = [psum.tile([P, COLS], F32, name="acc", tag="acc") for a in range(4)]
+            for g, plane in enumerate((first, 1)):
+                for a in range(4):
+                    m = slice(P * a, P * (a + 1))
+                    nc.tensor.matmul_mx(
+                        out=accs[a][:],
+                        lhsT=wc[:, plane, m].bitcast(FP8X4),
+                        lhsT_scale=ws[:, plane, m],
+                        rhs=(code0(c) if g == 0 else late["c1"][:, half, :]).bitcast(FP8X4),
+                        rhs_scale=(scale0(c) if g == 0 else s1[:, half, :]),
+                        start=(g == 0),
+                        stop=(g == 1),
+                    )
             return accs
 
         def out_tile(c):
@@ -498,7 +488,7 @@ def tile_hwdconv_t_kernel(tc, x, gn_scale, gn_bias, w_proj, out):
         for k, unit in enumerate(UNITS):
             n = len(unit)
             for c in unit:
-                xt = load_x(c, halves=(c == 0))
+                xt = load_x(c, quarters=(c == 0))
                 if c < 2:
                     load_lone(c)
                 if c in loads:
@@ -506,7 +496,7 @@ def tile_hwdconv_t_kernel(tc, x, gn_scale, gn_bias, w_proj, out):
                 if c == 10:
                     load_w()
                     load_gn()
-                haar_h(0, xt, c, halves=(c == 0))
+                haar_h(0, xt, c, quarters=(c == 0))
                 if c == 1:
                     guess_out(0, pz, 1)
             if k == 1:
@@ -518,19 +508,19 @@ def tile_hwdconv_t_kernel(tc, x, gn_scale, gn_bias, w_proj, out):
                 squares_pe(0)
             if k >= 2:
                 squares(0, UNITS[k - 1][0], len(UNITS[k - 1]), k - 1)
-            if k == 6:
-                squares_pe(1)
             if k == 3:
                 for t in range(4):
                     evacuate_pe(0, t, bands_pe(0, t), True)
-            if k == 5:
+            if k == 6:
                 for t in range(2):
                     evacuate_pe(1, t, bands_pe(1, t), True)
             haar_v(0, unit[0], n, k, 1)
-            if k == 5:
+            haar_v(0, unit[0], n, k, 0)
+            if k == 6:
                 for t in range(2, 4):
                     evacuate_pe(1, t, bands_pe(1, t), False)
-            haar_v(0, unit[0], n, k, 0)
+            if k == 7:
+                squares_pe(1)
             if k == 0:
                 lone = lone_pe(0)
                 pz = guess_mm(0)
@@ -541,32 +531,35 @@ def tile_hwdconv_t_kernel(tc, x, gn_scale, gn_bias, w_proj, out):
 
         for wide, narrow in ((gsf, gsb), (gbf, gbb), (gsf4, gsb4), (gbf4, gbb4)):
             nc.gpsimd.tensor_copy(out=wide[:], in_=narrow[:])
-        for plane in range(3):
-            transpose_w(plane)
+        transpose_w(0)
+        transpose_w(1)
         xt = load_x(0)
         haar_h(1, xt, slot2(0))
         pg = fin_a(0)
+        quantise_w(0)
+        fin_b(0, pg)
+        transpose_w(2)
+        quantise_w(1)
+        fin_c(0)
+        fin_c4()
         xt = load_x(1)
         haar_h(1, xt, slot2(1))
-        fin_b(0, pg)
+        quantise_w(2)
         haar_v(1, slot2(0), 2, 0, 1)
-        fin_c(0)
+        late["codes0"] = turns.tile([P, NPIX], U32, name="codes0", tag="codes0", align_bytes=64)
+        for c in range(2):
+            affine_scalar(0, c)
+        regroup(normed(1), 1, on_scalar=True)
+        for c in range(2, 6):
+            affine_scalar(0, c)
+        regroup(normed(0), 0)
         haar_v(1, slot2(0), 2, 0, 0)
         pz = guess_mm(1)
-        fin_c4()
-        for c in range(6):
-            affine_scalar(0, c)
-        for plane in range(3):
-            quantise_w(plane)
         guess_out(1, pz, 2)
-        late["codes0"] = turns.tile([P, NPIX], U32, name="codes0", tag="codes0", align_bytes=64)
-        regroup(normed(0), 0)
         for k in range(PAIRS - 1):
             a, b = 2 * k, 2 * k + 1
             xt = load_x(a + 2)
             haar_h(1, xt, slot2(a + 2))
-            if k == 0:
-                regroup(normed(1), 1)
             regroup(normed(b + 2), (b + 2) % 4, on_scalar=True)
             quantise(a % 4, code0(a), scale0(a))
             xt = load_x(b + 2)
@@ -574,14 +567,21 @@ def tile_hwdconv_t_kernel(tc, x, gn_scale, gn_bias, w_proj, out):
             square(1, slot2(a), 2, k, 1)
             quantise(b % 4, code0(b), scale0(b))
             square(1, slot2(a), 2, k, 0)
+            if k == PAIRS - 2:
+                for n, c in enumerate((a + 2, b + 2)):
+                    haar_v(1, slot2(c), 1, k + 1 + n, 1)
+                    if n == 0:
+                        regroup(normed(c), c % 4)
+                    haar_v(1, slot2(c), 1, k + 1 + n, 0)
+                break
             haar_v(1, slot2(a + 2), 2, k + 1, 1)
             for c in (a + 6, b + 6):
                 if c < NCH:
                     affine_scalar(0, c)
             regroup(normed(a + 2), (a + 2) % 4)
             haar_v(1, slot2(a + 2), 2, k + 1, 0)
-        for u in (1, 0):
-            square(1, slot2(NCH - 2), 2, PAIRS - 1, u)
+        for n in range(2):
+            squares(1, slot2(NCH - 2 + n), 1, PAIRS - 1 + n)
         quantise(2, code0(NCH - 2), scale0(NCH - 2))
         pg = fin_a(1)
         fin_b(1, pg)
@@ -606,15 +606,16 @@ def tile_hwdconv_t_kernel(tc, x, gn_scale, gn_bias, w_proj, out):
             src_b = normed(slot2(b)) if scalar_norms(b) else planar[:, 1, :, :]
             s1 = work.tile([P, 2, COLS], U8, name="s1", tag="s1", bufs=2, align_bytes=64)
             regroup(planar[:, 0, :, :], 2)
-            if final:
+            early = final or k == 0
+            if early:
                 quantise(2, late["c1"][:, 0, :], s1[:, 0, :])
             regroup(src_b, 3)
             if a >= 1:
                 relu_store(a - 1, accs, shared=final)
-            if not final:
+            if not early:
                 quantise(2, late["c1"][:, 0, :], s1[:, 0, :])
             accs = multiply(a, 0, s1)
-            if scalar_norms(b + 4):
+            if scalar_norms(b + 4) and b + 4 < NCH:
                 affine_scalar(1, slot2(b + 4))
             if final:
                 quantise(3, late["c1"][:, 1, :], s1[:, 1, :])

@@ -91,11 +91,11 @@ def tile_hwdconv_t_kernel(tc, x, gn_scale, gn_bias, w_proj, out):
         gmats = {}
         for name, src in (("2", rsum), ("4", rsum4)):
             to2 = keep.tile([P, 32, 4], F32, name="g%sto2" % name)
-            nc.gpsimd.tensor_copy(out=to2[:], in_=src[:].unsqueeze(2).to_broadcast([P, 32, 4]))
+            nc.vector.tensor_copy(out=to2[:], in_=src[:].unsqueeze(2).to_broadcast([P, 32, 4]))
             gmats[name + "2"] = to2[:].rearrange("p q j -> p (q j)")
             to4 = keep.tile([P, 2, 32, 2], F32, name="g%sto4" % name)
             for u in range(2):
-                nc.gpsimd.tensor_copy(out=to4[:, u, :, :], in_=src[:].unsqueeze(2).to_broadcast([P, 32, 2]))
+                nc.vector.tensor_copy(out=to4[:, u, :, :], in_=src[:].unsqueeze(2).to_broadcast([P, 32, 2]))
             gmats[name + "4"] = to4[:].rearrange("p u q j -> p (u q j)")
 
         wc = keep.tile([P, 3, CO], U32, name="wc", align_bytes=64)
@@ -176,21 +176,19 @@ def tile_hwdconv_t_kernel(tc, x, gn_scale, gn_bias, w_proj, out):
                 in_=grouped_w(plane),
             )
 
-        def load_x(c, quarters=False):
+        def load_x(c, halves=False):
             xt = work.tile([P, 2, 2048], BF16, name="xt", tag="xa", align_bytes=64)
-            if quarters:
+            if halves:
                 for e in range(2):
-                    for lo in (0, 1024):
-                        at = 2048 * c + lo
-                        nc.sync.dma_start(out=xt[:, e, lo : lo + 1024], in_=xv[:, e, at : at + 1024])
+                    nc.sync.dma_start(out=xt[:, e, :], in_=xv[:, e, 2048 * c : 2048 * (c + 1)])
             else:
                 nc.sync.dma_start(out=xt[:], in_=xv[:, :, 2048 * c : 2048 * (c + 1)])
             return xt
 
-        def haar_h(g, xt, slot, quarters=False):
+        def haar_h(g, xt, slot, halves=False):
             src = xt[:].rearrange("p e (i r j two) -> p (e i) r j two", r=2, j=P, two=2)
             dst = span(slot, 1).rearrange("p (r ei j) -> p ei r j", r=2, j=P)
-            step = 2 if quarters else 8
+            step = 4 if halves else 8
             for part in (slice(lo, lo + step) for lo in range(0, 8, step)):
                 nc.vector.tensor_tensor(
                     out=dst[:, part, :, :],
@@ -311,7 +309,7 @@ def tile_hwdconv_t_kernel(tc, x, gn_scale, gn_bias, w_proj, out):
             if g == 0:
                 for u in range(2):
                     q = slice(64 * u, 64 * u + 64)
-                    nc.gpsimd.tensor_copy(out=negc4[q, :], in_=negc[0][q, 1, u : u + 1])
+                    nc.vector.tensor_copy(out=negc4[q, :], in_=negc[0][q, 1, u : u + 1])
 
         def square(g, slot, n, col, u):
             nc.scalar.activation(
@@ -404,9 +402,9 @@ def tile_hwdconv_t_kernel(tc, x, gn_scale, gn_bias, w_proj, out):
             mg = sm("mg4", 0, [P, 4])
             for u in range(2):
                 q = slice(64 * u, 64 * u + 64)
-                nc.gpsimd.tensor_scalar_mul(out=gain4[q, :], in0=gsf4[q, :], scalar1=rs[q, 1, u : u + 1])
-                nc.gpsimd.tensor_scalar_mul(out=mg[q, :], in0=gain4[q, :], scalar1=mean[q, 1, u : u + 1])
-            nc.gpsimd.tensor_tensor(out=shift4[:], in0=gbf4[:], in1=mg[:], op=ALU.subtract)
+                nc.vector.tensor_scalar_mul(out=gain4[q, :], in0=gsf4[q, :], scalar1=rs[q, 1, u : u + 1])
+                nc.vector.tensor_scalar_mul(out=mg[q, :], in0=gain4[q, :], scalar1=mean[q, 1, u : u + 1])
+            nc.vector.tensor_tensor(out=shift4[:], in0=gbf4[:], in1=mg[:], op=ALU.subtract)
 
         def normed(slot):
             return span(slot, 1).bitcast(BF16).rearrange("p (t x) -> p t x", t=4)[:, :, 0:COLS]
@@ -488,7 +486,7 @@ def tile_hwdconv_t_kernel(tc, x, gn_scale, gn_bias, w_proj, out):
         for k, unit in enumerate(UNITS):
             n = len(unit)
             for c in unit:
-                xt = load_x(c, quarters=(c == 0))
+                xt = load_x(c, halves=(c == 0))
                 if c < 2:
                     load_lone(c)
                 if c in loads:
@@ -496,7 +494,7 @@ def tile_hwdconv_t_kernel(tc, x, gn_scale, gn_bias, w_proj, out):
                 if c == 10:
                     load_w()
                     load_gn()
-                haar_h(0, xt, c, quarters=(c == 0))
+                haar_h(0, xt, c, halves=(c == 0))
                 if c == 1:
                     guess_out(0, pz, 1)
             if k == 1:
@@ -541,20 +539,18 @@ def tile_hwdconv_t_kernel(tc, x, gn_scale, gn_bias, w_proj, out):
         transpose_w(2)
         quantise_w(1)
         fin_c(0)
-        fin_c4()
         xt = load_x(1)
         haar_h(1, xt, slot2(1))
         quantise_w(2)
         haar_v(1, slot2(0), 2, 0, 1)
         late["codes0"] = turns.tile([P, NPIX], U32, name="codes0", tag="codes0", align_bytes=64)
-        for c in range(2):
-            affine_scalar(0, c)
-        regroup(normed(1), 1, on_scalar=True)
-        for c in range(2, 6):
+        fin_c4()
+        for c in range(6):
             affine_scalar(0, c)
         regroup(normed(0), 0)
         haar_v(1, slot2(0), 2, 0, 0)
         pz = guess_mm(1)
+        regroup(normed(1), 1)
         guess_out(1, pz, 2)
         for k in range(PAIRS - 1):
             a, b = 2 * k, 2 * k + 1

@@ -20,7 +20,7 @@ NCH = 16
 COLS = 512
 SLOTS = 18
 SLOT = 4 * COLS
-UNITS = ((0,), (1,), (2,), (3, 4), (5, 6), (7, 8), (9,), (10,))
+UNITS = ((0,), (1,), (2,), (3, 4), (5, 6), (7, 8), (9, 10))
 LONE = 11
 FIRST_PE = 12
 GROUPS = 2
@@ -263,25 +263,14 @@ def tile_hwdconv_t_kernel(tc, x, gn_scale, gn_bias, w_proj, out):
                     accum_out=sums[0][:, u, col : col + 1],
                 )
 
-        def evacuate_pe(n, t, banks, on_scalar):
+        def evacuate_pe(n, t, banks):
             for h in range(2):
                 at = SLOT * (FIRST_PE + 2 * n + h) + COLS * t
                 col = 8 * n + 4 * h + t
                 acc = stat4[:, 0, col : col + 1]
-                if on_scalar:
-                    nc.scalar.activation(
-                        out=bands[:, at : at + COLS], in_=banks[h][:], func=ACTF.Identity, accum_out=acc
-                    )
-                else:
-                    nc.vector.tensor_scalar(
-                        out=bands[:, at : at + COLS],
-                        in0=banks[h][:],
-                        scalar1=1.0,
-                        scalar2=0.0,
-                        op0=ALU.mult,
-                        op1=ALU.add,
-                        accum_out=acc,
-                    )
+                nc.scalar.activation(
+                    out=bands[:, at : at + COLS], in_=banks[h][:], func=ACTF.Identity, accum_out=acc
+                )
 
         def squares_pe(n):
             for h in range(2):
@@ -504,21 +493,18 @@ def tile_hwdconv_t_kernel(tc, x, gn_scale, gn_bias, w_proj, out):
                 squares(0, LONE, 1, len(UNITS))
             if k == 4:
                 squares_pe(0)
+            if k == 6:
+                for t in range(4):
+                    evacuate_pe(1, t, bands_pe(1, t))
             if k >= 2:
                 squares(0, UNITS[k - 1][0], len(UNITS[k - 1]), k - 1)
             if k == 3:
                 for t in range(4):
-                    evacuate_pe(0, t, bands_pe(0, t), True)
+                    evacuate_pe(0, t, bands_pe(0, t))
             if k == 6:
-                for t in range(2):
-                    evacuate_pe(1, t, bands_pe(1, t), True)
+                squares_pe(1)
             haar_v(0, unit[0], n, k, 1)
             haar_v(0, unit[0], n, k, 0)
-            if k == 6:
-                for t in range(2, 4):
-                    evacuate_pe(1, t, bands_pe(1, t), False)
-            if k == 7:
-                squares_pe(1)
             if k == 0:
                 lone = lone_pe(0)
                 pz = guess_mm(0)
@@ -531,16 +517,15 @@ def tile_hwdconv_t_kernel(tc, x, gn_scale, gn_bias, w_proj, out):
             nc.gpsimd.tensor_copy(out=wide[:], in_=narrow[:])
         transpose_w(0)
         transpose_w(1)
-        xt = load_x(0)
-        haar_h(1, xt, slot2(0))
+        for c in range(2):
+            xt = load_x(c)
+            haar_h(1, xt, slot2(c))
         pg = fin_a(0)
         quantise_w(0)
         fin_b(0, pg)
         transpose_w(2)
         quantise_w(1)
         fin_c(0)
-        xt = load_x(1)
-        haar_h(1, xt, slot2(1))
         quantise_w(2)
         haar_v(1, slot2(0), 2, 0, 1)
         late["codes0"] = turns.tile([P, NPIX], U32, name="codes0", tag="codes0", align_bytes=64)

@@ -20,7 +20,7 @@ NCH = 16
 COLS = 512
 SLOTS = 18
 SLOT = 4 * COLS
-UNITS = ((0,), (1,), (2,), (3, 4), (5, 6), (7, 8), (9, 10))
+UNITS = ((0,), (1,), (2,), (3, 4), (5, 6), (7, 8), (9,), (10,))
 LONE = 11
 FIRST_PE = 12
 GROUPS = 2
@@ -268,16 +268,29 @@ def tile_hwdconv_t_kernel(tc, x, gn_scale, gn_bias, w_proj, out):
                 at = SLOT * (FIRST_PE + 2 * n + h) + COLS * t
                 col = 8 * n + 4 * h + t
                 acc = stat4[:, 0, col : col + 1]
-                nc.scalar.activation(
-                    out=bands[:, at : at + COLS], in_=banks[h][:], func=ACTF.Identity, accum_out=acc
-                )
+                if n == 1 and h == 1:
+                    nc.vector.tensor_scalar(
+                        out=bands[:, at : at + COLS],
+                        in0=banks[h][:],
+                        scalar1=1.0,
+                        scalar2=0.0,
+                        op0=ALU.mult,
+                        op1=ALU.add,
+                        accum_out=acc,
+                    )
+                else:
+                    nc.scalar.activation(
+                        out=bands[:, at : at + COLS], in_=banks[h][:], func=ACTF.Identity, accum_out=acc
+                    )
+
+        spare_junk = span(SLOTS - 1, 1)[:, 0:1024].bitcast(BF16)
 
         def squares_pe(n):
             for h in range(2):
                 slot = FIRST_PE + 2 * n + h
                 col = 2 * n + h
                 nc.scalar.activation(
-                    out=junk[:],
+                    out=(junk[:] if h == 0 else spare_junk),
                     in_=bands[:, SLOT * slot : SLOT * (slot + 1)],
                     func=ACTF.Square,
                     bias=negc4[:],
@@ -300,9 +313,10 @@ def tile_hwdconv_t_kernel(tc, x, gn_scale, gn_bias, w_proj, out):
                     q = slice(64 * u, 64 * u + 64)
                     nc.vector.tensor_copy(out=negc4[q, :], in_=negc[0][q, 1, u : u + 1])
 
-        def square(g, slot, n, col, u):
+        def square(g, slot, n, col, u, dump=None):
+            dump = junk[:] if dump is None else dump
             nc.scalar.activation(
-                out=junk[:, 0 : 2 * COLS * n].rearrange("p (n x) -> p n x", n=n),
+                out=dump[:, 0 : 2 * COLS * n].rearrange("p (n x) -> p n x", n=n),
                 in_=band(slot, n, u),
                 func=ACTF.Square,
                 bias=negc[g][:, 0, u : u + 1],
@@ -310,9 +324,9 @@ def tile_hwdconv_t_kernel(tc, x, gn_scale, gn_bias, w_proj, out):
                 accum_out=sqs[g][:, u, col : col + 1],
             )
 
-        def squares(g, slot, n, col):
+        def squares(g, slot, n, col, last=False):
             for u in (1, 0):
-                square(g, slot, n, col, u)
+                square(g, slot, n, col, u, spare_junk if g == 0 and u == 0 and not last else None)
 
         def sm(name, g, shape):
             t = keep.tile(shape, F32, name="%s%d" % (name, g))
@@ -473,7 +487,8 @@ def tile_hwdconv_t_kernel(tc, x, gn_scale, gn_bias, w_proj, out):
         loads = {3: (0, 0), 4: (0, 1), 6: (1, 0), 8: (1, 1)}
         pz = None
         for k, unit in enumerate(UNITS):
-            n = len(unit)
+            if k >= 2:
+                haar_v(0, UNITS[k - 1][0], len(UNITS[k - 1]), k - 1, 1)
             for c in unit:
                 xt = load_x(c, halves=(c == 0))
                 if c < 2:
@@ -486,6 +501,8 @@ def tile_hwdconv_t_kernel(tc, x, gn_scale, gn_bias, w_proj, out):
                 haar_h(0, xt, c, halves=(c == 0))
                 if c == 1:
                     guess_out(0, pz, 1)
+            if k >= 2:
+                haar_v(0, UNITS[k - 1][0], len(UNITS[k - 1]), k - 1, 0)
             if k == 1:
                 evacuate_lone(0, lone)
                 squares(0, UNITS[0][0], 1, 0)
@@ -503,12 +520,16 @@ def tile_hwdconv_t_kernel(tc, x, gn_scale, gn_bias, w_proj, out):
                     evacuate_pe(0, t, bands_pe(0, t))
             if k == 6:
                 squares_pe(1)
-            haar_v(0, unit[0], n, k, 1)
-            haar_v(0, unit[0], n, k, 0)
             if k == 0:
+                haar_v(0, 0, 1, 0, 1)
+                haar_v(0, 0, 1, 0, 0)
                 lone = lone_pe(0)
                 pz = guess_mm(0)
-        squares(0, UNITS[-1][0], len(UNITS[-1]), len(UNITS) - 1)
+        last = (0, UNITS[-1][0], len(UNITS[-1]), len(UNITS) - 1)
+        haar_v(*last, 1)
+        haar_h(1, load_x(0), NCH)
+        haar_v(*last, 0)
+        squares(*last, last=True)
 
         def slot2(c):
             return (c - 2) % SLOTS
@@ -517,9 +538,7 @@ def tile_hwdconv_t_kernel(tc, x, gn_scale, gn_bias, w_proj, out):
             nc.gpsimd.tensor_copy(out=wide[:], in_=narrow[:])
         transpose_w(0)
         transpose_w(1)
-        for c in range(2):
-            xt = load_x(c)
-            haar_h(1, xt, slot2(c))
+        haar_h(1, load_x(1), slot2(1))
         pg = fin_a(0)
         quantise_w(0)
         fin_b(0, pg)
@@ -547,7 +566,11 @@ def tile_hwdconv_t_kernel(tc, x, gn_scale, gn_bias, w_proj, out):
             haar_h(1, xt, slot2(b + 2))
             square(1, slot2(a), 2, k, 1)
             quantise(b % 4, code0(b), scale0(b))
+            if a + 6 < NCH:
+                affine_scalar(0, a + 6)
             square(1, slot2(a), 2, k, 0)
+            if b + 6 < NCH:
+                affine_scalar(0, b + 6)
             if k == PAIRS - 2:
                 for n, c in enumerate((a + 2, b + 2)):
                     haar_v(1, slot2(c), 1, k + 1 + n, 1)
@@ -556,9 +579,6 @@ def tile_hwdconv_t_kernel(tc, x, gn_scale, gn_bias, w_proj, out):
                     haar_v(1, slot2(c), 1, k + 1 + n, 0)
                 break
             haar_v(1, slot2(a + 2), 2, k + 1, 1)
-            for c in (a + 6, b + 6):
-                if c < NCH:
-                    affine_scalar(0, c)
             regroup(normed(a + 2), (a + 2) % 4)
             haar_v(1, slot2(a + 2), 2, k + 1, 0)
         for n in range(2):

from contextlib import ExitStack

import concourse.mybir as mybir
from concourse.masks import make_identity

F32 = mybir.dt.float32
BF16 = mybir.dt.bfloat16
U32 = mybir.dt.uint32
U8 = mybir.dt.uint8
FP8X4 = mybir.dt.float8_e4m3fn_x4
ALU = mybir.AluOpType
ACTF = mybir.ActivationFunctionType
AX = mybir.AxisListType

P = 128
CO = 512
K = 1024
NPIX = 8192
NCH = 16
COLS = 512
SLOTS = 18
SLOT = 4 * COLS
UNITS = ((0,), (1,), (2,), (3, 4), (5, 6), (7, 8), (9,), (10,))
LONE = 11
FIRST_PE = 12
GROUPS = 2
PAIRS = NCH // 2
EPS = 1e-5
FLOPS = 2 * CO * K * NPIX


def tile_hwdconv_t_kernel(tc, x, gn_scale, gn_bias, w_proj, out):
    nc = tc.nc
    xv = x.rearrange("(p e) h w -> p e (h w)", e=2)
    ov = out.rearrange("(a p) h w -> p a (h w)", p=P)
    wv = w_proj.rearrange("(a p) k -> p a k", p=P)
    xb = x.rearrange("(q t) (i r) w -> t r q i w", t=4, r=2)

    with ExitStack() as ctx:
        keep = ctx.enter_context(tc.tile_pool(name="keep", bufs=1))
        work = ctx.enter_context(tc.tile_pool(name="work", bufs=3))
        turns = ctx.enter_context(tc.tile_pool(name="turns", bufs=1))
        psum = ctx.enter_context(tc.psum_pool(name="psum", bufs=8))
        ctx.enter_context(tc.manual_schedule())

        one = keep.tile([P, 1], F32, name="one")
        nc.vector.memset(one[:], 1.0)
        wsq = keep.tile([P, 1], F32, name="wsq")
        nc.scalar.activation(out=wsq[:], in_=one[:], func=ACTF.Sqrt)

        gsb = keep.tile([P, 4, 2], BF16, name="gsb")
        gbb = keep.tile([P, 4, 2], BF16, name="gbb")
        gsf = keep.tile([P, 4, 2], F32, name="gsf")
        gbf = keep.tile([P, 4, 2], F32, name="gbf")
        gsb4 = keep.tile([P, 4], BF16, name="gsb4")
        gbb4 = keep.tile([P, 4], BF16, name="gbb4")
        gsf4 = keep.tile([P, 4], F32, name="gsf4")
        gbf4 = keep.tile([P, 4], F32, name="gbf4")

        ident = keep.tile([P, P], F32, name="ident")
        make_identity(nc, ident[:])
        nsum = (len(UNITS) + 2, PAIRS + 1)
        nsq = (len(UNITS) + 1, PAIRS + 1)
        sums = [keep.tile([P, 2, nsum[g]], F32, name="sums%d" % g) for g in range(2)]
        rsum = keep.tile([P, 32], F32, name="rsum")
        nc.vector.tensor_reduce(
            out=rsum[:], in_=ident[:].rearrange("p (q j) -> p q j", j=4), axis=AX.X, op=ALU.add
        )
        parity = ident[:].rearrange("p (q r) -> p q r", r=2)
        even, odd = parity[:, :, 0], parity[:, :, 1]
        lo, hi = ident[:, 0:64], ident[:, 64:128]
        haar = keep.tile([P, P], BF16, name="haar")
        nc.vector.tensor_tensor(out=haar[:, 0:64], in0=odd, in1=even, op=ALU.add)
        nc.vector.tensor_tensor(out=haar[:, 64:128], in0=odd, in1=even, op=ALU.subtract)
        identb = keep.tile([P, P], BF16, name="identb")
        nc.vector.tensor_copy(out=identb[:], in_=ident[:])
        nidentb = keep.tile([P, P], BF16, name="nidentb")
        nc.vector.tensor_scalar_mul(out=nidentb[:], in0=ident[:], scalar1=-1.0)
        eps = keep.tile([P, 1], F32, name="eps")
        nc.vector.memset(eps[:], 4.0 * EPS)
        same = keep.tile([P, 64], F32, name="same")
        nc.vector.tensor_tensor(out=same[:], in0=hi, in1=lo, op=ALU.add)
        rsum4 = keep.tile([P, 32], F32, name="rsum4")
        nc.vector.tensor_reduce(
            out=rsum4[:], in_=same[:].rearrange("p (q j) -> p q j", j=2), axis=AX.X, op=ALU.add
        )
        own = keep.tile([P, 2], F32, name="own")
        nc.vector.tensor_reduce(
            out=own[:], in_=ident[:].rearrange("p (u q) -> p u q", u=2), axis=AX.X, op=ALU.add
        )
        gmats = {}
        for name, src in (("2", rsum), ("4", rsum4)):
            to2 = keep.tile([P, 32, 4], F32, name="g%sto2" % name)
            nc.vector.tensor_copy(out=to2[:], in_=src[:].unsqueeze(2).to_broadcast([P, 32, 4]))
            gmats[name + "2"] = to2[:].rearrange("p q j -> p (q j)")
            to4 = keep.tile([P, 2, 32, 2], F32, name="g%sto4" % name)
            for u in range(2):
                nc.vector.tensor_copy(out=to4[:, u, :, :], in_=src[:].unsqueeze(2).to_broadcast([P, 32, 2]))
            gmats[name + "4"] = to4[:].rearrange("p u q j -> p (u q j)")

        wc = keep.tile([P, 3, CO], U32, name="wc", align_bytes=64)
        ws = keep.tile([P, 3, CO], U8, name="ws", align_bytes=64)
        early_x = turns.tile([P, 2, 8192], BF16, name="early_x", tag="codes0", align_bytes=64)
        scales0 = keep.tile([P, 4 * COLS], U8, name="scales0", align_bytes=64)

        bands = keep.tile([P, SLOTS * SLOT], F32, name="bands", align_bytes=64)
        ring = keep.tile([P, 4, 4 * COLS], BF16, name="ring", align_bytes=64)
        junk = turns.tile([P, 2048], BF16, name="junk", tag="c1", align_bytes=64)

        sqs = [keep.tile([P, 2, nsq[g]], F32, name="sqs%d" % g) for g in range(2)]
        layouts = (2, 1)
        negc = [keep.tile([P, layouts[g], 2], F32, name="negc%d" % g) for g in range(2)]
        negc4 = keep.tile([P, 1], F32, name="negc4")
        gain4 = keep.tile([P, 4], F32, name="gain4")
        shift4 = keep.tile([P, 4], F32, name="shift4")
        stat4 = keep.tile([P, 2, 8 * GROUPS], F32, name="stat4")
        nc.vector.memset(stat4[:], 0.0)
        gain = [keep.tile([P, 2, 2], F32, name="gain%d" % g) for g in range(2)]
        shift = [keep.tile([P, 2, 2], F32, name="shift%d" % g) for g in range(2)]
        small = {}
        late = {}

        def code0(c):
            return late["codes0"][:, COLS * c : COLS * (c + 1)]

        def scale0(c):
            return scales0[4 * (c // 4) : P, COLS * (c % 4) : COLS * (c % 4 + 1)]

        def span(slot, n):
            return bands[:, SLOT * slot : SLOT * (slot + n)]

        def band(slot, n, u):
            return span(slot, n).rearrange("p (n u x) -> p n u x", n=n, u=2)[:, :, u, :]

        def load_w():
            for h in range(2):
                nc.sync.dma_start(
                    out=ring[:, h, :].rearrange("p (a k) -> p a k", a=2),
                    in_=wv[:, 2 * h : 2 * h + 2, :],
                )

        def load_gn():
            with nc.allow_non_contiguous_dma(reason="two small vectors, four bytes a piece"):
                nc.sync.dma_start(out=gsb[:], in_=gn_scale.rearrange("(b p e) -> p b e", b=4, e=2))
                nc.sync.dma_start(out=gbb[:], in_=gn_bias.rearrange("(b p e) -> p b e", b=4, e=2))
                nc.sync.dma_start(out=gsb4[:], in_=gn_scale[0:512].rearrange("(p t) -> p t", t=4))
                nc.sync.dma_start(out=gbb4[:], in_=gn_bias[0:512].rearrange("(p t) -> p t", t=4))

        def grouped_w(plane):
            if plane < 2:
                return ring[:, 2 + plane, :]
            return early_x[:, 0, 0:2048]

        def transpose_w(plane):
            wgv = grouped_w(plane).bitcast(F32).rearrange("p (o u) -> p o u", u=2)
            for h in range(2):
                pt = psum.tile([P, 2, 2, P], F32, name="pt", tag="acc")
                src = ring[:, h, :].bitcast(F32)
                for a in range(2):
                    for u in range(2):
                        if plane == 2:
                            words = src[:, 512 * a + u : 512 * a + 256 : 2]
                        else:
                            at = 512 * a + 256 * plane + 128 * u
                            words = src[:, at : at + P]
                        nc.tensor.transpose(pt[:, a, u, :], words, ident[:])
                nc.scalar.copy(
                    out=wgv[:, 256 * h : 256 * h + 256, :].rearrange("p (a o) u -> p a o u", a=2),
                    in_=pt[:].rearrange("p a u o -> p a o u"),
                )

        def quantise_w(plane):
            nc.vector.quantize_mx(
                out=wc[:, plane, :].bitcast(FP8X4),
                scales=ws[:, plane, :],
                in_=grouped_w(plane),
            )

        def load_x(c, halves=False):
            xt = work.tile([P, 2, 2048], BF16, name="xt", tag="xa", align_bytes=64)
            if halves:
                for e in range(2):
                    nc.sync.dma_start(out=xt[:, e, :], in_=xv[:, e, 2048 * c : 2048 * (c + 1)])
            else:
                nc.sync.dma_start(out=xt[:], in_=xv[:, :, 2048 * c : 2048 * (c + 1)])
            return xt

        def haar_h(g, xt, slot, halves=False):
            src = xt[:].rearrange("p e (i r j two) -> p (e i) r j two", r=2, j=P, two=2)
            dst = span(slot, 1).rearrange("p (r ei j) -> p ei r j", r=2, j=P)
            step = 4 if halves else 8
            for part in (slice(lo, lo + step) for lo in range(0, 8, step)):
                nc.vector.tensor_tensor(
                    out=dst[:, part, :, :],
                    in0=src[:, part, :, :, 1],
                    in1=src[:, part, :, :, 0],
                    op=(ALU.add if g == 0 else ALU.subtract),
                )

        def haar_v(g, slot, n, col, u):
            nc.vector.scalar_tensor_tensor(
                out=band(slot, n, u),
                in0=band(slot, n, 0),
                scalar=(-1.0 if u == 1 else 2.0),
                in1=band(slot, n, 1),
                op0=ALU.mult,
                op1=ALU.add,
                accum_out=sums[g][:, u, col : col + 1],
            )

        def group_x(n):
            return early_x[:, n, :].rearrange("p (t i w) -> p t i w", t=4, i=8)

        def load_group(n, r):
            i0 = 4 * (FIRST_PE + 2 * n)
            for t in range(4):
                nc.sync.dma_start(out=group_x(n)[r:P:2, t, :, :], in_=xb[t, r, :, i0 : i0 + 8, :])

        def bands_pe(n, t):
            view = group_x(n).rearrange("p t i (j two) -> p t i j two", two=2)
            banks = []
            for h in range(2):
                ps = psum.tile([P, COLS], F32, name="ps", tag="acc")
                for m in range(2):
                    nc.tensor.matmul(
                        out=ps[:].rearrange("p (i j) -> p i j", i=4),
                        lhsT=haar[:],
                        rhs=view[:, t, 4 * h : 4 * h + 4, :, m],
                        start=(m == 0),
                        stop=(m == 1),
                    )
                banks.append(ps)
            return banks

        def load_lone(e):
            nc.sync.dma_start(out=ring[:, e, :], in_=xv[:, e, 2048 * LONE : 2048 * (LONE + 1)])

        def lone_pe(e):
            view = ring[:, e, :].rearrange("p (i r j two) -> p i r j two", i=4, r=2, two=2)
            banks = []
            for u in range(2):
                ps = psum.tile([P, COLS], F32, name="ps", tag="acc")
                for n in range(4):
                    r = n // 2
                    nc.tensor.matmul(
                        out=ps[:].rearrange("p (i j) -> p i j", i=4),
                        lhsT=(nidentb[:] if (u == 1 and r == 0) else identb[:]),
                        rhs=view[:, :, r, :, n % 2],
                        start=(n == 0),
                        stop=(n == 3),
                    )
                banks.append(ps)
            return banks

        def evacuate_lone(e, banks):
            for u in range(2):
                at = SLOT * LONE + 2 * COLS * u + COLS * e
                col = len(UNITS) + e
                nc.scalar.activation(
                    out=bands[:, at : at + COLS],
                    in_=banks[u][:],
                    func=ACTF.Identity,
                    accum_out=sums[0][:, u, col : col + 1],
                )

        def evacuate_pe(n, t, banks):
            for h in range(2):
                at = SLOT * (FIRST_PE + 2 * n + h) + COLS * t
                col = 8 * n + 4 * h + t
                acc = stat4[:, 0, col : col + 1]
                if n == 1 and h == 1:
                    nc.vector.tensor_scalar(
                        out=bands[:, at : at + COLS],
                        in0=banks[h][:],
                        scalar1=1.0,
                        scalar2=0.0,
                        op0=ALU.mult,
                        op1=ALU.add,
                        accum_out=acc,
                    )
                else:
                    nc.scalar.activation(
                        out=bands[:, at : at + COLS], in_=banks[h][:], func=ACTF.Identity, accum_out=acc
                    )

        spare_junk = span(SLOTS - 1, 1)[:, 0:1024].bitcast(BF16)

        def squares_pe(n):
            for h in range(2):
                slot = FIRST_PE + 2 * n + h
                col = 2 * n + h
                nc.scalar.activation(
                    out=(junk[:] if h == 0 else spare_junk),
                    in_=bands[:, SLOT * slot : SLOT * (slot + 1)],
                    func=ACTF.Square,
                    bias=negc4[:],
                    scale=1.0,
                    accum_out=stat4[:, 1, col : col + 1],
                )

        def guess_mm(g):
            pz = psum.tile([P, layouts[g], 2], F32, name="pz", tag="acc")
            for l in range(layouts[g]):
                nc.tensor.matmul(
                    out=pz[:, l, :], lhsT=gmats[("22", "24")[l]], rhs=sums[g][:, :, 0], start=True, stop=True
                )
            return pz

        def guess_out(g, pz, n):
            nc.vector.tensor_scalar_mul(out=negc[g][:], in0=pz[:], scalar1=-1.0 / (8 * COLS * n))
            if g == 0:
                for u in range(2):
                    q = slice(64 * u, 64 * u + 64)
                    nc.vector.tensor_copy(out=negc4[q, :], in_=negc[0][q, 1, u : u + 1])

        def square(g, slot, n, col, u, dump=None):
            dump = junk[:] if dump is None else dump
            nc.scalar.activation(
                out=dump[:, 0 : 2 * COLS * n].rearrange("p (n x) -> p n x", n=n),
                in_=band(slot, n, u),
                func=ACTF.Square,
                bias=negc[g][:, 0, u : u + 1],
                scale=1.0,
                accum_out=sqs[g][:, u, col : col + 1],
            )

        def squares(g, slot, n, col, last=False):
            for u in (1, 0):
                square(g, slot, n, col, u, spare_junk if g == 0 and u == 0 and not last else None)

        def sm(name, g, shape):
            t = keep.tile(shape, F32, name="%s%d" % (name, g))
            small[(name, g)] = t
            return t

        def fin_a(g):
            tot = sm("tot", g, [P, 2, 2])
            nc.vector.tensor_reduce(out=tot[:, 0, :], in_=sums[g][:], axis=AX.X, op=ALU.add)
            nc.vector.tensor_reduce(out=tot[:, 1, :], in_=sqs[g][:], axis=AX.X, op=ALU.add)
            flat = tot[:].rearrange("p s u -> p (s u)")
            flat4 = None
            if g == 0:
                tot4 = sm("tot4", g, [P, 2])
                nc.vector.tensor_reduce(out=tot4[:], in_=stat4[:], axis=AX.X, op=ALU.add)
                spread = sm("spread", g, [P, 2, 2])
                nc.vector.tensor_tensor(
                    out=spread[:],
                    in0=tot4[:].unsqueeze(2).to_broadcast([P, 2, 2]),
                    in1=own[:].unsqueeze(1).to_broadcast([P, 2, 2]),
                    op=ALU.mult,
                )
                flat4 = spread[:].rearrange("p s u -> p (s u)")
            pg = psum.tile([P, layouts[g], 4], F32, name="pg", tag="acc")
            for l in range(layouts[g]):
                nc.tensor.matmul(
                    out=pg[:, l, :], lhsT=gmats[("22", "24")[l]], rhs=flat, start=True, stop=(g == 1)
                )
                if g == 0:
                    nc.tensor.matmul(
                        out=pg[:, l, :], lhsT=gmats[("42", "44")[l]], rhs=flat4, start=False, stop=True
                    )
            return pg

        def fin_b(g, pg):
            n = layouts[g]
            per = 1.0 / (8 * NPIX)
            dl = sm("dl", g, [P, n, 2])
            nc.vector.scalar_tensor_tensor(
                out=dl[:], in0=pg[:, :, 0:2], scalar=per, in1=negc[g][:], op0=ALU.mult, op1=ALU.add
            )
            nd2 = sm("nd2", g, [P, n, 2])
            nc.vector.scalar_tensor_tensor(
                out=nd2[:], in0=dl[:], scalar=-1.0, in1=dl[:], op0=ALU.mult, op1=ALU.mult
            )
            var = sm("var", g, [P, n, 2])
            nc.vector.scalar_tensor_tensor(
                out=var[:], in0=pg[:, :, 2:4], scalar=per, in1=nd2[:], op0=ALU.mult, op1=ALU.add
            )
            sd = sm("sd", g, [P, n, 2])
            nc.scalar.activation(out=sd[:], in_=var[:], func=ACTF.Sqrt, bias=eps[:])
            mean = sm("mean", g, [P, n, 2])
            nc.vector.tensor_tensor(out=mean[:], in0=dl[:], in1=negc[g][:], op=ALU.subtract)
            gm = sm("gm", g, [P, 2, 2])
            nc.vector.tensor_tensor(
                out=gm[:],
                in0=gsf[:, 2 * g : 2 * g + 2, :],
                in1=mean[:, 0, :].unsqueeze(2).to_broadcast([P, 2, 2]),
                op=ALU.mult,
            )

        def fin_c(g):
            n = layouts[g]
            rs = sm("rs", g, [P, n, 2])
            nc.vector.reciprocal(out=rs[:], in_=small[("sd", g)][:])
            rs2 = rs[:, 0, :].unsqueeze(2).to_broadcast([P, 2, 2])
            sh = sm("sh", g, [P, 2, 2])
            nc.vector.tensor_tensor(out=sh[:], in0=small[("gm", g)][:], in1=rs2, op=ALU.mult)
            nc.vector.tensor_tensor(out=gain[g][:], in0=gsf[:, 2 * g : 2 * g + 2, :], in1=rs2, op=ALU.mult)
            nc.vector.tensor_tensor(
                out=shift[g][:], in0=gbf[:, 2 * g : 2 * g + 2, :], in1=sh[:], op=ALU.subtract
            )

        def fin_c4():
            rs, mean = small[("rs", 0)], small[("mean", 0)]
            mg = sm("mg4", 0, [P, 4])
            for u in range(2):
                q = slice(64 * u, 64 * u + 64)
                nc.vector.tensor_scalar_mul(out=gain4[q, :], in0=gsf4[q, :], scalar1=rs[q, 1, u : u + 1])
                nc.vector.tensor_scalar_mul(out=mg[q, :], in0=gain4[q, :], scalar1=mean[q, 1, u : u + 1])
            nc.vector.tensor_tensor(out=shift4[:], in0=gbf4[:], in1=mg[:], op=ALU.subtract)

        def normed(slot):
            return span(slot, 1).bitcast(BF16).rearrange("p (t x) -> p t x", t=4)[:, :, 0:COLS]

        def affine_scalar(g, slot):
            for t in range(4):
                u, e = t // 2, t % 2
                if g == 0 and slot >= FIRST_PE:
                    bias, scale = shift4[:, t : t + 1], gain4[:, t : t + 1]
                else:
                    bias, scale = shift[g][:, u, e : e + 1], gain[g][:, u, e : e + 1]
                nc.scalar.activation(
                    out=normed(slot)[:, t, :],
                    in_=span(slot, 1)[:, COLS * t : COLS * (t + 1)],
                    func=ACTF.Identity,
                    bias=bias,
                    scale=scale,
                )

        def affine_vector(slot, n):
            dst = ring[:, 0:n, :].rearrange("p n (t x) -> p n t x", t=4)
            for t in range(4):
                u, e = t // 2, t % 2
                nc.vector.tensor_scalar(
                    out=dst[:, :, t, :],
                    in0=band(slot, n, u)[:, :, COLS * e : COLS * (e + 1)],
                    scalar1=gain[1][:, u, e : e + 1],
                    scalar2=shift[1][:, u, e : e + 1],
                    op0=ALU.mult,
                    op1=ALU.add,
                )

        def regroup(src, buf, on_scalar=False):
            out = ring[:, buf, :].rearrange("p (c i t) -> p c t i", i=4, t=4)
            in_ = src.rearrange("p t (c i) -> p c t i", i=4)
            if on_scalar:
                nc.scalar.copy(out=out, in_=in_)
            else:
                nc.vector.tensor_copy(out=out, in_=in_)

        def quantise(buf, codes, scales):
            nc.vector.quantize_mx(out=codes.bitcast(FP8X4), scales=scales, in_=ring[:, buf, :])

        def multiply(c, half, s1):
            first = 0 if c < FIRST_PE else 2
            accs = [psum.tile([P, COLS], F32, name="acc", tag="acc") for a in range(4)]
            for g, plane in enumerate((first, 1)):
                for a in range(4):
                    m = slice(P * a, P * (a + 1))
                    nc.tensor.matmul_mx(
                        out=accs[a][:],
                        lhsT=wc[:, plane, m].bitcast(FP8X4),
                        lhsT_scale=ws[:, plane, m],
                        rhs=(code0(c) if g == 0 else late["c1"][:, half, :]).bitcast(FP8X4),
                        rhs_scale=(scale0(c) if g == 0 else s1[:, half, :]),
                        start=(g == 0),
                        stop=(g == 1),
                    )
            return accs

        def out_tile(c):
            slot = NCH - 2 + c if c < 2 else (c - 4) % SLOTS
            return span(slot, 1).rearrange("p (a x) -> p a x", a=4)

        def relu_store(c, accs, shared=False, pieces=1):
            ost = out_tile(c)
            for a in range(4):
                if shared and a % 2 == 1:
                    nc.vector.tensor_scalar_max(out=ost[:, a, :], in0=accs[a][:], scalar1=0.0)
                else:
                    nc.scalar.activation(out=ost[:, a, :], in_=accs[a][:], func=ACTF.Relu)
                step = 4 // pieces
                if (a + 1) % step == 0:
                    rows = slice(a + 1 - step, a + 1)
                    nc.sync.dma_start(out=ov[:, rows, COLS * c : COLS * (c + 1)], in_=ost[:, rows, :])

        loads = {3: (0, 0), 4: (0, 1), 6: (1, 0), 8: (1, 1)}
        pz = None
        for k, unit in enumerate(UNITS):
            if k >= 2:
                haar_v(0, UNITS[k - 1][0], len(UNITS[k - 1]), k - 1, 1)
            for c in unit:
                xt = load_x(c, halves=(c == 0))
                if c < 2:
                    load_lone(c)
                if c in loads:
                    load_group(*loads[c])
                if c == 10:
                    load_w()
                    load_gn()
                haar_h(0, xt, c, halves=(c == 0))
                if c == 1:
                    guess_out(0, pz, 1)
            if k >= 2:
                haar_v(0, UNITS[k - 1][0], len(UNITS[k - 1]), k - 1, 0)
            if k == 1:
                evacuate_lone(0, lone)
                squares(0, UNITS[0][0], 1, 0)
                evacuate_lone(1, lone_pe(1))
                squares(0, LONE, 1, len(UNITS))
            if k == 4:
                squares_pe(0)
            if k == 6:
                for t in range(4):
                    evacuate_pe(1, t, bands_pe(1, t))
            if k >= 2:
                squares(0, UNITS[k - 1][0], len(UNITS[k - 1]), k - 1)
            if k == 3:
                for t in range(4):
                    evacuate_pe(0, t, bands_pe(0, t))
            if k == 6:
                squares_pe(1)
            if k == 0:
                haar_v(0, 0, 1, 0, 1)
                haar_v(0, 0, 1, 0, 0)
                lone = lone_pe(0)
                pz = guess_mm(0)
        last = (0, UNITS[-1][0], len(UNITS[-1]), len(UNITS) - 1)
        haar_v(*last, 1)
        haar_h(1, load_x(0), NCH)
        haar_v(*last, 0)
        squares(*last, last=True)

        def slot2(c):
            return (c - 2) % SLOTS

        for wide, narrow in ((gsf, gsb), (gbf, gbb), (gsf4, gsb4), (gbf4, gbb4)):
            nc.gpsimd.tensor_copy(out=wide[:], in_=narrow[:])
        transpose_w(0)
        transpose_w(1)
        haar_h(1, load_x(1), slot2(1))
        pg = fin_a(0)
        quantise_w(0)
        fin_b(0, pg)
        transpose_w(2)
        quantise_w(1)
        fin_c(0)
        quantise_w(2)
        haar_v(1, slot2(0), 2, 0, 1)
        late["codes0"] = turns.tile([P, NPIX], U32, name="codes0", tag="codes0", align_bytes=64)
        fin_c4()
        for c in range(6):
            affine_scalar(0, c)
        regroup(normed(0), 0)
        haar_v(1, slot2(0), 2, 0, 0)
        pz = guess_mm(1)
        regroup(normed(1), 1)
        guess_out(1, pz, 2)
        for k in range(PAIRS - 1):
            a, b = 2 * k, 2 * k + 1
            xt = load_x(a + 2)
            haar_h(1, xt, slot2(a + 2))
            regroup(normed(b + 2), (b + 2) % 4, on_scalar=True)
            quantise(a % 4, code0(a), scale0(a))
            xt = load_x(b + 2)
            haar_h(1, xt, slot2(b + 2))
            square(1, slot2(a), 2, k, 1)
            quantise(b % 4, code0(b), scale0(b))
            if a + 6 < NCH:
                affine_scalar(0, a + 6)
            square(1, slot2(a), 2, k, 0)
            if b + 6 < NCH:
                affine_scalar(0, b + 6)
            if k == PAIRS - 2:
                for n, c in enumerate((a + 2, b + 2)):
                    haar_v(1, slot2(c), 1, k + 1 + n, 1)
                    if n == 0:
                        regroup(normed(c), c % 4)
                    haar_v(1, slot2(c), 1, k + 1 + n, 0)
                break
            haar_v(1, slot2(a + 2), 2, k + 1, 1)
            regroup(normed(a + 2), (a + 2) % 4)
            haar_v(1, slot2(a + 2), 2, k + 1, 0)
        for n in range(2):
            squares(1, slot2(NCH - 2 + n), 1, PAIRS - 1 + n)
        quantise(2, code0(NCH - 2), scale0(NCH - 2))
        pg = fin_a(1)
        fin_b(1, pg)
        quantise(3, code0(NCH - 1), scale0(NCH - 1))
        fin_c(1)

        def scalar_norms(c):
            return c == 1 or (c % 4 == 3 and c < NCH - 4)

        def vector_norms(a):
            affine_vector(slot2(a), 1 if scalar_norms(a + 1) else 2)

        late["c1"] = turns.tile([P, 2, COLS], U32, name="c1", tag="c1", align_bytes=64)
        vector_norms(0)
        affine_scalar(1, slot2(1))
        affine_scalar(1, slot2(3))
        accs = None
        for k in range(PAIRS):
            a, b = 2 * k, 2 * k + 1
            final = k + 1 == PAIRS
            planar = ring[:, 0:2, :].rearrange("p n (t x) -> p n t x", t=4)
            src_b = normed(slot2(b)) if scalar_norms(b) else planar[:, 1, :, :]
            s1 = work.tile([P, 2, COLS], U8, name="s1", tag="s1", bufs=2, align_bytes=64)
            regroup(planar[:, 0, :, :], 2)
            early = final or k == 0
            if early:
                quantise(2, late["c1"][:, 0, :], s1[:, 0, :])
            regroup(src_b, 3)
            if a >= 1:
                relu_store(a - 1, accs, shared=final)
            if not early:
                quantise(2, late["c1"][:, 0, :], s1[:, 0, :])
            accs = multiply(a, 0, s1)
            if scalar_norms(b + 4) and b + 4 < NCH:
                affine_scalar(1, slot2(b + 4))
            if final:
                quantise(3, late["c1"][:, 1, :], s1[:, 1, :])
            relu_store(a, accs, shared=final)
            if not final:
                vector_norms(a + 2)
                quantise(3, late["c1"][:, 1, :], s1[:, 1, :])
            accs = multiply(b, 1, s1)
        relu_store(NCH - 1, accs, shared=True, pieces=4)
